import numpy as np
import ml_dtypes


def mxq(x, axis, fmt="e4m3"):
    dtype, down = {"e4m3": (ml_dtypes.float8_e4m3fn, 7), "e5m2": (ml_dtypes.float8_e5m2, 14)}[fmt]
    v = np.moveaxis(np.asarray(x, np.float32).astype(ml_dtypes.bfloat16).astype(np.float64), axis, -1)
    blocks = v.reshape(v.shape[:-1] + (-1, 32))
    amax = np.abs(blocks).max(-1, keepdims=True)
    byte = np.maximum(np.where(amax > 0, np.frexp(amax)[1] - 1 + 127, 0) - down, 1)
    scale = np.exp2(byte - 127.0)
    codes = (blocks / scale).astype(np.float32).astype(dtype).astype(np.float64)
    return np.moveaxis((codes * scale).reshape(v.shape), -1, axis)


WIDE = False


def mx_kscale(k):
    if not WIDE:
        return np.ones(k)
    levels = np.array([10, -10, 5, -5, 0])
    a = np.random.permutation(np.resize(levels, k // 512 * 4)).reshape(k // 512, 4)
    idx = np.arange(k)
    return np.exp2(a[idx // 512, idx % 128 // 32])


BF16 = ml_dtypes.bfloat16


def bf(x):
    return np.asarray(x, np.float32).astype(BF16)


def f64(x):
    return np.asarray(x).astype(np.float64)


E2M1 = np.array([0.0, 0.5, 1.0, 1.5, 2.0, 3.0, 4.0, 6.0, -0.0, -0.5, -1.0, -1.5, -2.0, -3.0, -4.0, -6.0])


def pack_weight(w, fmt):
    k, n = w.shape
    w = f64(bf(w)).reshape(k // 32, 32, n)
    amax = np.abs(w).max(1)
    if fmt == "e4m3":
        byte = np.frexp(amax)[1] - 1 + 127 - 7
    else:
        mant, ex = np.frexp(amax / 6.0)
        byte = np.where(mant > 0.5, ex, ex - 1) + 127
    byte = np.clip(np.where(amax > 0, byte, 1), 1, 254)
    scaled = (w * np.exp2(127.0 - byte)[:, None, :]).reshape(k, n).astype(np.float32)
    by_word = np.ascontiguousarray(scaled.reshape(k // 512, 128, 4, n).transpose(0, 1, 3, 2))
    if fmt == "e4m3":
        words = by_word.astype(ml_dtypes.float8_e4m3fn).view(np.uint8)
    else:
        c = by_word.astype(ml_dtypes.float4_e2m1fn).view(np.uint8) & 0xF
        words = c[..., 0::2] | (c[..., 1::2] << 4)
    return np.ascontiguousarray(words), np.ascontiguousarray(byte.astype(np.uint8).reshape(k // 512, 16, n))


def unpack_weight(words, scales, fmt):
    g, p, n, _ = words.shape
    if fmt == "e4m3":
        vals = np.ascontiguousarray(words).view(ml_dtypes.float8_e4m3fn).astype(np.float64)
    else:
        nib = np.empty((g, p, n, 4), np.uint8)
        nib[..., 0::2] = words & 0xF
        nib[..., 1::2] = words >> 4
        vals = E2M1[nib]
    vals = vals * np.repeat(np.exp2(scales.astype(np.float64) - 127.0), 8, axis=1)[..., None]
    return vals.transpose(0, 1, 3, 2).reshape(g * 512, n)


B, D = 128, 1024
D2 = 2 * D
GATE_BIAS = 0.0
EPS = 1e-5
FMT = "e4m3"


def layernorm(v, w, b):
    mu = np.mean(v, axis=-1, keepdims=True)
    var = np.mean((v - mu) ** 2, axis=-1, keepdims=True)
    return (v - mu) * (1.0 / np.sqrt(var + EPS)) * w + b


def sigmoid(v):
    return 1.0 / (1.0 + np.exp(-v))


def setup_inputs():
    s, t = mx_kscale(D2), mx_kscale(D2)
    x = bf(np.random.standard_normal((B, D)))
    h = bf(np.random.standard_normal((B, D)))
    Wg_words, Wg_scales = pack_weight(np.ascontiguousarray((np.random.standard_normal((5 * D, D2)) / np.sqrt(D2) / s[None, :]).T), FMT)
    bg = bf(np.random.standard_normal(5 * D) * 0.3)
    Wu_words, Wu_scales = pack_weight(np.ascontiguousarray((np.random.standard_normal((D, D2)) / np.sqrt(D2) / t[None, :]).T), FMT)
    bu = bf(np.random.standard_normal(D) * 0.3)
    return {"x": x,
            "h": h,
            "Wg_words": Wg_words,
            "Wg_scales": Wg_scales,
            "bg": bg,
            "Wu_words": Wu_words,
            "Wu_scales": Wu_scales,
            "bu": bu,
            "ln_w": bf((1.0 + 0.1 * np.random.standard_normal(D2)) * s),
            "ln_b": bf(0.1 * np.random.standard_normal(D2) * s),
            "ln2_w": bf((1.0 + 0.1 * np.random.standard_normal(D2)) * t),
            "ln2_b": bf(0.1 * np.random.standard_normal(D2) * t),
            "dropout_mask": bf(1.0 + 0.1 * np.random.standard_normal(D2))}


def reference(x, h, Wg_words, Wg_scales, bg, Wu_words, Wu_scales, bu, ln_w, ln_b, ln2_w, ln2_b, dropout_mask):
    x, h, m = f64(x), f64(h), f64(dropout_mask)
    d = x.shape[-1]
    inp = np.concatenate([x, h], axis=1)
    inp = layernorm(inp, f64(ln_w), f64(ln_b))
    inp = inp * m[None, :]
    gates = (mxq(inp, 1, "e4m3") @ unpack_weight(Wg_words, Wg_scales, FMT)) + f64(bg)
    rx = sigmoid(gates[:, 0 * d:1 * d])
    rh = sigmoid(gates[:, 1 * d:2 * d])
    z_gates = np.stack([gates[:, 2 * d:3 * d], gates[:, 3 * d:4 * d], gates[:, 4 * d:5 * d] - GATE_BIAS], axis=-1)
    e = np.exp(z_gates - z_gates.max(axis=-1, keepdims=True))
    z = e / e.sum(axis=-1, keepdims=True)
    inp2 = np.concatenate([x * rx, h * rh], axis=1)
    inp2 = layernorm(inp2, f64(ln2_w), f64(ln2_b))
    inp2 = inp2 * m[None, :]
    u = np.tanh((mxq(inp2, 1, "e4m3") @ unpack_weight(Wu_words, Wu_scales, FMT)) + f64(bu))
    h_new = x * z[..., 0] + h * z[..., 1] + u * z[..., 2]
    return h_new

@@ -1,0 +1,255 @@
+from contextlib import ExitStack
+
+import concourse.mybir as mybir
+from concourse.masks import make_identity
+
+F32 = mybir.dt.float32
+BF16 = mybir.dt.bfloat16
+I32 = mybir.dt.int32
+U32 = mybir.dt.uint32
+U8 = mybir.dt.uint8
+FP8X4 = mybir.dt.float8_e4m3fn_x4
+ALU = mybir.AluOpType
+ACT = mybir.ActivationFunctionType
+AX = mybir.AxisListType
+
+P = 128
+D = 1024
+K = 2 * D
+G = K // 512
+EPS = 1e-5
+FLOPS = 2 * 128 * 2048 * 6144
+
+
+def tile_dgrucell_w_kernel(tc, x, h, Wg_words, Wg_scales, bg, Wu_words, Wu_scales, bu,
+                                      ln_w, ln_b, ln2_w, ln2_b, dropout_mask, out):
+    nc = tc.nc
+    with ExitStack() as ctx:
+        keep = ctx.enter_context(tc.tile_pool(name="keep", bufs=1))
+        work = ctx.enter_context(tc.tile_pool(name="work", bufs=2))
+        psum = ctx.enter_context(tc.psum_pool(name="psum", bufs=8))
+
+        xh = keep.tile([P, K], BF16, name="xh")
+        wsc = keep.tile([P, 6 * D], U8, name="wsc", align_bytes=64)
+        wg = keep.tile([P, G, 5 * D], U32, name="wg", align_bytes=64)
+        wu = keep.tile([P, G, D], U32, name="wu", align_bytes=64)
+        identf = keep.tile([P, P], F32, name="identf")
+        identb = keep.tile([P, P], BF16, name="identb")
+        rows1 = keep.tile([P, 512], BF16, name="rows1")
+        rows2 = keep.tile([P, 512], BF16, name="rows2")
+        mhalf = keep.tile([P, 1], F32, name="mhalf")
+
+        nc.vector.memset(wsc[:].bitcast(I32), 0)
+        nc.vector.memset(rows1[:], 0.0)
+        nc.vector.memset(rows2[:], 0.0)
+        nc.vector.memset(mhalf[:], -0.5)
+        make_identity(nc, identb[:])
+        make_identity(nc, identf[:])
+
+        nc.sync.dma_start(out=xh[:, 0:D], in_=x)
+        nc.scalar.dma_start(out=xh[:, D:K], in_=h)
+        nc.scalar.dma_start(out=rows1[0:4, :], in_=ln_w.rearrange("(g c) -> g c", g=G))
+        nc.scalar.dma_start(out=rows1[4:8, :], in_=ln_b.rearrange("(g c) -> g c", g=G))
+        nc.scalar.dma_start(out=rows1[8:12, :], in_=dropout_mask.rearrange("(g c) -> g c", g=G))
+        nc.gpsimd.dma_start(out=rows2[8:18, :], in_=bg.rearrange("(r c) -> r c", c=512))
+        nc.gpsimd.dma_start(out=rows2[0:4, :], in_=ln2_w.rearrange("(g c) -> g c", g=G))
+        nc.gpsimd.dma_start(out=rows2[4:8, :], in_=ln2_b.rearrange("(g c) -> g c", g=G))
+        nc.gpsimd.dma_start(out=rows2[18:20, :], in_=bu.rearrange("(r c) -> r c", c=512))
+
+        wsc32 = wsc[:].bitcast(I32)
+        for q in range(4):
+            nc.sync.dma_start(out=wsc32[32 * q:32 * q + 16, 0:1280],
+                              in_=Wg_scales.bitcast(I32)[:, 4 * q:4 * q + 4, :])
+        for q in range(4):
+            nc.sync.dma_start(out=wsc32[32 * q:32 * q + 16, 1280:1536],
+                              in_=Wu_scales.bitcast(I32)[:, 4 * q:4 * q + 4, :])
+
+        wg_src = Wg_words.rearrange("g p n t -> g p (n t)").bitcast(I32).rearrange("g p n -> p g n")
+        wu_src = Wu_words.rearrange("g p n t -> g p (n t)").bitcast(I32).rearrange("g p n -> p g n")
+        wg32 = wg[:].bitcast(I32)
+        wu32 = wu[:].bitcast(I32)
+        for c0, c1 in ((0, 1024), (1024, 2048), (2048, 3072), (3072, 4096), (4096, 4608), (4608, 5120)):
+            nc.sync.dma_start(out=wg32[:, :, c0:c1], in_=wg_src[:, :, c0:c1])
+        u_chunks = ((0, 512), (512, 768), (768, 1024))
+        for c0, c1 in u_chunks:
+            nc.sync.dma_start(out=wu32[:, :, c0:c1], in_=wu_src[:, :, c0:c1])
+
+        def mx_group(acc, codes, plane, w, c0, n, s0):
+            for g in range(G):
+                nc.tensor.matmul_mx(out=acc,
+                                    lhsT=codes[:, g, :].bitcast(FP8X4), lhsT_scale=plane[:, g, :],
+                                    rhs=w[:, g, c0:c0 + n].bitcast(FP8X4), rhs_scale=wsc[4 * g:P, s0:s0 + n],
+                                    start=(g == 0), stop=(g == G - 1))
+
+        def ln_tail(src, gains, codes, plane):
+            planar = keep.tile([P, G, 4, P], BF16, name="planar")
+            grouped = keep.tile([P, G, P, 4], BF16, name="grouped", align_bytes=64)
+            for g in range(G):
+                pt = psum.tile([P, 4, P], F32, name="pt", tag="bank")
+                for t in range(4):
+                    nc.tensor.transpose(pt[:, t, :], src[:, 512 * g + t:512 * (g + 1):4], identf[:])
+                for t in range(4):
+                    gw = gains[:, t, 0, g:g + 1]
+                    gb = gains[:, t, 1, g:g + 1]
+                    if g % 2 == 0:
+                        nc.vector.tensor_scalar(out=planar[:, g, t, :], in0=pt[:, t, :], scalar1=gw, scalar2=gb,
+                                                op0=ALU.mult, op1=ALU.add)
+                    else:
+                        nc.scalar.activation(out=planar[:, g, t, :], in_=pt[:, t, :], func=ACT.Identity,
+                                             bias=gb, scale=gw)
+                nc.vector.tensor_copy(out=grouped[:, g, :, :], in_=planar[:, g, :, :].rearrange("p t b -> p b t"))
+                nc.vector.quantize_mx(out=codes[:, g, :].bitcast(FP8X4), scales=plane[:, g, :],
+                                      in_=grouped[:, g, :, :].rearrange("p b t -> p (b t)"))
+
+        def normalise(dst, src, mean, rstd, nmr):
+            for g in range(G):
+                sl = slice(512 * g, 512 * (g + 1))
+                if g % 2 == 0:
+                    nc.vector.tensor_scalar(out=dst[:, sl], in0=src[:, sl], scalar1=mean, scalar2=rstd,
+                                            op0=ALU.subtract, op1=ALU.mult)
+                else:
+                    nc.scalar.activation(out=dst[:, sl], in_=src[:, sl], func=ACT.Identity, bias=nmr, scale=rstd)
+
+        st = keep.tile([P, 4, 6], F32, name="st")
+        for j in range(4):
+            nc.vector.bn_stats(out=st[:, j, :], in_=xh[:, 512 * j:512 * (j + 1)])
+        mv = keep.tile([P, 2], F32, name="mv")
+        nc.vector.bn_aggr(out=mv[:], in_=st[:].rearrange("p a b -> p (a b)"))
+        vpe1 = keep.tile([P, 1], F32, name="vpe1")
+        nc.vector.tensor_scalar(out=vpe1[:], in0=mv[:, 1:2], scalar1=EPS, scalar2=None, op0=ALU.add)
+        rstd1 = keep.tile([P, 1], F32, name="rstd1")
+        nc.gpsimd.tensor_tensor(out=rstd1[:], in0=vpe1[:], in1=mhalf[:], op=ALU.pow)
+        nmr1 = keep.tile([P, 1], F32, name="nmr1")
+        nc.vector.tensor_scalar(out=nmr1[:], in0=mv[:, 0:1], scalar1=rstd1[:, 0:1], scalar2=-1.0,
+                                op0=ALU.mult, op1=ALU.mult)
+
+        vp1 = psum.tile([P, 4, P], BF16, name="vp1", tag="bank")
+        for t in range(4):
+            nc.tensor.transpose(vp1[:, t, :], rows1[:, t:512:4], identb[:])
+        vt1 = keep.tile([P, 4, 12], F32, name="vt1")
+        nc.vector.tensor_copy(out=vt1[:], in_=vp1[:, :, 0:12])
+        mask_b = vt1[:, :, 8:12].unsqueeze(2).to_broadcast([P, 4, 2, 4])
+        gains1 = keep.tile([P, 4, 2, 4], F32, name="gains1")
+        nc.vector.tensor_tensor(out=gains1[:], in0=vt1[:, :, 0:8].rearrange("p t (v g) -> p t v g", v=2),
+                                in1=mask_b, op=ALU.mult)
+
+        nrm = keep.tile([P, K], F32, name="nrm")
+        normalise(nrm, xh, mv[:, 0:1], rstd1[:, 0:1], nmr1[:, 0:1])
+        acode = keep.tile([P, G, P], U32, name="acode", align_bytes=64)
+        aplane = keep.tile([P, G, P], U8, name="aplane", align_bytes=64)
+        ln_tail(nrm, gains1, acode, aplane)
+
+        vp2 = psum.tile([P, 4, P], BF16, name="vp2", tag="bank")
+        for t in range(4):
+            nc.tensor.transpose(vp2[:, t, :], rows2[:, t:512:4], identb[:])
+        vt2 = keep.tile([P, 4, 8], F32, name="vt2")
+        nc.vector.tensor_copy(out=vt2[:], in_=vp2[:, :, 0:8])
+        gains2 = keep.tile([P, 4, 2, 4], F32, name="gains2")
+        nc.vector.tensor_tensor(out=gains2[:], in0=vt2[:].rearrange("p t (v g) -> p t v g", v=2),
+                                in1=mask_b, op=ALU.mult)
+
+        seld = keep.tile([P, 4], BF16, name="seld")
+        nc.vector.tensor_tensor(out=seld[:, 0:2], in0=identb[:, 12:14], in1=identb[:, 16:18], op=ALU.subtract)
+        nc.vector.tensor_tensor(out=seld[:, 2:4], in0=identb[:, 14:16], in1=identb[:, 16:18], op=ALU.subtract)
+
+        def spread(sel, dst):
+            pb = psum.tile([P, 512], F32, name="pb", tag="bank")
+            nc.tensor.matmul(pb[:], lhsT=sel.to_broadcast([P, P]), rhs=rows2[:], start=True, stop=True)
+            nc.scalar.copy(out=dst, in_=pb[:])
+
+        b_r = keep.tile([P, K], F32, name="b_r")
+        b_z = keep.tile([P, 2, D], F32, name="b_z")
+        b_u = keep.tile([P, D], F32, name="b_u")
+        for j in range(4):
+            spread(identb[:, 8 + j:9 + j], b_r[:, 512 * j:512 * (j + 1)])
+        for i in range(2):
+            for c in range(2):
+                spread(seld[:, 2 * i + c:2 * i + c + 1], b_z[:, i, 512 * c:512 * (c + 1)])
+        for c in range(2):
+            spread(identb[:, 18 + c:19 + c], b_u[:, 512 * c:512 * (c + 1)])
+
+        xs = keep.tile([P, D], F32, name="xs")
+        xd = keep.tile([P, D], F32, name="xd")
+        nc.gpsimd.tensor_tensor(out=xs[:], in0=xh[:, 0:D], in1=xh[:, D:K], op=ALU.add)
+        nc.gpsimd.tensor_tensor(out=xd[:], in0=xh[:, 0:D], in1=xh[:, D:K], op=ALU.subtract)
+
+        c2 = keep.tile([P, K], F32, name="c2")
+        s1 = keep.tile([P, 4], F32, name="s1")
+        s2 = keep.tile([P, 4], F32, name="s2")
+        for j in range(4):
+            sl = slice(512 * j, 512 * (j + 1))
+            acc = psum.tile([P, 512], F32, name="acc_r", tag="bank")
+            mx_group(acc[:], acode, aplane, wg, 512 * j, 512, 512 * j)
+            tb = work.tile([P, 512], F32, name="tb")
+            nc.vector.tensor_tensor(out=tb[:], in0=acc[:], in1=b_r[:, sl], op=ALU.add)
+            nc.scalar.activation(out=tb[:], in_=tb[:], func=ACT.Tanh, scale=0.5)
+            nc.vector.scalar_tensor_tensor(out=c2[:, sl], in0=tb[:], scalar=1.0, in1=xh[:, sl],
+                                           op0=ALU.add, op1=ALU.mult, accum_out=s1[:, j:j + 1])
+            junk = work.tile([P, 512], BF16, name="junk")
+            nc.scalar.activation(out=junk[:], in_=c2[:, sl], func=ACT.Square, accum_out=s2[:, j:j + 1])
+
+        a1 = keep.tile([P, 1], F32, name="a1")
+        a2 = keep.tile([P, 1], F32, name="a2")
+        nc.vector.tensor_reduce(out=a1[:], in_=s1[:], axis=AX.X, op=ALU.add)
+        nc.vector.tensor_reduce(out=a2[:], in_=s2[:], axis=AX.X, op=ALU.add)
+        mean2 = keep.tile([P, 1], F32, name="mean2")
+        nc.vector.tensor_scalar(out=mean2[:], in0=a1[:], scalar1=1.0 / K, scalar2=None, op0=ALU.mult)
+        msq = keep.tile([P, 1], F32, name="msq")
+        nc.vector.tensor_scalar(out=msq[:], in0=mean2[:], scalar1=mean2[:, 0:1], scalar2=4.0 * EPS,
+                                op0=ALU.mult, op1=ALU.subtract)
+        vpe2 = keep.tile([P, 1], F32, name="vpe2")
+        nc.vector.scalar_tensor_tensor(out=vpe2[:], in0=a2[:], scalar=1.0 / K, in1=msq[:],
+                                       op0=ALU.mult, op1=ALU.subtract)
+        rstd2 = keep.tile([P, 1], F32, name="rstd2")
+        nc.gpsimd.tensor_tensor(out=rstd2[:], in0=vpe2[:], in1=mhalf[:], op=ALU.pow)
+        nmr2 = keep.tile([P, 1], F32, name="nmr2")
+        nc.vector.tensor_scalar(out=nmr2[:], in0=mean2[:], scalar1=rstd2[:, 0:1], scalar2=-1.0,
+                                op0=ALU.mult, op1=ALU.mult)
+        normalise(c2, c2, mean2[:, 0:1], rstd2[:, 0:1], nmr2[:, 0:1])
+        ucode = keep.tile([P, G, P], U32, name="ucode", align_bytes=64)
+        uplane = keep.tile([P, G, P], U8, name="uplane", align_bytes=64)
+        ln_tail(c2, gains2, ucode, uplane)
+
+        t0 = keep.tile([P, D], F32, name="t0")
+        t1 = keep.tile([P, D], F32, name="t1")
+        dp = keep.tile([P, D], F32, name="dp")
+        for c in range(2):
+            sl = slice(512 * c, 512 * (c + 1))
+            acc = psum.tile([P, 512], F32, name="acc0", tag="bank")
+            mx_group(acc[:], acode, aplane, wg, 2048 + 512 * c, 512, 2048 + 512 * c)
+            nc.vector.tensor_tensor(out=t0[:, sl], in0=acc[:], in1=b_z[:, 0, sl], op=ALU.add)
+        for c in range(2):
+            sl = slice(512 * c, 512 * (c + 1))
+            acc = psum.tile([P, 512], F32, name="acc1", tag="bank")
+            mx_group(acc[:], acode, aplane, wg, 3072 + 512 * c, 512, 3072 + 512 * c)
+            nc.vector.tensor_tensor(out=t1[:, sl], in0=acc[:], in1=b_z[:, 1, sl], op=ALU.add)
+            nc.vector.tensor_tensor(out=dp[:, sl], in0=t0[:, sl], in1=t1[:, sl], op=ALU.subtract)
+            nc.scalar.activation(out=dp[:, sl], in_=dp[:, sl], func=ACT.Tanh, scale=0.5)
+            nc.vector.tensor_tensor(out=dp[:, sl], in0=dp[:, sl], in1=xd[:, sl], op=ALU.mult)
+            nc.vector.tensor_tensor(out=dp[:, sl], in0=dp[:, sl], in1=xs[:, sl], op=ALU.add)
+        for c in range(2):
+            sl = slice(512 * c, 512 * (c + 1))
+            acc = psum.tile([P, 512], F32, name="acc2", tag="bank")
+            mx_group(acc[:], acode, aplane, wg, 4096 + 512 * c, 512, 4096 + 512 * c)
+            nc.vector.tensor_tensor(out=t0[:, sl], in0=t0[:, sl], in1=acc[:], op=ALU.subtract)
+            nc.vector.tensor_tensor(out=t1[:, sl], in0=t1[:, sl], in1=acc[:], op=ALU.subtract)
+            nc.scalar.activation(out=t0[:, sl], in_=t0[:, sl], func=ACT.Exp)
+            nc.scalar.activation(out=t1[:, sl], in_=t1[:, sl], func=ACT.Exp)
+            nc.vector.scalar_tensor_tensor(out=t0[:, sl], in0=t0[:, sl], scalar=1.0, in1=t1[:, sl],
+                                           op0=ALU.add, op1=ALU.add)
+            nc.vector.reciprocal(out=t0[:, sl], in_=t0[:, sl])
+            nc.vector.scalar_tensor_tensor(out=dp[:, sl], in0=t0[:, sl], scalar=1.0, in1=dp[:, sl],
+                                           op0=ALU.subtract, op1=ALU.mult)
+
+        for c0, c1 in u_chunks:
+            n = c1 - c0
+            acc = psum.tile([P, n], F32, name="acc_u", tag="bank")
+            mx_group(acc[:], ucode, uplane, wu, c0, n, 5 * D + c0)
+            ub = work.tile([P, n], F32, name="ub", tag="ub")
+            nc.vector.tensor_tensor(out=ub[:], in0=acc[:], in1=b_u[:, c0:c1], op=ALU.add)
+            nc.scalar.activation(out=ub[:], in_=ub[:], func=ACT.Tanh)
+            nc.vector.tensor_tensor(out=ub[:], in0=ub[:], in1=t0[:, c0:c1], op=ALU.mult)
+            res = work.tile([P, n], F32, name="res", tag="res")
+            nc.vector.scalar_tensor_tensor(out=res[:], in0=dp[:, c0:c1], scalar=-0.5, in1=ub[:],
+                                           op0=ALU.mult, op1=ALU.add)
+            nc.sync.dma_start(out=out[:, c0:c1], in_=res[:])

@@ -26,8 +26,9 @@ def tile_dgrucell_w_kernel(tc, x, h, Wg_words, Wg_scales, bg, Wu_words, Wu_scale
     nc = tc.nc
     with ExitStack() as ctx:
         keep = ctx.enter_context(tc.tile_pool(name="keep", bufs=1))
-        work = ctx.enter_context(tc.tile_pool(name="work", bufs=2))
-        psum = ctx.enter_context(tc.psum_pool(name="psum", bufs=8))
+        psum = ctx.enter_context(tc.psum_pool(name="psum", bufs=1))
+        ctx.enter_context(tc.manual_schedule())
+        eng = {"V": nc.vector, "S": nc.scalar, "G": nc.gpsimd, "SP": nc.sync}
 
         xh = keep.tile([P, K], BF16, name="xh")
         wsc = keep.tile([P, 6 * D], U8, name="wsc", align_bytes=64)
@@ -35,221 +36,439 @@ def tile_dgrucell_w_kernel(tc, x, h, Wg_words, Wg_scales, bg, Wu_words, Wu_scale
         wu = keep.tile([P, G, D], U32, name="wu", align_bytes=64)
         identf = keep.tile([P, P], F32, name="identf")
         identb = keep.tile([P, P], BF16, name="identb")
-        rows1 = keep.tile([P, 512], BF16, name="rows1")
-        rows2 = keep.tile([P, 512], BF16, name="rows2")
+        rows = {1: keep.tile([P, 512], BF16, name="rows1"), 2: keep.tile([P, 512], BF16, name="rows2")}
         mhalf = keep.tile([P, 1], F32, name="mhalf")
+        seld = keep.tile([P, 4], BF16, name="seld")
+        st = keep.tile([P, 4, 6], F32, name="st")
+        mv = keep.tile([P, 2], F32, name="mv")
+        vpe = {1: keep.tile([P, 1], F32, name="vpe1"), 2: keep.tile([P, 1], F32, name="vpe2")}
+        negm = {1: keep.tile([P, 1], F32, name="negm1"), 2: keep.tile([P, 1], F32, name="negm2")}
+        rstd = {1: keep.tile([P, 1], F32, name="rstd1"), 2: keep.tile([P, 1], F32, name="rstd2")}
+        nmr = {1: keep.tile([P, 1], F32, name="nmr1"), 2: keep.tile([P, 1], F32, name="nmr2")}
+        mean2 = keep.tile([P, 1], F32, name="mean2")
+        vt = {1: keep.tile([P, 4, 12], F32, name="vt1"), 2: keep.tile([P, 4, 8], F32, name="vt2")}
+        gains = {1: keep.tile([P, 4, 2, 4], F32, name="gains1"), 2: keep.tile([P, 4, 2, 4], F32, name="gains2")}
+        nrm = keep.tile([P, K], F32, name="nrm")
+        c2 = keep.tile([P, K], F32, name="c2")
+        planar = keep.tile([P, G, 4, P], BF16, name="planar")
+        grouped = keep.tile([P, G, P, 4], BF16, name="grouped", align_bytes=64)
+        code = {1: keep.tile([P, G, P], U32, name="code1", align_bytes=64),
+                2: keep.tile([P, G, P], U32, name="code2", align_bytes=64)}
+        plane = {1: keep.tile([P, G, P], U8, name="plane1", align_bytes=64),
+                 2: keep.tile([P, G, P], U8, name="plane2", align_bytes=64)}
+        b_r = keep.tile([P, K], BF16, name="b_r")
+        b_z = keep.tile([P, 2, D], F32, name="b_z")
+        b_u = keep.tile([P, D], BF16, name="b_u")
+        xsd = {"xs": keep.tile([P, D], F32, name="xs"), "xd": keep.tile([P, D], F32, name="xd")}
+        tb = keep.tile([P, K], F32, name="tb")
+        junk = keep.tile([P, 512], BF16, name="junk")
+        s1 = keep.tile([P, 4], F32, name="s1")
+        s2 = keep.tile([P, 4], F32, name="s2")
+        a1 = keep.tile([P, 1], F32, name="a1")
+        a2 = keep.tile([P, 1], F32, name="a2")
+        msq = keep.tile([P, 1], F32, name="msq")
+        tz = {0: keep.tile([P, D], F32, name="t0"), 1: keep.tile([P, D], F32, name="t1")}
+        ez = {0: keep.tile([P, D], F32, name="e0"), 1: keep.tile([P, D], F32, name="e1")}
+        dp = keep.tile([P, D], F32, name="dp")
+        ub = keep.tile([P, D], F32, name="ub")
+        res = keep.tile([P, D], F32, name="res")
 
-        nc.vector.memset(wsc[:].bitcast(I32), 0)
-        nc.vector.memset(rows1[:], 0.0)
-        nc.vector.memset(rows2[:], 0.0)
-        nc.vector.memset(mhalf[:], -0.5)
-        make_identity(nc, identb[:])
-        make_identity(nc, identf[:])
+        ps = {}
+        count = [0]
 
-        nc.sync.dma_start(out=xh[:, 0:D], in_=x)
-        nc.scalar.dma_start(out=xh[:, D:K], in_=h)
-        nc.scalar.dma_start(out=rows1[0:4, :], in_=ln_w.rearrange("(g c) -> g c", g=G))
-        nc.scalar.dma_start(out=rows1[4:8, :], in_=ln_b.rearrange("(g c) -> g c", g=G))
-        nc.scalar.dma_start(out=rows1[8:12, :], in_=dropout_mask.rearrange("(g c) -> g c", g=G))
-        nc.gpsimd.dma_start(out=rows2[8:18, :], in_=bg.rearrange("(r c) -> r c", c=512))
-        nc.gpsimd.dma_start(out=rows2[0:4, :], in_=ln2_w.rearrange("(g c) -> g c", g=G))
-        nc.gpsimd.dma_start(out=rows2[4:8, :], in_=ln2_b.rearrange("(g c) -> g c", g=G))
-        nc.gpsimd.dma_start(out=rows2[18:20, :], in_=bu.rearrange("(r c) -> r c", c=512))
+        def bank(key, shape, dtype):
+            n = count[0] % 8
+            count[0] = count[0] + 1
+            ps[key] = psum.tile(shape, dtype, name="bank%d" % n, tag="bank%d" % n)
+            return ps[key]
+
+        def sl(c):
+            return slice(512 * c, 512 * (c + 1))
 
         wsc32 = wsc[:].bitcast(I32)
-        for q in range(4):
-            nc.sync.dma_start(out=wsc32[32 * q:32 * q + 16, 0:1280],
-                              in_=Wg_scales.bitcast(I32)[:, 4 * q:4 * q + 4, :])
-        for q in range(4):
-            nc.sync.dma_start(out=wsc32[32 * q:32 * q + 16, 1280:1536],
-                              in_=Wu_scales.bitcast(I32)[:, 4 * q:4 * q + 4, :])
+        wsrc = {"g": Wg_words.rearrange("g p n t -> g p (n t)").bitcast(I32).rearrange("g p n -> p g n"),
+                "u": Wu_words.rearrange("g p n t -> g p (n t)").bitcast(I32).rearrange("g p n -> p g n")}
+        wdst = {"g": wg[:].bitcast(I32), "u": wu[:].bitcast(I32)}
+        small = {"lnw": (1, 0, 4, ln_w), "lnb": (1, 4, 8, ln_b), "mask": (1, 8, 12, dropout_mask),
+                 "ln2w": (2, 0, 4, ln2_w), "ln2b": (2, 4, 8, ln2_b), "bg": (2, 8, 18, bg), "bu": (2, 18, 20, bu)}
+        wcols = {"rx": ("g", 0, 1024), "rh": ("g", 1024, 2048), "g0": ("g", 2048, 3072), "g1a": ("g", 3072, 3584),
+                 "g1b": ("g", 3584, 4096), "g2": ("g", 4096, 5120),
+                 "ua": ("u", 0, 512), "ub": ("u", 512, 768), "uc": ("u", 768, 1024)}
 
-        wg_src = Wg_words.rearrange("g p n t -> g p (n t)").bitcast(I32).rearrange("g p n -> p g n")
-        wu_src = Wu_words.rearrange("g p n t -> g p (n t)").bitcast(I32).rearrange("g p n -> p g n")
-        wg32 = wg[:].bitcast(I32)
-        wu32 = wu[:].bitcast(I32)
-        for c0, c1 in ((0, 1024), (1024, 2048), (2048, 3072), (3072, 4096), (4096, 4608), (4608, 5120)):
-            nc.sync.dma_start(out=wg32[:, :, c0:c1], in_=wg_src[:, :, c0:c1])
-        u_chunks = ((0, 512), (512, 768), (768, 1024))
-        for c0, c1 in u_chunks:
-            nc.sync.dma_start(out=wu32[:, :, c0:c1], in_=wu_src[:, :, c0:c1])
+        def init():
+            nc.vector.memset(wsc32, 0)
+            nc.vector.memset(rows[1][:], 0.0)
+            nc.vector.memset(rows[2][:], 0.0)
+            nc.vector.memset(mhalf[:], -0.5)
+            make_identity(nc, identb[:])
+            make_identity(nc, identf[:])
+            nc.vector.tensor_tensor(out=seld[:, 0:2], in0=identb[:, 12:14], in1=identb[:, 16:18], op=ALU.subtract)
+            nc.vector.tensor_tensor(out=seld[:, 2:4], in0=identb[:, 14:16], in1=identb[:, 16:18], op=ALU.subtract)
 
-        def mx_group(acc, codes, plane, w, c0, n, s0):
+        def dma(q, name):
+            if name == "x":
+                eng[q].dma_start(out=xh[:, 0:D], in_=x)
+            elif name == "h":
+                eng[q].dma_start(out=xh[:, D:K], in_=h)
+            elif name in small:
+                i, r0, r1, src = small[name]
+                eng[q].dma_start(out=rows[i][r0:r1, :], in_=src.rearrange("(r c) -> r c", c=512))
+            elif name[0:3] == "wgs":
+                qd = int(name[3])
+                eng[q].dma_start(out=wsc32[32 * qd:32 * qd + 16, 0:1280],
+                                 in_=Wg_scales.bitcast(I32)[:, 4 * qd:4 * qd + 4, :])
+            elif name[0:3] == "wus":
+                qd = int(name[3])
+                eng[q].dma_start(out=wsc32[32 * qd:32 * qd + 16, 1280:1536],
+                                 in_=Wu_scales.bitcast(I32)[:, 4 * qd:4 * qd + 4, :])
+            else:
+                w, c0, c1 = wcols[name[1:]]
+                eng[q].dma_start(out=wdst[w][:, :, c0:c1], in_=wsrc[w][:, :, c0:c1])
+
+        def bn(j):
+            nc.vector.bn_stats(out=st[:, j, :], in_=xh[:, sl(j)])
+
+        def stats1():
+            nc.vector.bn_aggr(out=mv[:], in_=st[:].rearrange("p a b -> p (a b)"))
+            nc.vector.tensor_scalar(out=vpe[1][:], in0=mv[:, 1:2], scalar1=EPS, scalar2=None, op0=ALU.add)
+            nc.vector.tensor_scalar(out=negm[1][:], in0=mv[:, 0:1], scalar1=-1.0, scalar2=None, op0=ALU.mult)
+
+        def pow_(ln):
+            nc.gpsimd.tensor_tensor(out=rstd[ln][:], in0=vpe[ln][:], in1=mhalf[:], op=ALU.pow)
+            nc.gpsimd.tensor_tensor(out=nmr[ln][:], in0=rstd[ln][:], in1=negm[ln][:], op=ALU.mult)
+
+        def t_rows(i):
+            t_ = bank(("vp", i), [P, 4, P], BF16)
+            for t in range(4):
+                nc.tensor.transpose(t_[:, t, :], rows[i][:, t:512:4], identb[:])
+
+        def gains_(i):
+            n = 12 if i == 1 else 8
+            nc.vector.tensor_copy(out=vt[i][:], in_=ps["vp", i][:, :, 0:n])
+            nc.vector.tensor_tensor(out=gains[i][:], in0=vt[i][:, :, 0:8].rearrange("p t (v g) -> p t v g", v=2),
+                                    in1=vt[1][:, :, 8:12].unsqueeze(2).to_broadcast([P, 4, 2, 4]), op=ALU.mult)
+
+        def spread2(key, r0):
+            t_ = bank(key, [P, 1024], BF16)
+            for c in range(2):
+                nc.tensor.matmul(t_[:, sl(c)], lhsT=identb[:, r0 + c:r0 + c + 1].to_broadcast([P, P]), rhs=rows[2][:],
+                                 start=True, stop=True)
+
+        def spread_r(i):
+            spread2(("br", i), 8 + 2 * i)
+
+        def copy_br(i):
+            nc.scalar.copy(out=b_r[:, 1024 * i:1024 * (i + 1)], in_=ps["br", i][:])
+
+        def spread_u():
+            spread2("bu", 18)
+
+        def copy_bu():
+            nc.scalar.copy(out=b_u[:], in_=ps["bu"][:])
+
+        def spread_z(i, c):
+            t_ = bank(("bz", i, c), [P, 512], F32)
+            nc.tensor.matmul(t_[:], lhsT=seld[:, 2 * i + c:2 * i + c + 1].to_broadcast([P, P]), rhs=rows[2][:],
+                             start=True, stop=True)
+
+        def copy_bz(i, c):
+            nc.scalar.copy(out=b_z[:, i, sl(c)], in_=ps["bz", i, c][:])
+
+        def xsxd(name, c, e):
+            eng[e].tensor_tensor(out=xsd[name][:, sl(c)], in0=xh[:, sl(c)], in1=xh[:, sl(c + 2)],
+                                 op=(ALU.add if name == "xs" else ALU.subtract))
+
+        def norm(ln, g, e):
+            src = xh if ln == 1 else c2
+            dst = nrm if ln == 1 else c2
+            mean = mv[:, 0:1] if ln == 1 else mean2[:, 0:1]
+            if e == "S":
+                nc.scalar.activation(out=dst[:, sl(g)], in_=src[:, sl(g)], func=ACT.Identity,
+                                     bias=nmr[ln][:, 0:1], scale=rstd[ln][:, 0:1])
+            else:
+                eng[e].tensor_scalar(out=dst[:, sl(g)], in0=src[:, sl(g)], scalar1=mean, scalar2=rstd[ln][:, 0:1],
+                                     op0=ALU.subtract, op1=ALU.mult)
+
+        def t_ln(ln, g):
+            src = nrm if ln == 1 else c2
+            t_ = bank(("pt", ln, g), [P, 4, P], F32)
+            for t in range(4):
+                nc.tensor.transpose(t_[:, t, :], src[:, 512 * g + t:512 * (g + 1):4], identf[:])
+
+        def evac(ln, g, e):
+            for t in range(4):
+                gw = gains[ln][:, t, 0, g:g + 1]
+                gb = gains[ln][:, t, 1, g:g + 1]
+                if e == "V":
+                    nc.vector.tensor_scalar(out=planar[:, g, t, :], in0=ps["pt", ln, g][:, t, :], scalar1=gw,
+                                            scalar2=gb, op0=ALU.mult, op1=ALU.add)
+                else:
+                    nc.scalar.activation(out=planar[:, g, t, :], in_=ps["pt", ln, g][:, t, :], func=ACT.Identity,
+                                         bias=gb, scale=gw)
+
+        def regroup(ln, g, e):
+            if e == "V":
+                nc.vector.tensor_copy(out=grouped[:, g, :, :], in_=planar[:, g, :, :].rearrange("p t b -> p b t"))
+            else:
+                nc.scalar.copy(out=grouped[:, g, :, :], in_=planar[:, g, :, :].rearrange("p t b -> p b t"))
+
+        def quant(ln, g):
+            nc.vector.quantize_mx(out=code[ln][:, g, :].bitcast(FP8X4), scales=plane[ln][:, g, :],
+                                  in_=grouped[:, g, :, :].rearrange("p b t -> p (b t)"))
+
+        mxcols = {"r0": (wg, 0), "r1": (wg, 512), "r2": (wg, 1024), "r3": (wg, 1536),
+                  "g00": (wg, 2048), "g01": (wg, 2560), "g10": (wg, 3072), "g11": (wg, 3584),
+                  "g20": (wg, 4096), "g21": (wg, 4608), "u0": (wu, 0), "u1": (wu, 512), "u2": (wu, 768)}
+
+        def mx(key, ln, n):
+            w, c0 = mxcols[key]
+            s0 = c0 if key[0] != "u" else 5 * D + c0
+            t_ = bank(key, [P, n], F32)
             for g in range(G):
-                nc.tensor.matmul_mx(out=acc,
-                                    lhsT=codes[:, g, :].bitcast(FP8X4), lhsT_scale=plane[:, g, :],
+                nc.tensor.matmul_mx(out=t_[:], lhsT=code[ln][:, g, :].bitcast(FP8X4), lhsT_scale=plane[ln][:, g, :],
                                     rhs=w[:, g, c0:c0 + n].bitcast(FP8X4), rhs_scale=wsc[4 * g:P, s0:s0 + n],
                                     start=(g == 0), stop=(g == G - 1))
 
-        def ln_tail(src, gains, codes, plane):
-            planar = keep.tile([P, G, 4, P], BF16, name="planar")
-            grouped = keep.tile([P, G, P, 4], BF16, name="grouped", align_bytes=64)
-            for g in range(G):
-                pt = psum.tile([P, 4, P], F32, name="pt", tag="bank")
-                for t in range(4):
-                    nc.tensor.transpose(pt[:, t, :], src[:, 512 * g + t:512 * (g + 1):4], identf[:])
-                for t in range(4):
-                    gw = gains[:, t, 0, g:g + 1]
-                    gb = gains[:, t, 1, g:g + 1]
-                    if g % 2 == 0:
-                        nc.vector.tensor_scalar(out=planar[:, g, t, :], in0=pt[:, t, :], scalar1=gw, scalar2=gb,
-                                                op0=ALU.mult, op1=ALU.add)
-                    else:
-                        nc.scalar.activation(out=planar[:, g, t, :], in_=pt[:, t, :], func=ACT.Identity,
-                                             bias=gb, scale=gw)
-                nc.vector.tensor_copy(out=grouped[:, g, :, :], in_=planar[:, g, :, :].rearrange("p t b -> p b t"))
-                nc.vector.quantize_mx(out=codes[:, g, :].bitcast(FP8X4), scales=plane[:, g, :],
-                                      in_=grouped[:, g, :, :].rearrange("p b t -> p (b t)"))
+        def r_add(j):
+            nc.vector.tensor_tensor(out=tb[:, sl(j)], in0=ps["r%d" % j][:], in1=b_r[:, sl(j)], op=ALU.add)
 
-        def normalise(dst, src, mean, rstd, nmr):
-            for g in range(G):
-                sl = slice(512 * g, 512 * (g + 1))
-                if g % 2 == 0:
-                    nc.vector.tensor_scalar(out=dst[:, sl], in0=src[:, sl], scalar1=mean, scalar2=rstd,
-                                            op0=ALU.subtract, op1=ALU.mult)
-                else:
-                    nc.scalar.activation(out=dst[:, sl], in_=src[:, sl], func=ACT.Identity, bias=nmr, scale=rstd)
+        def r_tanh(j):
+            nc.scalar.activation(out=tb[:, sl(j)], in_=tb[:, sl(j)], func=ACT.Tanh, scale=0.5)
 
-        st = keep.tile([P, 4, 6], F32, name="st")
-        for j in range(4):
-            nc.vector.bn_stats(out=st[:, j, :], in_=xh[:, 512 * j:512 * (j + 1)])
-        mv = keep.tile([P, 2], F32, name="mv")
-        nc.vector.bn_aggr(out=mv[:], in_=st[:].rearrange("p a b -> p (a b)"))
-        vpe1 = keep.tile([P, 1], F32, name="vpe1")
-        nc.vector.tensor_scalar(out=vpe1[:], in0=mv[:, 1:2], scalar1=EPS, scalar2=None, op0=ALU.add)
-        rstd1 = keep.tile([P, 1], F32, name="rstd1")
-        nc.gpsimd.tensor_tensor(out=rstd1[:], in0=vpe1[:], in1=mhalf[:], op=ALU.pow)
-        nmr1 = keep.tile([P, 1], F32, name="nmr1")
-        nc.vector.tensor_scalar(out=nmr1[:], in0=mv[:, 0:1], scalar1=rstd1[:, 0:1], scalar2=-1.0,
-                                op0=ALU.mult, op1=ALU.mult)
-
-        vp1 = psum.tile([P, 4, P], BF16, name="vp1", tag="bank")
-        for t in range(4):
-            nc.tensor.transpose(vp1[:, t, :], rows1[:, t:512:4], identb[:])
-        vt1 = keep.tile([P, 4, 12], F32, name="vt1")
-        nc.vector.tensor_copy(out=vt1[:], in_=vp1[:, :, 0:12])
-        mask_b = vt1[:, :, 8:12].unsqueeze(2).to_broadcast([P, 4, 2, 4])
-        gains1 = keep.tile([P, 4, 2, 4], F32, name="gains1")
-        nc.vector.tensor_tensor(out=gains1[:], in0=vt1[:, :, 0:8].rearrange("p t (v g) -> p t v g", v=2),
-                                in1=mask_b, op=ALU.mult)
-
-        nrm = keep.tile([P, K], F32, name="nrm")
-        normalise(nrm, xh, mv[:, 0:1], rstd1[:, 0:1], nmr1[:, 0:1])
-        acode = keep.tile([P, G, P], U32, name="acode", align_bytes=64)
-        aplane = keep.tile([P, G, P], U8, name="aplane", align_bytes=64)
-        ln_tail(nrm, gains1, acode, aplane)
-
-        vp2 = psum.tile([P, 4, P], BF16, name="vp2", tag="bank")
-        for t in range(4):
-            nc.tensor.transpose(vp2[:, t, :], rows2[:, t:512:4], identb[:])
-        vt2 = keep.tile([P, 4, 8], F32, name="vt2")
-        nc.vector.tensor_copy(out=vt2[:], in_=vp2[:, :, 0:8])
-        gains2 = keep.tile([P, 4, 2, 4], F32, name="gains2")
-        nc.vector.tensor_tensor(out=gains2[:], in0=vt2[:].rearrange("p t (v g) -> p t v g", v=2),
-                                in1=mask_b, op=ALU.mult)
-
-        seld = keep.tile([P, 4], BF16, name="seld")
-        nc.vector.tensor_tensor(out=seld[:, 0:2], in0=identb[:, 12:14], in1=identb[:, 16:18], op=ALU.subtract)
-        nc.vector.tensor_tensor(out=seld[:, 2:4], in0=identb[:, 14:16], in1=identb[:, 16:18], op=ALU.subtract)
-
-        def spread(sel, dst):
-            pb = psum.tile([P, 512], F32, name="pb", tag="bank")
-            nc.tensor.matmul(pb[:], lhsT=sel.to_broadcast([P, P]), rhs=rows2[:], start=True, stop=True)
-            nc.scalar.copy(out=dst, in_=pb[:])
-
-        b_r = keep.tile([P, K], F32, name="b_r")
-        b_z = keep.tile([P, 2, D], F32, name="b_z")
-        b_u = keep.tile([P, D], F32, name="b_u")
-        for j in range(4):
-            spread(identb[:, 8 + j:9 + j], b_r[:, 512 * j:512 * (j + 1)])
-        for i in range(2):
-            for c in range(2):
-                spread(seld[:, 2 * i + c:2 * i + c + 1], b_z[:, i, 512 * c:512 * (c + 1)])
-        for c in range(2):
-            spread(identb[:, 18 + c:19 + c], b_u[:, 512 * c:512 * (c + 1)])
-
-        xs = keep.tile([P, D], F32, name="xs")
-        xd = keep.tile([P, D], F32, name="xd")
-        nc.gpsimd.tensor_tensor(out=xs[:], in0=xh[:, 0:D], in1=xh[:, D:K], op=ALU.add)
-        nc.gpsimd.tensor_tensor(out=xd[:], in0=xh[:, 0:D], in1=xh[:, D:K], op=ALU.subtract)
-
-        c2 = keep.tile([P, K], F32, name="c2")
-        s1 = keep.tile([P, 4], F32, name="s1")
-        s2 = keep.tile([P, 4], F32, name="s2")
-        for j in range(4):
-            sl = slice(512 * j, 512 * (j + 1))
-            acc = psum.tile([P, 512], F32, name="acc_r", tag="bank")
-            mx_group(acc[:], acode, aplane, wg, 512 * j, 512, 512 * j)
-            tb = work.tile([P, 512], F32, name="tb")
-            nc.vector.tensor_tensor(out=tb[:], in0=acc[:], in1=b_r[:, sl], op=ALU.add)
-            nc.scalar.activation(out=tb[:], in_=tb[:], func=ACT.Tanh, scale=0.5)
-            nc.vector.scalar_tensor_tensor(out=c2[:, sl], in0=tb[:], scalar=1.0, in1=xh[:, sl],
+        def r_mul(j):
+            nc.vector.scalar_tensor_tensor(out=c2[:, sl(j)], in0=tb[:, sl(j)], scalar=1.0, in1=xh[:, sl(j)],
                                            op0=ALU.add, op1=ALU.mult, accum_out=s1[:, j:j + 1])
-            junk = work.tile([P, 512], BF16, name="junk")
-            nc.scalar.activation(out=junk[:], in_=c2[:, sl], func=ACT.Square, accum_out=s2[:, j:j + 1])
 
-        a1 = keep.tile([P, 1], F32, name="a1")
-        a2 = keep.tile([P, 1], F32, name="a2")
-        nc.vector.tensor_reduce(out=a1[:], in_=s1[:], axis=AX.X, op=ALU.add)
-        nc.vector.tensor_reduce(out=a2[:], in_=s2[:], axis=AX.X, op=ALU.add)
-        mean2 = keep.tile([P, 1], F32, name="mean2")
-        nc.vector.tensor_scalar(out=mean2[:], in0=a1[:], scalar1=1.0 / K, scalar2=None, op0=ALU.mult)
-        msq = keep.tile([P, 1], F32, name="msq")
-        nc.vector.tensor_scalar(out=msq[:], in0=mean2[:], scalar1=mean2[:, 0:1], scalar2=4.0 * EPS,
-                                op0=ALU.mult, op1=ALU.subtract)
-        vpe2 = keep.tile([P, 1], F32, name="vpe2")
-        nc.vector.scalar_tensor_tensor(out=vpe2[:], in0=a2[:], scalar=1.0 / K, in1=msq[:],
-                                       op0=ALU.mult, op1=ALU.subtract)
-        rstd2 = keep.tile([P, 1], F32, name="rstd2")
-        nc.gpsimd.tensor_tensor(out=rstd2[:], in0=vpe2[:], in1=mhalf[:], op=ALU.pow)
-        nmr2 = keep.tile([P, 1], F32, name="nmr2")
-        nc.vector.tensor_scalar(out=nmr2[:], in0=mean2[:], scalar1=rstd2[:, 0:1], scalar2=-1.0,
-                                op0=ALU.mult, op1=ALU.mult)
-        normalise(c2, c2, mean2[:, 0:1], rstd2[:, 0:1], nmr2[:, 0:1])
-        ucode = keep.tile([P, G, P], U32, name="ucode", align_bytes=64)
-        uplane = keep.tile([P, G, P], U8, name="uplane", align_bytes=64)
-        ln_tail(c2, gains2, ucode, uplane)
+        def r_sq(j):
+            nc.scalar.activation(out=junk[:], in_=c2[:, sl(j)], func=ACT.Square, accum_out=s2[:, j:j + 1])
 
-        t0 = keep.tile([P, D], F32, name="t0")
-        t1 = keep.tile([P, D], F32, name="t1")
-        dp = keep.tile([P, D], F32, name="dp")
-        for c in range(2):
-            sl = slice(512 * c, 512 * (c + 1))
-            acc = psum.tile([P, 512], F32, name="acc0", tag="bank")
-            mx_group(acc[:], acode, aplane, wg, 2048 + 512 * c, 512, 2048 + 512 * c)
-            nc.vector.tensor_tensor(out=t0[:, sl], in0=acc[:], in1=b_z[:, 0, sl], op=ALU.add)
-        for c in range(2):
-            sl = slice(512 * c, 512 * (c + 1))
-            acc = psum.tile([P, 512], F32, name="acc1", tag="bank")
-            mx_group(acc[:], acode, aplane, wg, 3072 + 512 * c, 512, 3072 + 512 * c)
-            nc.vector.tensor_tensor(out=t1[:, sl], in0=acc[:], in1=b_z[:, 1, sl], op=ALU.add)
-            nc.vector.tensor_tensor(out=dp[:, sl], in0=t0[:, sl], in1=t1[:, sl], op=ALU.subtract)
-            nc.scalar.activation(out=dp[:, sl], in_=dp[:, sl], func=ACT.Tanh, scale=0.5)
-            nc.vector.tensor_tensor(out=dp[:, sl], in0=dp[:, sl], in1=xd[:, sl], op=ALU.mult)
-            nc.vector.tensor_tensor(out=dp[:, sl], in0=dp[:, sl], in1=xs[:, sl], op=ALU.add)
-        for c in range(2):
-            sl = slice(512 * c, 512 * (c + 1))
-            acc = psum.tile([P, 512], F32, name="acc2", tag="bank")
-            mx_group(acc[:], acode, aplane, wg, 4096 + 512 * c, 512, 4096 + 512 * c)
-            nc.vector.tensor_tensor(out=t0[:, sl], in0=t0[:, sl], in1=acc[:], op=ALU.subtract)
-            nc.vector.tensor_tensor(out=t1[:, sl], in0=t1[:, sl], in1=acc[:], op=ALU.subtract)
-            nc.scalar.activation(out=t0[:, sl], in_=t0[:, sl], func=ACT.Exp)
-            nc.scalar.activation(out=t1[:, sl], in_=t1[:, sl], func=ACT.Exp)
-            nc.vector.scalar_tensor_tensor(out=t0[:, sl], in0=t0[:, sl], scalar=1.0, in1=t1[:, sl],
+        def stats2a():
+            nc.vector.tensor_reduce(out=a1[:], in_=s1[:], axis=AX.X, op=ALU.add)
+            nc.vector.tensor_scalar(out=mean2[:], in0=a1[:], scalar1=1.0 / K, scalar2=None, op0=ALU.mult)
+            nc.vector.tensor_scalar(out=negm[2][:], in0=a1[:], scalar1=-1.0 / K, scalar2=None, op0=ALU.mult)
+            nc.vector.tensor_scalar(out=msq[:], in0=mean2[:], scalar1=mean2[:, 0:1], scalar2=4.0 * EPS,
+                                    op0=ALU.mult, op1=ALU.subtract)
+
+        def stats2b():
+            nc.vector.tensor_reduce(out=a2[:], in_=s2[:], axis=AX.X, op=ALU.add)
+            nc.vector.scalar_tensor_tensor(out=vpe[2][:], in0=a2[:], scalar=1.0 / K, in1=msq[:],
+                                           op0=ALU.mult, op1=ALU.subtract)
+
+        def z_c(i, c):
+            nc.vector.tensor_tensor(out=tz[i][:, sl(c)], in0=b_z[:, i, sl(c)], in1=ps["g2%d" % c][:], op=ALU.subtract)
+
+        def z_D(i, c):
+            nc.vector.tensor_tensor(out=tz[i][:, sl(c)], in0=ps["g%d%d" % (i, c)][:], in1=tz[i][:, sl(c)], op=ALU.add)
+
+        def z_dp(c, e):
+            eng[e].tensor_tensor(out=dp[:, sl(c)], in0=tz[0][:, sl(c)], in1=tz[1][:, sl(c)], op=ALU.subtract)
+
+        def z_ptanh(c):
+            nc.scalar.activation(out=dp[:, sl(c)], in_=dp[:, sl(c)], func=ACT.Tanh, scale=0.5)
+
+        def z_pmul(c, e):
+            eng[e].tensor_tensor(out=dp[:, sl(c)], in0=dp[:, sl(c)], in1=xsd["xd"][:, sl(c)], op=ALU.mult)
+
+        def z_padd(c, e):
+            eng[e].tensor_tensor(out=dp[:, sl(c)], in0=dp[:, sl(c)], in1=xsd["xs"][:, sl(c)], op=ALU.add)
+
+        def z_exp(i, c):
+            nc.scalar.activation(out=ez[i][:, sl(c)], in_=tz[i][:, sl(c)], func=ACT.Exp)
+
+        def z_sum(c):
+            nc.vector.scalar_tensor_tensor(out=ez[0][:, sl(c)], in0=ez[0][:, sl(c)], scalar=1.0, in1=ez[1][:, sl(c)],
                                            op0=ALU.add, op1=ALU.add)
-            nc.vector.reciprocal(out=t0[:, sl], in_=t0[:, sl])
-            nc.vector.scalar_tensor_tensor(out=dp[:, sl], in0=t0[:, sl], scalar=1.0, in1=dp[:, sl],
+
+        def z_rec(c):
+            nc.vector.reciprocal(out=ez[0][:, sl(c)], in_=ez[0][:, sl(c)])
+
+        def z_nvq(c):
+            nc.vector.scalar_tensor_tensor(out=dp[:, sl(c)], in0=ez[0][:, sl(c)], scalar=1.0, in1=dp[:, sl(c)],
                                            op0=ALU.subtract, op1=ALU.mult)
 
-        for c0, c1 in u_chunks:
-            n = c1 - c0
-            acc = psum.tile([P, n], F32, name="acc_u", tag="bank")
-            mx_group(acc[:], ucode, uplane, wu, c0, n, 5 * D + c0)
-            ub = work.tile([P, n], F32, name="ub", tag="ub")
-            nc.vector.tensor_tensor(out=ub[:], in0=acc[:], in1=b_u[:, c0:c1], op=ALU.add)
-            nc.scalar.activation(out=ub[:], in_=ub[:], func=ACT.Tanh)
-            nc.vector.tensor_tensor(out=ub[:], in0=ub[:], in1=t0[:, c0:c1], op=ALU.mult)
-            res = work.tile([P, n], F32, name="res", tag="res")
-            nc.vector.scalar_tensor_tensor(out=res[:], in0=dp[:, c0:c1], scalar=-0.5, in1=ub[:],
-                                           op0=ALU.mult, op1=ALU.add)
-            nc.sync.dma_start(out=out[:, c0:c1], in_=res[:])
+        ucols = {0: slice(0, 512), 1: slice(512, 768), 2: slice(768, 1024)}
+
+        def u_add(k):
+            nc.vector.tensor_tensor(out=ub[:, ucols[k]], in0=ps["u%d" % k][:], in1=b_u[:, ucols[k]], op=ALU.add)
+
+        def u_tanh(k):
+            nc.scalar.activation(out=ub[:, ucols[k]], in_=ub[:, ucols[k]], func=ACT.Tanh)
+
+        def u_mul(k):
+            nc.vector.tensor_tensor(out=ub[:, ucols[k]], in0=ub[:, ucols[k]], in1=ez[0][:, ucols[k]], op=ALU.mult)
+
+        def u_res(k):
+            nc.vector.scalar_tensor_tensor(out=res[:, ucols[k]], in0=dp[:, ucols[k]], scalar=-0.5,
+                                           in1=ub[:, ucols[k]], op0=ALU.mult, op1=ALU.add)
+
+        def store(k):
+            nc.sync.dma_start(out=out[:, ucols[k]], in_=res[:, ucols[k]])
+
+        init()
+        dma("SP", "x")
+        dma("S", "h")
+        dma("S", "lnw")
+        dma("S", "lnb")
+        dma("S", "mask")
+        dma("G", "bg")
+        dma("G", "ln2w")
+        dma("G", "ln2b")
+        dma("G", "bu")
+        dma("SP", "wgs0")
+        dma("SP", "wgs1")
+        dma("SP", "wgs2")
+        dma("SP", "wgs3")
+        dma("SP", "wus0")
+        dma("SP", "wus1")
+        dma("SP", "wus2")
+        dma("SP", "wus3")
+        dma("SP", "Wrx")
+        dma("SP", "Wrh")
+        dma("SP", "Wg2")
+        dma("SP", "Wg0")
+        dma("SP", "Wg1a")
+        dma("SP", "Wg1b")
+        dma("SP", "Wua")
+        dma("SP", "Wub")
+        dma("SP", "Wuc")
+        t_rows(1)
+        bn(0)
+        bn(1)
+        bn(2)
+        bn(3)
+        stats1()
+        pow_(1)
+        gains_(1)
+        norm(1, 0, "V")
+        norm(1, 2, "S")
+        t_ln(1, 0)
+        norm(1, 1, "V")
+        norm(1, 3, "S")
+        t_ln(1, 1)
+        t_ln(1, 2)
+        t_ln(1, 3)
+        evac(1, 0, "V")
+        evac(1, 1, "S")
+        regroup(1, 0, "V")
+        quant(1, 0)
+        evac(1, 2, "V")
+        evac(1, 3, "S")
+        regroup(1, 1, "V")
+        quant(1, 1)
+        regroup(1, 2, "V")
+        quant(1, 2)
+        regroup(1, 3, "V")
+        quant(1, 3)
+        t_rows(2)
+        spread_r(0)
+        spread_r(1)
+        copy_br(0)
+        copy_br(1)
+        gains_(2)
+        xsxd("xd", 0, "G")
+        xsxd("xd", 1, "G")
+        xsxd("xs", 0, "G")
+        xsxd("xs", 1, "G")
+        spread_z(0, 0)
+        mx("r0", 1, 512)
+        copy_bz(0, 0)
+        mx("r1", 1, 512)
+        r_add(0)
+        r_tanh(0)
+        spread_z(1, 0)
+        spread_z(0, 1)
+        r_add(1)
+        spread_z(1, 1)
+        copy_bz(1, 0)
+        spread_u()
+        r_mul(0)
+        r_tanh(1)
+        r_sq(0)
+        r_mul(1)
+        mx("r2", 1, 512)
+        copy_bz(0, 1)
+        r_sq(1)
+        mx("r3", 1, 512)
+        copy_bz(1, 1)
+        r_add(2)
+        copy_bu()
+        r_add(3)
+        r_tanh(2)
+        r_tanh(3)
+        r_mul(2)
+        r_mul(3)
+        r_sq(2)
+        mx("g20", 1, 512)
+        stats2a()
+        r_sq(3)
+        stats2b()
+        mx("g21", 1, 512)
+        pow_(2)
+        z_c(0, 0)
+        norm(2, 1, "G")
+        z_c(1, 0)
+        norm(2, 0, "S")
+        norm(2, 3, "G")
+        z_c(0, 1)
+        t_ln(2, 1)
+        norm(2, 2, "S")
+        z_c(1, 1)
+        t_ln(2, 0)
+        evac(2, 1, "S")
+        t_ln(2, 3)
+        t_ln(2, 2)
+        evac(2, 0, "S")
+        mx("g00", 1, 512)
+        regroup(2, 1, "V")
+        quant(2, 1)
+        evac(2, 3, "S")
+        mx("g01", 1, 512)
+        regroup(2, 0, "V")
+        z_D(0, 0)
+        quant(2, 0)
+        mx("g10", 1, 512)
+        evac(2, 2, "S")
+        regroup(2, 3, "V")
+        z_D(0, 1)
+        quant(2, 3)
+        z_exp(0, 0)
+        z_D(1, 0)
+        z_exp(0, 1)
+        regroup(2, 2, "V")
+        z_dp(0, "G")
+        mx("g11", 1, 512)
+        z_exp(1, 0)
+        quant(2, 2)
+        z_sum(0)
+        z_ptanh(0)
+        z_D(1, 1)
+        z_pmul(0, "G")
+        z_rec(0)
+        z_exp(1, 1)
+        mx("u0", 2, 512)
+        z_sum(1)
+        z_dp(1, "G")
+        z_rec(1)
+        mx("u1", 2, 256)
+        u_add(0)
+        z_padd(0, "G")
+        z_ptanh(1)
+        u_add(1)
+        u_tanh(0)
+        mx("u2", 2, 256)
+        z_pmul(1, "G")
+        u_tanh(1)
+        z_nvq(0)
+        u_add(2)
+        u_mul(0)
+        z_padd(1, "G")
+        u_tanh(2)
+        u_mul(1)
+        u_mul(2)
+        u_res(0)
+        z_nvq(1)
+        store(0)
+        u_res(1)
+        u_res(2)
+        store(1)
+        store(2)

@@ -32,8 +32,12 @@ def tile_dgrucell_w_kernel(tc, x, h, Wg_words, Wg_scales, bg, Wu_words, Wu_scale
 
         xh = keep.tile([P, K], BF16, name="xh")
         wsc = keep.tile([P, 6 * D], U8, name="wsc", align_bytes=64)
-        wg = keep.tile([P, G, 5 * D], U32, name="wg", align_bytes=64)
-        wu = keep.tile([P, G, D], U32, name="wu", align_bytes=64)
+        wcols = {"rx": ("g", 0, 1024), "rh": ("g", 1024, 2048), "g0": ("g", 2048, 3072), "g1a": ("g", 3072, 3584),
+                 "g1b": ("g", 3584, 4096), "g2": ("g", 4096, 5120),
+                 "ua": ("u", 0, 512), "ub": ("u", 512, 768), "uc": ("u", 768, 1024)}
+        wt = {}
+        for nm in wcols:
+            wt[nm] = keep.tile([P, G, wcols[nm][2] - wcols[nm][1]], U32, name="w_" + nm, align_bytes=64)
         identf = keep.tile([P, P], F32, name="identf")
         identb = keep.tile([P, P], BF16, name="identb")
         rows = {1: keep.tile([P, 512], BF16, name="rows1"), 2: keep.tile([P, 512], BF16, name="rows2")}
@@ -88,12 +92,8 @@ def tile_dgrucell_w_kernel(tc, x, h, Wg_words, Wg_scales, bg, Wu_words, Wu_scale
         wsc32 = wsc[:].bitcast(I32)
         wsrc = {"g": Wg_words.rearrange("g p n t -> g p (n t)").bitcast(I32).rearrange("g p n -> p g n"),
                 "u": Wu_words.rearrange("g p n t -> g p (n t)").bitcast(I32).rearrange("g p n -> p g n")}
-        wdst = {"g": wg[:].bitcast(I32), "u": wu[:].bitcast(I32)}
         small = {"lnw": (1, 0, 4, ln_w), "lnb": (1, 4, 8, ln_b), "mask": (1, 8, 12, dropout_mask),
                  "ln2w": (2, 0, 4, ln2_w), "ln2b": (2, 4, 8, ln2_b), "bg": (2, 8, 18, bg), "bu": (2, 18, 20, bu)}
-        wcols = {"rx": ("g", 0, 1024), "rh": ("g", 1024, 2048), "g0": ("g", 2048, 3072), "g1a": ("g", 3072, 3584),
-                 "g1b": ("g", 3584, 4096), "g2": ("g", 4096, 5120),
-                 "ua": ("u", 0, 512), "ub": ("u", 512, 768), "uc": ("u", 768, 1024)}
 
         def init():
             nc.vector.memset(wsc32, 0)
@@ -123,7 +123,7 @@ def tile_dgrucell_w_kernel(tc, x, h, Wg_words, Wg_scales, bg, Wu_words, Wu_scale
                                  in_=Wu_scales.bitcast(I32)[:, 4 * qd:4 * qd + 4, :])
             else:
                 w, c0, c1 = wcols[name[1:]]
-                eng[q].dma_start(out=wdst[w][:, :, c0:c1], in_=wsrc[w][:, :, c0:c1])
+                eng[q].dma_start(out=wt[name[1:]][:].bitcast(I32), in_=wsrc[w][:, :, c0:c1])
 
         def bn(j):
             nc.vector.bn_stats(out=st[:, j, :], in_=xh[:, sl(j)])
@@ -216,13 +216,14 @@ def tile_dgrucell_w_kernel(tc, x, h, Wg_words, Wg_scales, bg, Wu_words, Wu_scale
             nc.vector.quantize_mx(out=code[ln][:, g, :].bitcast(FP8X4), scales=plane[ln][:, g, :],
                                   in_=grouped[:, g, :, :].rearrange("p b t -> p (b t)"))
 
-        mxcols = {"r0": (wg, 0), "r1": (wg, 512), "r2": (wg, 1024), "r3": (wg, 1536),
-                  "g00": (wg, 2048), "g01": (wg, 2560), "g10": (wg, 3072), "g11": (wg, 3584),
-                  "g20": (wg, 4096), "g21": (wg, 4608), "u0": (wu, 0), "u1": (wu, 512), "u2": (wu, 768)}
+        mxcols = {"r0": ("rx", 0), "r1": ("rx", 512), "r2": ("rh", 0), "r3": ("rh", 512),
+                  "g00": ("g0", 0), "g01": ("g0", 512), "g10": ("g1a", 0), "g11": ("g1b", 0),
+                  "g20": ("g2", 0), "g21": ("g2", 512), "u0": ("ua", 0), "u1": ("ub", 0), "u2": ("uc", 0)}
 
         def mx(key, ln, n):
-            w, c0 = mxcols[key]
-            s0 = c0 if key[0] != "u" else 5 * D + c0
+            nm, c0 = mxcols[key]
+            w = wt[nm]
+            s0 = wcols[nm][1] + c0 + (5 * D if wcols[nm][0] == "u" else 0)
             t_ = bank(key, [P, n], F32)
             for g in range(G):
                 nc.tensor.matmul_mx(out=t_[:], lhsT=code[ln][:, g, :].bitcast(FP8X4), lhsT_scale=plane[ln][:, g, :],
@@ -310,10 +311,10 @@ def tile_dgrucell_w_kernel(tc, x, h, Wg_words, Wg_scales, bg, Wu_words, Wu_scale
         dma("S", "lnw")
         dma("S", "lnb")
         dma("S", "mask")
-        dma("G", "bg")
-        dma("G", "ln2w")
-        dma("G", "ln2b")
-        dma("G", "bu")
+        dma("S", "bg")
+        dma("S", "ln2w")
+        dma("S", "ln2b")
+        dma("S", "bu")
         dma("SP", "wgs0")
         dma("SP", "wgs1")
         dma("SP", "wgs2")

@@ -32,15 +32,19 @@ def tile_dgrucell_w_kernel(tc, x, h, Wg_words, Wg_scales, bg, Wu_words, Wu_scale
 
         xh = keep.tile([P, K], BF16, name="xh")
         wsc = keep.tile([P, 6 * D], U8, name="wsc", align_bytes=64)
-        wcols = {"rx": ("g", 0, 1024), "rh": ("g", 1024, 2048), "g0": ("g", 2048, 3072), "g1a": ("g", 3072, 3584),
-                 "g1b": ("g", 3584, 4096), "g2": ("g", 4096, 5120),
+        wcols = {"rx": ("g", 0, 1024), "rh": ("g", 1024, 2048), "g0": ("g", 2048, 3072), "g1": ("g", 3072, 4096),
+                 "g2a": ("g", 4096, 4608), "g2b": ("g", 4608, 5120),
                  "ua": ("u", 0, 512), "ub": ("u", 512, 768), "uc": ("u", 768, 1024)}
         wt = {}
         for nm in wcols:
             wt[nm] = keep.tile([P, G, wcols[nm][2] - wcols[nm][1]], U32, name="w_" + nm, align_bytes=64)
         identf = keep.tile([P, P], F32, name="identf")
         identb = keep.tile([P, P], BF16, name="identb")
-        rows = {1: keep.tile([P, 512], BF16, name="rows1"), 2: keep.tile([P, 512], BF16, name="rows2")}
+        rows = {1: keep.tile([P, 512], BF16, name="rows1"), 2: keep.tile([P, 512], BF16, name="rows2"),
+                3: keep.tile([P, 512], BF16, name="rows3")}
+        dummy_t = keep.tile([P, 1], F32, name="dummy_t")
+        st2 = keep.tile([P, 4, 6], F32, name="st2")
+        mv2 = keep.tile([P, 2], F32, name="mv2")
         mhalf = keep.tile([P, 1], F32, name="mhalf")
         seld = keep.tile([P, 4], BF16, name="seld")
         st = keep.tile([P, 4, 6], F32, name="st")
@@ -49,9 +53,9 @@ def tile_dgrucell_w_kernel(tc, x, h, Wg_words, Wg_scales, bg, Wu_words, Wu_scale
         negm = {1: keep.tile([P, 1], F32, name="negm1"), 2: keep.tile([P, 1], F32, name="negm2")}
         rstd = {1: keep.tile([P, 1], F32, name="rstd1"), 2: keep.tile([P, 1], F32, name="rstd2")}
         nmr = {1: keep.tile([P, 1], F32, name="nmr1"), 2: keep.tile([P, 1], F32, name="nmr2")}
-        mean2 = keep.tile([P, 1], F32, name="mean2")
-        vt = {1: keep.tile([P, 4, 12], F32, name="vt1"), 2: keep.tile([P, 4, 8], F32, name="vt2")}
+        vt = {1: keep.tile([P, 4, 12], F32, name="vt1"), 3: keep.tile([P, 4, 8], F32, name="vt3")}
         gains = {1: keep.tile([P, 4, 2, 4], F32, name="gains1"), 2: keep.tile([P, 4, 2, 4], F32, name="gains2")}
+        gains[3] = gains[2]
         nrm = keep.tile([P, K], F32, name="nrm")
         c2 = keep.tile([P, K], F32, name="c2")
         planar = keep.tile([P, G, 4, P], BF16, name="planar")
@@ -65,14 +69,10 @@ def tile_dgrucell_w_kernel(tc, x, h, Wg_words, Wg_scales, bg, Wu_words, Wu_scale
         b_u = keep.tile([P, D], BF16, name="b_u")
         xsd = {"xs": keep.tile([P, D], F32, name="xs"), "xd": keep.tile([P, D], F32, name="xd")}
         tb = keep.tile([P, K], F32, name="tb")
-        junk = keep.tile([P, 512], BF16, name="junk")
-        s1 = keep.tile([P, 4], F32, name="s1")
-        s2 = keep.tile([P, 4], F32, name="s2")
-        a1 = keep.tile([P, 1], F32, name="a1")
-        a2 = keep.tile([P, 1], F32, name="a2")
-        msq = keep.tile([P, 1], F32, name="msq")
-        tz = {0: keep.tile([P, D], F32, name="t0"), 1: keep.tile([P, D], F32, name="t1")}
-        ez = {0: keep.tile([P, D], F32, name="e0"), 1: keep.tile([P, D], F32, name="e1")}
+        t1 = keep.tile([P, D], F32, name="t1")
+        tp = keep.tile([P, D], F32, name="tp")
+        rt = keep.tile([P, D], F32, name="rt")
+        at = keep.tile([P, D], F32, name="at")
         dp = keep.tile([P, D], F32, name="dp")
         ub = keep.tile([P, D], F32, name="ub")
         res = keep.tile([P, D], F32, name="res")
@@ -93,17 +93,18 @@ def tile_dgrucell_w_kernel(tc, x, h, Wg_words, Wg_scales, bg, Wu_words, Wu_scale
         wsrc = {"g": Wg_words.rearrange("g p n t -> g p (n t)").bitcast(I32).rearrange("g p n -> p g n"),
                 "u": Wu_words.rearrange("g p n t -> g p (n t)").bitcast(I32).rearrange("g p n -> p g n")}
         small = {"lnw": (1, 0, 4, ln_w), "lnb": (1, 4, 8, ln_b), "mask": (1, 8, 12, dropout_mask),
-                 "ln2w": (2, 0, 4, ln2_w), "ln2b": (2, 4, 8, ln2_b), "bg": (2, 8, 18, bg), "bu": (2, 18, 20, bu)}
+                 "ln2w": (3, 0, 4, ln2_w), "ln2b": (3, 4, 8, ln2_b), "bg": (2, 0, 10, bg), "bu": (3, 8, 10, bu)}
 
         def init():
-            nc.vector.memset(wsc32, 0)
             nc.vector.memset(rows[1][:], 0.0)
             nc.vector.memset(rows[2][:], 0.0)
+            nc.vector.memset(wsc32, 0)
+            nc.vector.memset(rows[3][:], 0.0)
             nc.vector.memset(mhalf[:], -0.5)
             make_identity(nc, identb[:])
             make_identity(nc, identf[:])
-            nc.vector.tensor_tensor(out=seld[:, 0:2], in0=identb[:, 12:14], in1=identb[:, 16:18], op=ALU.subtract)
-            nc.vector.tensor_tensor(out=seld[:, 2:4], in0=identb[:, 14:16], in1=identb[:, 16:18], op=ALU.subtract)
+            nc.vector.tensor_tensor(out=seld[:, 0:2], in0=identb[:, 4:6], in1=identb[:, 6:8], op=ALU.subtract)
+            nc.vector.tensor_tensor(out=seld[:, 2:4], in0=identb[:, 6:8], in1=identb[:, 8:10], op=ALU.subtract)
 
         def dma(q, name):
             if name == "x":
@@ -124,6 +125,9 @@ def tile_dgrucell_w_kernel(tc, x, h, Wg_words, Wg_scales, bg, Wu_words, Wu_scale
             else:
                 w, c0, c1 = wcols[name[1:]]
                 eng[q].dma_start(out=wt[name[1:]][:].bitcast(I32), in_=wsrc[w][:, :, c0:c1])
+
+        def dummy():
+            nc.scalar.activation(out=dummy_t[:], in_=mhalf[:], func=ACT.Tanh)
 
         def bn(j):
             nc.vector.bn_stats(out=st[:, j, :], in_=xh[:, sl(j)])
@@ -148,46 +152,51 @@ def tile_dgrucell_w_kernel(tc, x, h, Wg_words, Wg_scales, bg, Wu_words, Wu_scale
             nc.vector.tensor_tensor(out=gains[i][:], in0=vt[i][:, :, 0:8].rearrange("p t (v g) -> p t v g", v=2),
                                     in1=vt[1][:, :, 8:12].unsqueeze(2).to_broadcast([P, 4, 2, 4]), op=ALU.mult)
 
-        def spread2(key, r0):
+        def spread2(key, i, r0):
             t_ = bank(key, [P, 1024], BF16)
             for c in range(2):
-                nc.tensor.matmul(t_[:, sl(c)], lhsT=identb[:, r0 + c:r0 + c + 1].to_broadcast([P, P]), rhs=rows[2][:],
+                nc.tensor.matmul(t_[:, sl(c)], lhsT=identb[:, r0 + c:r0 + c + 1].to_broadcast([P, P]), rhs=rows[i][:],
                                  start=True, stop=True)
 
         def spread_r(i):
-            spread2(("br", i), 8 + 2 * i)
+            spread2(("br", i), 2, 2 * i)
 
         def copy_br(i):
             nc.scalar.copy(out=b_r[:, 1024 * i:1024 * (i + 1)], in_=ps["br", i][:])
 
         def spread_u():
-            spread2("bu", 18)
+            spread2("bu", 3, 8)
 
         def copy_bu():
             nc.scalar.copy(out=b_u[:], in_=ps["bu"][:])
 
         def spread_z(i, c):
             t_ = bank(("bz", i, c), [P, 512], F32)
-            nc.tensor.matmul(t_[:], lhsT=seld[:, 2 * i + c:2 * i + c + 1].to_broadcast([P, P]), rhs=rows[2][:],
+            nc.tensor.matmul(t_[:], lhsT=seld[:, 4 - 2 * i + c:5 - 2 * i + c].to_broadcast([P, P]), rhs=rows[2][:],
                              start=True, stop=True)
 
         def copy_bz(i, c):
-            nc.scalar.copy(out=b_z[:, i, sl(c)], in_=ps["bz", i, c][:])
+            nc.scalar.copy(out=b_z[:, i - 1, sl(c)], in_=ps["bz", i, c][:])
 
-        def xsxd(name, c, e):
-            eng[e].tensor_tensor(out=xsd[name][:, sl(c)], in0=xh[:, sl(c)], in1=xh[:, sl(c + 2)],
-                                 op=(ALU.add if name == "xs" else ALU.subtract))
+        def xsxd(name, c):
+            nc.gpsimd.tensor_tensor(out=xsd[name][:, sl(c)], in0=xh[:, sl(c)], in1=xh[:, sl(c + 2)],
+                                    op=(ALU.add if name == "xs" else ALU.subtract))
+            nc.gpsimd.tensor_scalar(out=xsd[name][:, sl(c)], in0=xsd[name][:, sl(c)], scalar1=0.25, scalar2=0.0,
+                                    op0=ALU.mult, op1=ALU.add)
 
         def norm(ln, g, e):
             src = xh if ln == 1 else c2
             dst = nrm if ln == 1 else c2
-            mean = mv[:, 0:1] if ln == 1 else mean2[:, 0:1]
+            mean = mv[:, 0:1] if ln == 1 else mv2[:, 0:1]
             if e == "S":
                 nc.scalar.activation(out=dst[:, sl(g)], in_=src[:, sl(g)], func=ACT.Identity,
                                      bias=nmr[ln][:, 0:1], scale=rstd[ln][:, 0:1])
+            elif e == "G":
+                nc.gpsimd.tensor_scalar(out=dst[:, sl(g)], in0=src[:, sl(g)], scalar1=negm[ln][:, 0:1],
+                                        scalar2=rstd[ln][:, 0:1], op0=ALU.add, op1=ALU.mult)
             else:
-                eng[e].tensor_scalar(out=dst[:, sl(g)], in0=src[:, sl(g)], scalar1=mean, scalar2=rstd[ln][:, 0:1],
-                                     op0=ALU.subtract, op1=ALU.mult)
+                nc.vector.tensor_scalar(out=dst[:, sl(g)], in0=src[:, sl(g)], scalar1=mean, scalar2=rstd[ln][:, 0:1],
+                                        op0=ALU.subtract, op1=ALU.mult)
 
         def t_ln(ln, g):
             src = nrm if ln == 1 else c2
@@ -217,8 +226,8 @@ def tile_dgrucell_w_kernel(tc, x, h, Wg_words, Wg_scales, bg, Wu_words, Wu_scale
                                   in_=grouped[:, g, :, :].rearrange("p b t -> p (b t)"))
 
         mxcols = {"r0": ("rx", 0), "r1": ("rx", 512), "r2": ("rh", 0), "r3": ("rh", 512),
-                  "g00": ("g0", 0), "g01": ("g0", 512), "g10": ("g1a", 0), "g11": ("g1b", 0),
-                  "g20": ("g2", 0), "g21": ("g2", 512), "u0": ("ua", 0), "u1": ("ub", 0), "u2": ("uc", 0)}
+                  "g00": ("g0", 0), "g01": ("g0", 512), "g10": ("g1", 0), "g11": ("g1", 512),
+                  "g20": ("g2a", 0), "g21": ("g2b", 0), "u0": ("ua", 0), "u1": ("ub", 0), "u2": ("uc", 0)}
 
         def mx(key, ln, n):
             nm, c0 = mxcols[key]
@@ -238,54 +247,52 @@ def tile_dgrucell_w_kernel(tc, x, h, Wg_words, Wg_scales, bg, Wu_words, Wu_scale
 
         def r_mul(j):
             nc.vector.scalar_tensor_tensor(out=c2[:, sl(j)], in0=tb[:, sl(j)], scalar=1.0, in1=xh[:, sl(j)],
-                                           op0=ALU.add, op1=ALU.mult, accum_out=s1[:, j:j + 1])
+                                           op0=ALU.add, op1=ALU.mult)
 
-        def r_sq(j):
-            nc.scalar.activation(out=junk[:], in_=c2[:, sl(j)], func=ACT.Square, accum_out=s2[:, j:j + 1])
+        def r_bn(j):
+            nc.vector.bn_stats(out=st2[:, j, :], in_=c2[:, sl(j)])
 
-        def stats2a():
-            nc.vector.tensor_reduce(out=a1[:], in_=s1[:], axis=AX.X, op=ALU.add)
-            nc.vector.tensor_scalar(out=mean2[:], in0=a1[:], scalar1=1.0 / K, scalar2=None, op0=ALU.mult)
-            nc.vector.tensor_scalar(out=negm[2][:], in0=a1[:], scalar1=-1.0 / K, scalar2=None, op0=ALU.mult)
-            nc.vector.tensor_scalar(out=msq[:], in0=mean2[:], scalar1=mean2[:, 0:1], scalar2=4.0 * EPS,
-                                    op0=ALU.mult, op1=ALU.subtract)
+        def stats2():
+            nc.vector.bn_aggr(out=mv2[:], in_=st2[:].rearrange("p a b -> p (a b)"))
+            nc.vector.tensor_scalar(out=vpe[2][:], in0=mv2[:, 1:2], scalar1=4.0 * EPS, scalar2=None, op0=ALU.add)
+            nc.vector.tensor_scalar(out=negm[2][:], in0=mv2[:, 0:1], scalar1=-1.0, scalar2=None, op0=ALU.mult)
 
-        def stats2b():
-            nc.vector.tensor_reduce(out=a2[:], in_=s2[:], axis=AX.X, op=ALU.add)
-            nc.vector.scalar_tensor_tensor(out=vpe[2][:], in0=a2[:], scalar=1.0 / K, in1=msq[:],
-                                           op0=ALU.mult, op1=ALU.subtract)
+        def z_t0p(c):
+            nc.vector.tensor_tensor(out=dp[:, sl(c)], in0=ps["g0%d" % c][:], in1=b_z[:, 1, sl(c)], op=ALU.add)
 
-        def z_c(i, c):
-            nc.vector.tensor_tensor(out=tz[i][:, sl(c)], in0=b_z[:, i, sl(c)], in1=ps["g2%d" % c][:], op=ALU.subtract)
+        def z_dp(c):
+            nc.vector.tensor_tensor(out=dp[:, sl(c)], in0=dp[:, sl(c)], in1=ps["g1%d" % c][:], op=ALU.subtract)
 
-        def z_D(i, c):
-            nc.vector.tensor_tensor(out=tz[i][:, sl(c)], in0=ps["g%d%d" % (i, c)][:], in1=tz[i][:, sl(c)], op=ALU.add)
-
-        def z_dp(c, e):
-            eng[e].tensor_tensor(out=dp[:, sl(c)], in0=tz[0][:, sl(c)], in1=tz[1][:, sl(c)], op=ALU.subtract)
+        def z_t(i, c):
+            nc.vector.tensor_tensor(out=t1[:, sl(c)], in0=ps["g1%d" % c][:], in1=b_z[:, 0, sl(c)], op=ALU.add)
 
         def z_ptanh(c):
-            nc.scalar.activation(out=dp[:, sl(c)], in_=dp[:, sl(c)], func=ACT.Tanh, scale=0.5)
+            nc.scalar.activation(out=tp[:, sl(c)], in_=dp[:, sl(c)], func=ACT.Tanh, scale=0.5)
+
+        def z_abs(c):
+            nc.scalar.activation(out=at[:, sl(c)], in_=tp[:, sl(c)], func=ACT.Abs)
+
+        def z_ln(c):
+            nc.scalar.activation(out=at[:, sl(c)], in_=at[:, sl(c)], func=ACT.Ln, bias=0.5, scale=0.5)
+
+        def z_rt(c):
+            nc.vector.scalar_tensor_tensor(out=rt[:, sl(c)], in0=dp[:, sl(c)], scalar=0.0, in1=t1[:, sl(c)],
+                                           op0=ALU.max, op1=ALU.add)
+
+        def z_ar(c):
+            nc.vector.tensor_tensor(out=rt[:, sl(c)], in0=ps["g2%d" % c][:], in1=rt[:, sl(c)], op=ALU.subtract)
+
+        def z_arg(c):
+            nc.vector.tensor_tensor(out=at[:, sl(c)], in0=at[:, sl(c)], in1=rt[:, sl(c)], op=ALU.add)
 
         def z_pmul(c, e):
-            eng[e].tensor_tensor(out=dp[:, sl(c)], in0=dp[:, sl(c)], in1=xsd["xd"][:, sl(c)], op=ALU.mult)
+            eng[e].tensor_tensor(out=tp[:, sl(c)], in0=tp[:, sl(c)], in1=xsd["xd"][:, sl(c)], op=ALU.mult)
 
         def z_padd(c, e):
-            eng[e].tensor_tensor(out=dp[:, sl(c)], in0=dp[:, sl(c)], in1=xsd["xs"][:, sl(c)], op=ALU.add)
+            eng[e].tensor_tensor(out=tp[:, sl(c)], in0=tp[:, sl(c)], in1=xsd["xs"][:, sl(c)], op=ALU.add)
 
-        def z_exp(i, c):
-            nc.scalar.activation(out=ez[i][:, sl(c)], in_=tz[i][:, sl(c)], func=ACT.Exp)
-
-        def z_sum(c):
-            nc.vector.scalar_tensor_tensor(out=ez[0][:, sl(c)], in0=ez[0][:, sl(c)], scalar=1.0, in1=ez[1][:, sl(c)],
-                                           op0=ALU.add, op1=ALU.add)
-
-        def z_rec(c):
-            nc.vector.reciprocal(out=ez[0][:, sl(c)], in_=ez[0][:, sl(c)])
-
-        def z_nvq(c):
-            nc.vector.scalar_tensor_tensor(out=dp[:, sl(c)], in0=ez[0][:, sl(c)], scalar=1.0, in1=dp[:, sl(c)],
-                                           op0=ALU.subtract, op1=ALU.mult)
+        def z_qtanh(c):
+            nc.scalar.activation(out=at[:, sl(c)], in_=at[:, sl(c)], func=ACT.Tanh, scale=0.5)
 
         ucols = {0: slice(0, 512), 1: slice(512, 768), 2: slice(768, 1024)}
 
@@ -295,12 +302,17 @@ def tile_dgrucell_w_kernel(tc, x, h, Wg_words, Wg_scales, bg, Wu_words, Wu_scale
         def u_tanh(k):
             nc.scalar.activation(out=ub[:, ucols[k]], in_=ub[:, ucols[k]], func=ACT.Tanh)
 
-        def u_mul(k):
-            nc.vector.tensor_tensor(out=ub[:, ucols[k]], in0=ub[:, ucols[k]], in1=ez[0][:, ucols[k]], op=ALU.mult)
+        def u_du(k):
+            nc.vector.scalar_tensor_tensor(out=ub[:, ucols[k]], in0=ub[:, ucols[k]], scalar=0.5, in1=tp[:, ucols[k]],
+                                           op0=ALU.mult, op1=ALU.subtract)
 
-        def u_res(k):
-            nc.vector.scalar_tensor_tensor(out=res[:, ucols[k]], in0=dp[:, ucols[k]], scalar=-0.5,
-                                           in1=ub[:, ucols[k]], op0=ALU.mult, op1=ALU.add)
+        def u_prod(k):
+            nc.vector.scalar_tensor_tensor(out=ub[:, ucols[k]], in0=at[:, ucols[k]], scalar=1.0, in1=ub[:, ucols[k]],
+                                           op0=ALU.add, op1=ALU.mult)
+
+        def u_out(k):
+            nc.vector.scalar_tensor_tensor(out=res[:, ucols[k]], in0=tp[:, ucols[k]], scalar=2.0, in1=ub[:, ucols[k]],
+                                           op0=ALU.mult, op1=ALU.add)
 
         def store(k):
             nc.sync.dma_start(out=out[:, ucols[k]], in_=res[:, ucols[k]])
@@ -308,30 +320,31 @@ def tile_dgrucell_w_kernel(tc, x, h, Wg_words, Wg_scales, bg, Wu_words, Wu_scale
         init()
         dma("SP", "x")
         dma("S", "h")
-        dma("S", "lnw")
-        dma("S", "lnb")
-        dma("S", "mask")
-        dma("S", "bg")
-        dma("S", "ln2w")
-        dma("S", "ln2b")
-        dma("S", "bu")
+        dma("SP", "lnw")
+        dma("SP", "lnb")
+        dma("SP", "mask")
+        dma("SP", "bg")
         dma("SP", "wgs0")
         dma("SP", "wgs1")
         dma("SP", "wgs2")
         dma("SP", "wgs3")
+        dma("SP", "Wrx")
+        dma("SP", "Wrh")
+        dma("SP", "ln2w")
+        dma("SP", "ln2b")
+        dma("SP", "bu")
+        dma("SP", "Wg0")
+        dma("SP", "Wg1")
         dma("SP", "wus0")
         dma("SP", "wus1")
         dma("SP", "wus2")
         dma("SP", "wus3")
-        dma("SP", "Wrx")
-        dma("SP", "Wrh")
-        dma("SP", "Wg2")
-        dma("SP", "Wg0")
-        dma("SP", "Wg1a")
-        dma("SP", "Wg1b")
+        dma("SP", "Wg2a")
+        dma("SP", "Wg2b")
         dma("SP", "Wua")
         dma("SP", "Wub")
         dma("SP", "Wuc")
+        dummy()
         t_rows(1)
         bn(0)
         bn(1)
@@ -360,116 +373,116 @@ def tile_dgrucell_w_kernel(tc, x, h, Wg_words, Wg_scales, bg, Wu_words, Wu_scale
         quant(1, 2)
         regroup(1, 3, "V")
         quant(1, 3)
-        t_rows(2)
         spread_r(0)
         spread_r(1)
         copy_br(0)
         copy_br(1)
-        gains_(2)
-        xsxd("xd", 0, "G")
-        xsxd("xd", 1, "G")
-        xsxd("xs", 0, "G")
-        xsxd("xs", 1, "G")
-        spread_z(0, 0)
+        xsxd("xd", 0)
+        xsxd("xd", 1)
+        xsxd("xs", 0)
+        xsxd("xs", 1)
         mx("r0", 1, 512)
-        copy_bz(0, 0)
         mx("r1", 1, 512)
+        spread_z(2, 0)
+        spread_z(2, 1)
+        spread_z(1, 0)
+        spread_z(1, 1)
         r_add(0)
         r_tanh(0)
-        spread_z(1, 0)
-        spread_z(0, 1)
         r_add(1)
-        spread_z(1, 1)
-        copy_bz(1, 0)
-        spread_u()
-        r_mul(0)
         r_tanh(1)
-        r_sq(0)
+        copy_bz(2, 0)
+        copy_bz(2, 1)
+        r_mul(0)
+        r_bn(0)
         r_mul(1)
-        mx("r2", 1, 512)
-        copy_bz(0, 1)
-        r_sq(1)
-        mx("r3", 1, 512)
+        r_bn(1)
+        copy_bz(1, 0)
         copy_bz(1, 1)
+        mx("r2", 1, 512)
+        mx("r3", 1, 512)
+        t_rows(3)
+        spread_u()
         r_add(2)
-        copy_bu()
-        r_add(3)
         r_tanh(2)
+        r_add(3)
         r_tanh(3)
+        gains_(3)
         r_mul(2)
         r_mul(3)
-        r_sq(2)
-        mx("g20", 1, 512)
-        stats2a()
-        r_sq(3)
-        stats2b()
-        mx("g21", 1, 512)
+        r_bn(2)
+        r_bn(3)
+        copy_bu()
+        stats2()
         pow_(2)
-        z_c(0, 0)
-        norm(2, 1, "G")
-        z_c(1, 0)
-        norm(2, 0, "S")
-        norm(2, 3, "G")
-        z_c(0, 1)
-        t_ln(2, 1)
-        norm(2, 2, "S")
-        z_c(1, 1)
-        t_ln(2, 0)
-        evac(2, 1, "S")
-        t_ln(2, 3)
-        t_ln(2, 2)
-        evac(2, 0, "S")
         mx("g00", 1, 512)
+        mx("g01", 1, 512)
+        z_t0p(0)
+        z_t0p(1)
+        norm(2, 0, "S")
+        norm(2, 1, "G")
+        t_ln(2, 0)
+        norm(2, 2, "S")
+        norm(2, 3, "G")
+        t_ln(2, 1)
+        t_ln(2, 2)
+        t_ln(2, 3)
+        mx("g10", 1, 512)
+        mx("g11", 1, 512)
+        evac(2, 0, "V")
+        evac(2, 1, "S")
+        regroup(2, 0, "V")
+        quant(2, 0)
+        evac(2, 2, "V")
+        evac(2, 3, "S")
         regroup(2, 1, "V")
         quant(2, 1)
-        evac(2, 3, "S")
-        mx("g01", 1, 512)
-        regroup(2, 0, "V")
-        z_D(0, 0)
-        quant(2, 0)
-        mx("g10", 1, 512)
-        evac(2, 2, "S")
-        regroup(2, 3, "V")
-        z_D(0, 1)
-        quant(2, 3)
-        z_exp(0, 0)
-        z_D(1, 0)
-        z_exp(0, 1)
-        regroup(2, 2, "V")
-        z_dp(0, "G")
-        mx("g11", 1, 512)
-        z_exp(1, 0)
-        quant(2, 2)
-        z_sum(0)
+        z_dp(0)
         z_ptanh(0)
-        z_D(1, 1)
-        z_pmul(0, "G")
-        z_rec(0)
-        z_exp(1, 1)
-        mx("u0", 2, 512)
-        z_sum(1)
-        z_dp(1, "G")
-        z_rec(1)
-        mx("u1", 2, 256)
-        u_add(0)
-        z_padd(0, "G")
+        z_abs(0)
+        z_t(1, 0)
+        z_dp(1)
         z_ptanh(1)
+        z_abs(1)
+        z_t(1, 1)
+        z_ln(0)
+        z_ln(1)
+        regroup(2, 2, "V")
+        quant(2, 2)
+        z_rt(0)
+        regroup(2, 3, "V")
+        quant(2, 3)
+        z_rt(1)
+        z_pmul(0, "G")
+        z_padd(0, "G")
+        z_pmul(1, "G")
+        z_padd(1, "G")
+        mx("g20", 1, 512)
+        mx("g21", 1, 512)
+        z_ar(0)
+        z_ar(1)
+        z_arg(0)
+        mx("u0", 2, 512)
+        z_arg(1)
+        u_add(0)
+        mx("u1", 2, 256)
         u_add(1)
         u_tanh(0)
-        mx("u2", 2, 256)
-        z_pmul(1, "G")
+        z_qtanh(0)
+        z_qtanh(1)
         u_tanh(1)
-        z_nvq(0)
+        u_du(0)
+        u_prod(0)
+        mx("u2", 2, 256)
         u_add(2)
-        u_mul(0)
-        z_padd(1, "G")
         u_tanh(2)
-        u_mul(1)
-        u_mul(2)
-        u_res(0)
-        z_nvq(1)
+        u_out(0)
         store(0)
-        u_res(1)
-        u_res(2)
+        u_du(1)
+        u_prod(1)
+        u_out(1)
         store(1)
+        u_du(2)
+        u_prod(2)
+        u_out(2)
         store(2)

@@ -32,7 +32,7 @@ def tile_dgrucell_w_kernel(tc, x, h, Wg_words, Wg_scales, bg, Wu_words, Wu_scale
 
         xh = keep.tile([P, K], BF16, name="xh")
         wsc = keep.tile([P, 6 * D], U8, name="wsc", align_bytes=64)
-        wcols = {"rx": ("g", 0, 1024), "rh": ("g", 1024, 2048), "g0": ("g", 2048, 3072), "g1": ("g", 3072, 4096),
+        wcols = {"rx": ("g", 0, 1024), "rha": ("g", 1024, 1536), "rhb": ("g", 1536, 2048), "g0": ("g", 2048, 3072), "g1": ("g", 3072, 4096),
                  "g2a": ("g", 4096, 4608), "g2b": ("g", 4608, 5120),
                  "ua": ("u", 0, 512), "ub": ("u", 512, 768), "uc": ("u", 768, 1024)}
         wt = {}
@@ -47,6 +47,7 @@ def tile_dgrucell_w_kernel(tc, x, h, Wg_words, Wg_scales, bg, Wu_words, Wu_scale
         mv2 = keep.tile([P, 2], F32, name="mv2")
         mhalf = keep.tile([P, 1], F32, name="mhalf")
         seld = keep.tile([P, 4], BF16, name="seld")
+        negidb = keep.tile([P, P], BF16, name="negidb")
         st = keep.tile([P, 4, 6], F32, name="st")
         mv = keep.tile([P, 2], F32, name="mv")
         vpe = {1: keep.tile([P, 1], F32, name="vpe1"), 2: keep.tile([P, 1], F32, name="vpe2")}
@@ -103,6 +104,7 @@ def tile_dgrucell_w_kernel(tc, x, h, Wg_words, Wg_scales, bg, Wu_words, Wu_scale
             nc.vector.memset(mhalf[:], -0.5)
             make_identity(nc, identb[:])
             make_identity(nc, identf[:])
+            nc.vector.tensor_scalar(out=negidb[:], in0=identb[:], scalar1=-1.0, scalar2=None, op0=ALU.mult)
             nc.vector.tensor_tensor(out=seld[:, 0:2], in0=identb[:, 4:6], in1=identb[:, 6:8], op=ALU.subtract)
             nc.vector.tensor_tensor(out=seld[:, 2:4], in0=identb[:, 6:8], in1=identb[:, 8:10], op=ALU.subtract)
 
@@ -178,11 +180,14 @@ def tile_dgrucell_w_kernel(tc, x, h, Wg_words, Wg_scales, bg, Wu_words, Wu_scale
         def copy_bz(i, c):
             nc.scalar.copy(out=b_z[:, i - 1, sl(c)], in_=ps["bz", i, c][:])
 
-        def xsxd(name, c):
-            nc.gpsimd.tensor_tensor(out=xsd[name][:, sl(c)], in0=xh[:, sl(c)], in1=xh[:, sl(c + 2)],
-                                    op=(ALU.add if name == "xs" else ALU.subtract))
-            nc.gpsimd.tensor_scalar(out=xsd[name][:, sl(c)], in0=xsd[name][:, sl(c)], scalar1=0.25, scalar2=0.0,
-                                    op0=ALU.mult, op1=ALU.add)
+        def xs_mm(name, c):
+            t_ = bank((name, c), [P, 512], F32)
+            nc.tensor.matmul(t_[:], lhsT=identb[:], rhs=xh[:, sl(c)], start=True, stop=False)
+            nc.tensor.matmul(t_[:], lhsT=(identb[:] if name == "xs" else negidb[:]), rhs=xh[:, sl(c + 2)],
+                             start=False, stop=True)
+
+        def xs_cp(name, c):
+            nc.scalar.activation(out=xsd[name][:, sl(c)], in_=ps[name, c][:], func=ACT.Copy, scale=0.25)
 
         def norm(ln, g, e):
             src = xh if ln == 1 else c2
@@ -225,7 +230,7 @@ def tile_dgrucell_w_kernel(tc, x, h, Wg_words, Wg_scales, bg, Wu_words, Wu_scale
             nc.vector.quantize_mx(out=code[ln][:, g, :].bitcast(FP8X4), scales=plane[ln][:, g, :],
                                   in_=grouped[:, g, :, :].rearrange("p b t -> p (b t)"))
 
-        mxcols = {"r0": ("rx", 0), "r1": ("rx", 512), "r2": ("rh", 0), "r3": ("rh", 512),
+        mxcols = {"r0": ("rx", 0), "r1": ("rx", 512), "r2": ("rha", 0), "r3": ("rhb", 0),
                   "g00": ("g0", 0), "g01": ("g0", 512), "g10": ("g1", 0), "g11": ("g1", 512),
                   "g20": ("g2a", 0), "g21": ("g2b", 0), "u0": ("ua", 0), "u1": ("ub", 0), "u2": ("uc", 0)}
 
@@ -329,16 +334,17 @@ def tile_dgrucell_w_kernel(tc, x, h, Wg_words, Wg_scales, bg, Wu_words, Wu_scale
         dma("SP", "wgs2")
         dma("SP", "wgs3")
         dma("SP", "Wrx")
-        dma("SP", "Wrh")
         dma("SP", "ln2w")
         dma("SP", "ln2b")
         dma("SP", "bu")
+        dma("SP", "Wrha")
+        dma("SP", "Wrhb")
         dma("SP", "Wg0")
-        dma("SP", "Wg1")
         dma("SP", "wus0")
         dma("SP", "wus1")
         dma("SP", "wus2")
         dma("SP", "wus3")
+        dma("SP", "Wg1")
         dma("SP", "Wg2a")
         dma("SP", "Wg2b")
         dma("SP", "Wua")
@@ -346,6 +352,14 @@ def tile_dgrucell_w_kernel(tc, x, h, Wg_words, Wg_scales, bg, Wu_words, Wu_scale
         dma("SP", "Wuc")
         dummy()
         t_rows(1)
+        xs_mm("xd", 0)
+        xs_mm("xs", 0)
+        xs_mm("xd", 1)
+        xs_mm("xs", 1)
+        xs_cp("xd", 0)
+        xs_cp("xs", 0)
+        xs_cp("xd", 1)
+        xs_cp("xs", 1)
         bn(0)
         bn(1)
         bn(2)
@@ -375,114 +389,110 @@ def tile_dgrucell_w_kernel(tc, x, h, Wg_words, Wg_scales, bg, Wu_words, Wu_scale
         quant(1, 3)
         spread_r(0)
         spread_r(1)
+        mx("r0", 1, 512)
         copy_br(0)
         copy_br(1)
-        xsxd("xd", 0)
-        xsxd("xd", 1)
-        xsxd("xs", 0)
-        xsxd("xs", 1)
-        mx("r0", 1, 512)
         mx("r1", 1, 512)
-        spread_z(2, 0)
-        spread_z(2, 1)
-        spread_z(1, 0)
-        spread_z(1, 1)
         r_add(0)
+        mx("r2", 1, 512)
         r_tanh(0)
         r_add(1)
-        r_tanh(1)
-        copy_bz(2, 0)
-        copy_bz(2, 1)
         r_mul(0)
-        r_bn(0)
+        spread_z(2, 0)
+        r_tanh(1)
+        t_rows(3)
+        r_add(2)
+        mx("r3", 1, 512)
+        copy_bz(2, 0)
         r_mul(1)
+        r_tanh(2)
+        r_bn(0)
+        spread_z(2, 1)
+        spread_z(1, 0)
+        r_add(3)
+        spread_z(1, 1)
+        copy_bz(2, 1)
+        spread_u()
+        r_mul(2)
+        r_tanh(3)
         r_bn(1)
         copy_bz(1, 0)
-        copy_bz(1, 1)
-        mx("r2", 1, 512)
-        mx("r3", 1, 512)
-        t_rows(3)
-        spread_u()
-        r_add(2)
-        r_tanh(2)
-        r_add(3)
-        r_tanh(3)
-        gains_(3)
-        r_mul(2)
         r_mul(3)
+        copy_bz(1, 1)
         r_bn(2)
-        r_bn(3)
         copy_bu()
-        stats2()
-        pow_(2)
         mx("g00", 1, 512)
+        r_bn(3)
+        stats2()
         mx("g01", 1, 512)
+        gains_(3)
+        pow_(2)
         z_t0p(0)
-        z_t0p(1)
-        norm(2, 0, "S")
         norm(2, 1, "G")
-        t_ln(2, 0)
-        norm(2, 2, "S")
+        norm(2, 0, "S")
+        z_t0p(1)
         norm(2, 3, "G")
         t_ln(2, 1)
-        t_ln(2, 2)
-        t_ln(2, 3)
-        mx("g10", 1, 512)
-        mx("g11", 1, 512)
-        evac(2, 0, "V")
+        norm(2, 2, "S")
+        t_ln(2, 0)
         evac(2, 1, "S")
-        regroup(2, 0, "V")
-        quant(2, 0)
-        evac(2, 2, "V")
+        t_ln(2, 3)
+        evac(2, 0, "V")
+        t_ln(2, 2)
+        mx("g10", 1, 512)
         evac(2, 3, "S")
         regroup(2, 1, "V")
-        quant(2, 1)
+        evac(2, 2, "V")
+        mx("g11", 1, 512)
+        regroup(2, 0, "V")
         z_dp(0)
+        mx("g20", 1, 512)
+        regroup(2, 3, "V")
         z_ptanh(0)
-        z_abs(0)
-        z_t(1, 0)
+        regroup(2, 2, "V")
         z_dp(1)
+        z_abs(0)
+        quant(2, 1)
+        quant(2, 0)
         z_ptanh(1)
+        z_pmul(0, "G")
+        quant(2, 3)
+        quant(2, 2)
+        z_t(1, 0)
         z_abs(1)
+        mx("g21", 1, 512)
         z_t(1, 1)
         z_ln(0)
-        z_ln(1)
-        regroup(2, 2, "V")
-        quant(2, 2)
-        z_rt(0)
-        regroup(2, 3, "V")
-        quant(2, 3)
-        z_rt(1)
-        z_pmul(0, "G")
         z_padd(0, "G")
+        z_rt(0)
+        z_rt(1)
         z_pmul(1, "G")
-        z_padd(1, "G")
-        mx("g20", 1, 512)
-        mx("g21", 1, 512)
         z_ar(0)
-        z_ar(1)
-        z_arg(0)
         mx("u0", 2, 512)
-        z_arg(1)
-        u_add(0)
+        z_ar(1)
+        z_ln(1)
+        z_padd(1, "G")
+        z_arg(0)
         mx("u1", 2, 256)
-        u_add(1)
-        u_tanh(0)
+        z_arg(1)
         z_qtanh(0)
-        z_qtanh(1)
+        u_add(0)
+        u_add(1)
+        mx("u2", 2, 256)
+        u_tanh(0)
+        u_add(2)
         u_tanh(1)
         u_du(0)
+        z_qtanh(1)
         u_prod(0)
-        mx("u2", 2, 256)
-        u_add(2)
         u_tanh(2)
-        u_out(0)
-        store(0)
         u_du(1)
-        u_prod(1)
-        u_out(1)
-        store(1)
         u_du(2)
+        u_prod(1)
         u_prod(2)
+        u_out(0)
+        u_out(1)
+        store(0)
         u_out(2)
+        store(1)
         store(2)

@@ -99,10 +99,10 @@ def tile_dgrucell_w_kernel(tc, x, h, Wg_words, Wg_scales, bg, Wu_words, Wu_scale
         def init():
             nc.vector.memset(rows[1][:], 0.0)
             nc.vector.memset(rows[2][:], 0.0)
-            nc.vector.memset(wsc32, 0)
             nc.vector.memset(rows[3][:], 0.0)
             nc.vector.memset(mhalf[:], -0.5)
             make_identity(nc, identb[:])
+            nc.gpsimd.memset(wsc32, 0)
             make_identity(nc, identf[:])
             nc.vector.tensor_scalar(out=negidb[:], in0=identb[:], scalar1=-1.0, scalar2=None, op0=ALU.mult)
             nc.vector.tensor_tensor(out=seld[:, 0:2], in0=identb[:, 4:6], in1=identb[:, 6:8], op=ALU.subtract)
@@ -329,11 +329,11 @@ def tile_dgrucell_w_kernel(tc, x, h, Wg_words, Wg_scales, bg, Wu_words, Wu_scale
         dma("SP", "lnb")
         dma("SP", "mask")
         dma("SP", "bg")
+        dma("SP", "Wrx")
         dma("SP", "wgs0")
         dma("SP", "wgs1")
         dma("SP", "wgs2")
         dma("SP", "wgs3")
-        dma("SP", "Wrx")
         dma("SP", "ln2w")
         dma("SP", "ln2b")
         dma("SP", "bu")

@@ -22,7 +22,7 @@ FLOPS = 2 * 128 * 2048 * 6144
 
 
 def tile_dgrucell_w_kernel(tc, x, h, Wg_words, Wg_scales, bg, Wu_words, Wu_scales, bu,
-                                      ln_w, ln_b, ln2_w, ln2_b, dropout_mask, out):
+                                         ln_w, ln_b, ln2_w, ln2_b, dropout_mask, out):
     nc = tc.nc
     with ExitStack() as ctx:
         keep = ctx.enter_context(tc.tile_pool(name="keep", bufs=1))
@@ -32,7 +32,8 @@ def tile_dgrucell_w_kernel(tc, x, h, Wg_words, Wg_scales, bg, Wu_words, Wu_scale
 
         xh = keep.tile([P, K], BF16, name="xh")
         wsc = keep.tile([P, 6 * D], U8, name="wsc", align_bytes=64)
-        wcols = {"rx": ("g", 0, 1024), "rha": ("g", 1024, 1536), "rhb": ("g", 1536, 2048), "g0": ("g", 2048, 3072), "g1": ("g", 3072, 4096),
+        wcols = {"rx": ("g", 0, 1024), "rha": ("g", 1024, 1536), "rhb": ("g", 1536, 2048),
+                 "g0a": ("g", 2048, 2560), "g0b": ("g", 2560, 3072), "g1a": ("g", 3072, 3584), "g1b": ("g", 3584, 4096),
                  "g2a": ("g", 4096, 4608), "g2b": ("g", 4608, 5120),
                  "ua": ("u", 0, 512), "ub": ("u", 512, 768), "uc": ("u", 768, 1024)}
         wt = {}
@@ -43,11 +44,8 @@ def tile_dgrucell_w_kernel(tc, x, h, Wg_words, Wg_scales, bg, Wu_words, Wu_scale
         rows = {1: keep.tile([P, 512], BF16, name="rows1"), 2: keep.tile([P, 512], BF16, name="rows2"),
                 3: keep.tile([P, 512], BF16, name="rows3")}
         dummy_t = keep.tile([P, 1], F32, name="dummy_t")
-        st2 = keep.tile([P, 4, 6], F32, name="st2")
-        mv2 = keep.tile([P, 2], F32, name="mv2")
         mhalf = keep.tile([P, 1], F32, name="mhalf")
         seld = keep.tile([P, 4], BF16, name="seld")
-        negidb = keep.tile([P, P], BF16, name="negidb")
         st = keep.tile([P, 4, 6], F32, name="st")
         mv = keep.tile([P, 2], F32, name="mv")
         vpe = {1: keep.tile([P, 1], F32, name="vpe1"), 2: keep.tile([P, 1], F32, name="vpe2")}
@@ -65,14 +63,22 @@ def tile_dgrucell_w_kernel(tc, x, h, Wg_words, Wg_scales, bg, Wu_words, Wu_scale
                 2: keep.tile([P, G, P], U32, name="code2", align_bytes=64)}
         plane = {1: keep.tile([P, G, P], U8, name="plane1", align_bytes=64),
                  2: keep.tile([P, G, P], U8, name="plane2", align_bytes=64)}
-        b_r = keep.tile([P, K], BF16, name="b_r")
+        bucol = keep.tile([P, 4, 2], F32, name="bucol")
         b_z = keep.tile([P, 2, D], F32, name="b_z")
-        b_u = keep.tile([P, D], BF16, name="b_u")
-        xsd = {"xs": keep.tile([P, D], F32, name="xs"), "xd": keep.tile([P, D], F32, name="xd")}
+        hq = keep.tile([P, D], F32, name="hq")
+        hh = keep.tile([P, D], F32, name="hh")
+        d4 = keep.tile([P, D], F32, name="d4")
         tb = keep.tile([P, K], F32, name="tb")
-        t1 = keep.tile([P, D], F32, name="t1")
+        b_r = keep.tile([P, K], BF16, name="b_r")
+        junk = keep.tile([P, 512], F32, name="junk")
+        sacc = keep.tile([P, 2, 4], F32, name="sacc")
+        sred = keep.tile([P, 2], F32, name="sred")
+        mean2 = keep.tile([P, 1], F32, name="mean2")
+        esq = keep.tile([P, 1], F32, name="esq")
+        utt = keep.tile([P, 8, P], F32, name="utt")
+        mxt = keep.tile([P, D], F32, name="mxt")
+        bh = keep.tile([P, D], F32, name="bh")
         tp = keep.tile([P, D], F32, name="tp")
-        rt = keep.tile([P, D], F32, name="rt")
         at = keep.tile([P, D], F32, name="at")
         dp = keep.tile([P, D], F32, name="dp")
         ub = keep.tile([P, D], F32, name="ub")
@@ -94,17 +100,16 @@ def tile_dgrucell_w_kernel(tc, x, h, Wg_words, Wg_scales, bg, Wu_words, Wu_scale
         wsrc = {"g": Wg_words.rearrange("g p n t -> g p (n t)").bitcast(I32).rearrange("g p n -> p g n"),
                 "u": Wu_words.rearrange("g p n t -> g p (n t)").bitcast(I32).rearrange("g p n -> p g n")}
         small = {"lnw": (1, 0, 4, ln_w), "lnb": (1, 4, 8, ln_b), "mask": (1, 8, 12, dropout_mask),
-                 "ln2w": (3, 0, 4, ln2_w), "ln2b": (3, 4, 8, ln2_b), "bg": (2, 0, 10, bg), "bu": (3, 8, 10, bu)}
+                 "ln2w": (3, 0, 4, ln2_w), "ln2b": (3, 4, 8, ln2_b), "bg": (2, 0, 10, bg), "bu": (2, 12, 14, bu)}
 
         def init():
+            make_identity(nc, identb[:])
             nc.vector.memset(rows[1][:], 0.0)
             nc.vector.memset(rows[2][:], 0.0)
-            nc.vector.memset(rows[3][:], 0.0)
             nc.vector.memset(mhalf[:], -0.5)
-            make_identity(nc, identb[:])
+            nc.vector.memset(rows[3][:], 0.0)
             nc.gpsimd.memset(wsc32, 0)
             make_identity(nc, identf[:])
-            nc.vector.tensor_scalar(out=negidb[:], in0=identb[:], scalar1=-1.0, scalar2=None, op0=ALU.mult)
             nc.vector.tensor_tensor(out=seld[:, 0:2], in0=identb[:, 4:6], in1=identb[:, 6:8], op=ALU.subtract)
             nc.vector.tensor_tensor(out=seld[:, 2:4], in0=identb[:, 6:8], in1=identb[:, 8:10], op=ALU.subtract)
 
@@ -116,10 +121,11 @@ def tile_dgrucell_w_kernel(tc, x, h, Wg_words, Wg_scales, bg, Wu_words, Wu_scale
             elif name in small:
                 i, r0, r1, src = small[name]
                 eng[q].dma_start(out=rows[i][r0:r1, :], in_=src.rearrange("(r c) -> r c", c=512))
-            elif name[0:3] == "wgs":
+            elif name[0:3] in ("wrs", "wzs"):
                 qd = int(name[3])
-                eng[q].dma_start(out=wsc32[32 * qd:32 * qd + 16, 0:1280],
-                                 in_=Wg_scales.bitcast(I32)[:, 4 * qd:4 * qd + 4, :])
+                a, b = (0, 512) if name[1] == "r" else (512, 1280)
+                eng[q].dma_start(out=wsc32[32 * qd:32 * qd + 16, a:b],
+                                 in_=Wg_scales.bitcast(I32)[:, 4 * qd:4 * qd + 4, a:b])
             elif name[0:3] == "wus":
                 qd = int(name[3])
                 eng[q].dma_start(out=wsc32[32 * qd:32 * qd + 16, 1280:1536],
@@ -154,23 +160,23 @@ def tile_dgrucell_w_kernel(tc, x, h, Wg_words, Wg_scales, bg, Wu_words, Wu_scale
             nc.vector.tensor_tensor(out=gains[i][:], in0=vt[i][:, :, 0:8].rearrange("p t (v g) -> p t v g", v=2),
                                     in1=vt[1][:, :, 8:12].unsqueeze(2).to_broadcast([P, 4, 2, 4]), op=ALU.mult)
 
-        def spread2(key, i, r0):
-            t_ = bank(key, [P, 1024], BF16)
-            for c in range(2):
-                nc.tensor.matmul(t_[:, sl(c)], lhsT=identb[:, r0 + c:r0 + c + 1].to_broadcast([P, P]), rhs=rows[i][:],
-                                 start=True, stop=True)
+        def t_bias():
+            t_ = bank("bc", [P, 4, P], BF16)
+            for m in range(4):
+                nc.tensor.transpose(t_[:, m, :], rows[2][:, P * m:P * (m + 1)], identb[:])
+
+        def copy_bias():
+            nc.vector.tensor_copy(out=bucol[:], in_=ps["bc"][:, :, 12:14])
 
         def spread_r(i):
-            spread2(("br", i), 2, 2 * i)
+            t_ = bank(("br", i), [P, 1024], BF16)
+            for c in range(2):
+                r0 = 2 * i + c
+                nc.tensor.matmul(t_[:, sl(c)], lhsT=identb[:, r0:r0 + 1].to_broadcast([P, P]), rhs=rows[2][:],
+                                 start=True, stop=True)
 
         def copy_br(i):
             nc.scalar.copy(out=b_r[:, 1024 * i:1024 * (i + 1)], in_=ps["br", i][:])
-
-        def spread_u():
-            spread2("bu", 3, 8)
-
-        def copy_bu():
-            nc.scalar.copy(out=b_u[:], in_=ps["bu"][:])
 
         def spread_z(i, c):
             t_ = bank(("bz", i, c), [P, 512], F32)
@@ -180,28 +186,22 @@ def tile_dgrucell_w_kernel(tc, x, h, Wg_words, Wg_scales, bg, Wu_words, Wu_scale
         def copy_bz(i, c):
             nc.scalar.copy(out=b_z[:, i - 1, sl(c)], in_=ps["bz", i, c][:])
 
-        def xs_mm(name, c):
-            t_ = bank((name, c), [P, 512], F32)
-            nc.tensor.matmul(t_[:], lhsT=identb[:], rhs=xh[:, sl(c)], start=True, stop=False)
-            nc.tensor.matmul(t_[:], lhsT=(identb[:] if name == "xs" else negidb[:]), rhs=xh[:, sl(c + 2)],
-                             start=False, stop=True)
+        def h_scaled(dst, factor):
+            nc.scalar.activation(out=dst[:], in_=xh[:, D:K], func=ACT.Copy, scale=factor)
 
-        def xs_cp(name, c):
-            nc.scalar.activation(out=xsd[name][:, sl(c)], in_=ps[name, c][:], func=ACT.Copy, scale=0.25)
+        def xd(c):
+            nc.vector.scalar_tensor_tensor(out=d4[:, sl(c)], in0=xh[:, sl(c)], scalar=0.25, in1=hq[:, sl(c)],
+                                           op0=ALU.mult, op1=ALU.subtract)
 
         def norm(ln, g, e):
             src = xh if ln == 1 else c2
             dst = nrm if ln == 1 else c2
-            mean = mv[:, 0:1] if ln == 1 else mv2[:, 0:1]
             if e == "S":
                 nc.scalar.activation(out=dst[:, sl(g)], in_=src[:, sl(g)], func=ACT.Identity,
                                      bias=nmr[ln][:, 0:1], scale=rstd[ln][:, 0:1])
-            elif e == "G":
-                nc.gpsimd.tensor_scalar(out=dst[:, sl(g)], in0=src[:, sl(g)], scalar1=negm[ln][:, 0:1],
-                                        scalar2=rstd[ln][:, 0:1], op0=ALU.add, op1=ALU.mult)
             else:
-                nc.vector.tensor_scalar(out=dst[:, sl(g)], in0=src[:, sl(g)], scalar1=mean, scalar2=rstd[ln][:, 0:1],
-                                        op0=ALU.subtract, op1=ALU.mult)
+                nc.vector.tensor_scalar(out=dst[:, sl(g)], in0=src[:, sl(g)], scalar1=negm[ln][:, 0:1],
+                                        scalar2=rstd[ln][:, 0:1], op0=ALU.add, op1=ALU.mult)
 
         def t_ln(ln, g):
             src = nrm if ln == 1 else c2
@@ -220,56 +220,78 @@ def tile_dgrucell_w_kernel(tc, x, h, Wg_words, Wg_scales, bg, Wu_words, Wu_scale
                     nc.scalar.activation(out=planar[:, g, t, :], in_=ps["pt", ln, g][:, t, :], func=ACT.Identity,
                                          bias=gb, scale=gw)
 
-        def regroup(ln, g, e):
-            if e == "V":
-                nc.vector.tensor_copy(out=grouped[:, g, :, :], in_=planar[:, g, :, :].rearrange("p t b -> p b t"))
-            else:
-                nc.scalar.copy(out=grouped[:, g, :, :], in_=planar[:, g, :, :].rearrange("p t b -> p b t"))
+        def regroup(g):
+            nc.vector.tensor_copy(out=grouped[:, g, :, :], in_=planar[:, g, :, :].rearrange("p t b -> p b t"))
 
         def quant(ln, g):
             nc.vector.quantize_mx(out=code[ln][:, g, :].bitcast(FP8X4), scales=plane[ln][:, g, :],
                                   in_=grouped[:, g, :, :].rearrange("p b t -> p (b t)"))
 
-        mxcols = {"r0": ("rx", 0), "r1": ("rx", 512), "r2": ("rha", 0), "r3": ("rhb", 0),
-                  "g00": ("g0", 0), "g01": ("g0", 512), "g10": ("g1", 0), "g11": ("g1", 512),
-                  "g20": ("g2a", 0), "g21": ("g2b", 0), "u0": ("ua", 0), "u1": ("ub", 0), "u2": ("uc", 0)}
+        zcols = {"g00": "g0a", "g01": "g0b", "g10": "g1a", "g11": "g1b", "g20": "g2a", "g21": "g2b"}
 
-        def mx(key, ln, n):
-            nm, c0 = mxcols[key]
-            w = wt[nm]
-            s0 = wcols[nm][1] + c0 + (5 * D if wcols[nm][0] == "u" else 0)
-            t_ = bank(key, [P, n], F32)
+        def mx(key):
+            nm = zcols[key]
+            s0 = wcols[nm][1]
+            t_ = bank(key, [P, 512], F32)
             for g in range(G):
-                nc.tensor.matmul_mx(out=t_[:], lhsT=code[ln][:, g, :].bitcast(FP8X4), lhsT_scale=plane[ln][:, g, :],
-                                    rhs=w[:, g, c0:c0 + n].bitcast(FP8X4), rhs_scale=wsc[4 * g:P, s0:s0 + n],
+                nc.tensor.matmul_mx(out=t_[:], lhsT=code[1][:, g, :].bitcast(FP8X4), lhsT_scale=plane[1][:, g, :],
+                                    rhs=wt[nm][:, g, :].bitcast(FP8X4), rhs_scale=wsc[4 * g:P, s0:s0 + 512],
                                     start=(g == 0), stop=(g == G - 1))
 
+        def mxt_pass(dst, ln, nm, c, g):
+            s0 = wcols[nm][1] + c + (5 * D if wcols[nm][0] == "u" else 0)
+            nc.tensor.matmul_mx(out=dst, lhsT=wt[nm][:, g, c:c + P].bitcast(FP8X4), lhsT_scale=wsc[4 * g:P, s0:s0 + P],
+                                rhs=code[ln][:, g, :].bitcast(FP8X4), rhs_scale=plane[ln][:, g, :],
+                                start=(g == 0), stop=(g == G - 1))
+
+        rcols = {0: ("rx", 0), 1: ("rx", 512), 2: ("rha", 0), 3: ("rhb", 0)}
+
+        def r_pass(j, g):
+            nm, c0 = rcols[j]
+            s0 = wcols[nm][1] + c0
+            if g == 0:
+                bank(("r", j), [P, 512], F32)
+            nc.tensor.matmul_mx(out=ps["r", j][:], lhsT=code[1][:, g, :].bitcast(FP8X4), lhsT_scale=plane[1][:, g, :],
+                                rhs=wt[nm][:, g, c0:c0 + 512].bitcast(FP8X4), rhs_scale=wsc[4 * g:P, s0:s0 + 512],
+                                start=(g == 0), stop=(g == G - 1))
+
+        def r_mx(j):
+            for g in range(G):
+                r_pass(j, g)
+
         def r_add(j):
-            nc.vector.tensor_tensor(out=tb[:, sl(j)], in0=ps["r%d" % j][:], in1=b_r[:, sl(j)], op=ALU.add)
+            nc.vector.tensor_tensor(out=tb[:, sl(j)], in0=ps["r", j][:], in1=b_r[:, sl(j)], op=ALU.add)
 
         def r_tanh(j):
             nc.scalar.activation(out=tb[:, sl(j)], in_=tb[:, sl(j)], func=ACT.Tanh, scale=0.5)
 
         def r_mul(j):
             nc.vector.scalar_tensor_tensor(out=c2[:, sl(j)], in0=tb[:, sl(j)], scalar=1.0, in1=xh[:, sl(j)],
-                                           op0=ALU.add, op1=ALU.mult)
+                                           op0=ALU.add, op1=ALU.mult, accum_out=sacc[:, 0, j:j + 1])
 
-        def r_bn(j):
-            nc.vector.bn_stats(out=st2[:, j, :], in_=c2[:, sl(j)])
+        def r_sq(j):
+            nc.scalar.activation(out=junk[:], in_=c2[:, sl(j)], func=ACT.Square, accum_out=sacc[:, 1, j:j + 1])
 
         def stats2():
-            nc.vector.bn_aggr(out=mv2[:], in_=st2[:].rearrange("p a b -> p (a b)"))
-            nc.vector.tensor_scalar(out=vpe[2][:], in0=mv2[:, 1:2], scalar1=4.0 * EPS, scalar2=None, op0=ALU.add)
-            nc.vector.tensor_scalar(out=negm[2][:], in0=mv2[:, 0:1], scalar1=-1.0, scalar2=None, op0=ALU.mult)
+            nc.vector.tensor_reduce(out=sred[:], in_=sacc[:], op=ALU.add, axis=AX.X)
+            nc.vector.tensor_scalar(out=negm[2][:], in0=sred[:, 0:1], scalar1=-1.0 / K, scalar2=None, op0=ALU.mult)
+            nc.vector.tensor_scalar(out=mean2[:], in0=sred[:, 0:1], scalar1=1.0 / K, scalar2=None, op0=ALU.mult)
+            nc.vector.tensor_scalar(out=esq[:], in0=sred[:, 1:2], scalar1=1.0 / K, scalar2=4.0 * EPS,
+                                    op0=ALU.mult, op1=ALU.add)
+            nc.vector.scalar_tensor_tensor(out=vpe[2][:], in0=mean2[:], scalar=negm[2][:, 0:1], in1=esq[:],
+                                           op0=ALU.mult, op1=ALU.add)
 
         def z_t0p(c):
             nc.vector.tensor_tensor(out=dp[:, sl(c)], in0=ps["g0%d" % c][:], in1=b_z[:, 1, sl(c)], op=ALU.add)
 
+        def z_max(c):
+            nc.vector.tensor_tensor(out=mxt[:, sl(c)], in0=dp[:, sl(c)], in1=ps["g1%d" % c][:], op=ALU.max)
+
         def z_dp(c):
             nc.vector.tensor_tensor(out=dp[:, sl(c)], in0=dp[:, sl(c)], in1=ps["g1%d" % c][:], op=ALU.subtract)
 
-        def z_t(i, c):
-            nc.vector.tensor_tensor(out=t1[:, sl(c)], in0=ps["g1%d" % c][:], in1=b_z[:, 0, sl(c)], op=ALU.add)
+        def z_maxb(c):
+            nc.vector.tensor_tensor(out=mxt[:, sl(c)], in0=mxt[:, sl(c)], in1=b_z[:, 0, sl(c)], op=ALU.add)
 
         def z_ptanh(c):
             nc.scalar.activation(out=tp[:, sl(c)], in_=dp[:, sl(c)], func=ACT.Tanh, scale=0.5)
@@ -280,47 +302,70 @@ def tile_dgrucell_w_kernel(tc, x, h, Wg_words, Wg_scales, bg, Wu_words, Wu_scale
         def z_ln(c):
             nc.scalar.activation(out=at[:, sl(c)], in_=at[:, sl(c)], func=ACT.Ln, bias=0.5, scale=0.5)
 
-        def z_rt(c):
-            nc.vector.scalar_tensor_tensor(out=rt[:, sl(c)], in0=dp[:, sl(c)], scalar=0.0, in1=t1[:, sl(c)],
-                                           op0=ALU.max, op1=ALU.add)
+        def z_soft(c):
+            nc.scalar.activation(out=at[:, sl(c)], in_=dp[:, sl(c)], func=ACT.Abs)
+            nc.scalar.activation(out=at[:, sl(c)], in_=at[:, sl(c)], func=ACT.Exp, scale=-1.0)
+            nc.scalar.activation(out=at[:, sl(c)], in_=at[:, sl(c)], func=ACT.Ln, bias=1.0, scale=1.0)
 
-        def z_ar(c):
-            nc.vector.tensor_tensor(out=rt[:, sl(c)], in0=ps["g2%d" % c][:], in1=rt[:, sl(c)], op=ALU.subtract)
+        def z_pres(c):
+            nc.vector.scalar_tensor_tensor(out=at[:, sl(c)], in0=at[:, sl(c)], scalar=-1.0, in1=mxt[:, sl(c)],
+                                           op0=ALU.mult, op1=ALU.subtract)
+
+        def z_pre(c):
+            nc.vector.tensor_tensor(out=at[:, sl(c)], in0=at[:, sl(c)], in1=mxt[:, sl(c)], op=ALU.subtract)
 
         def z_arg(c):
-            nc.vector.tensor_tensor(out=at[:, sl(c)], in0=at[:, sl(c)], in1=rt[:, sl(c)], op=ALU.add)
+            nc.vector.tensor_tensor(out=at[:, sl(c)], in0=ps["g2%d" % c][:], in1=at[:, sl(c)], op=ALU.add)
 
-        def z_pmul(c, e):
-            eng[e].tensor_tensor(out=tp[:, sl(c)], in0=tp[:, sl(c)], in1=xsd["xd"][:, sl(c)], op=ALU.mult)
+        def z_pd(c):
+            nc.vector.scalar_tensor_tensor(out=bh[:, sl(c)], in0=tp[:, sl(c)], scalar=1.0, in1=d4[:, sl(c)],
+                                           op0=ALU.add, op1=ALU.mult)
 
-        def z_padd(c, e):
-            eng[e].tensor_tensor(out=tp[:, sl(c)], in0=tp[:, sl(c)], in1=xsd["xs"][:, sl(c)], op=ALU.add)
+        def z_bh(c):
+            nc.vector.tensor_tensor(out=bh[:, sl(c)], in0=bh[:, sl(c)], in1=hh[:, sl(c)], op=ALU.add)
 
         def z_qtanh(c):
             nc.scalar.activation(out=at[:, sl(c)], in_=at[:, sl(c)], func=ACT.Tanh, scale=0.5)
 
-        ucols = {0: slice(0, 512), 1: slice(512, 768), 2: slice(768, 1024)}
+        def z_na(c):
+            nc.vector.scalar_tensor_tensor(out=bh[:, sl(c)], in0=at[:, sl(c)], scalar=1.0, in1=bh[:, sl(c)],
+                                           op0=ALU.subtract, op1=ALU.mult)
 
-        def u_add(k):
-            nc.vector.tensor_tensor(out=ub[:, ucols[k]], in0=ps["u%d" % k][:], in1=b_u[:, ucols[k]], op=ALU.add)
+        uparts = {0: ("ua", 0, 4), 1: ("ub", 4, 2), 2: ("uc", 6, 2)}
+
+        def ucols(k):
+            return slice(P * uparts[k][1], P * (uparts[k][1] + uparts[k][2]))
+
+        def u_mx(k):
+            nm, i0, n = uparts[k]
+            t_ = bank(("u", k), [P, n, P], F32)
+            for m in range(n):
+                for g in range(G):
+                    mxt_pass(t_[:, m, :], 2, nm, P * m, g)
 
         def u_tanh(k):
-            nc.scalar.activation(out=ub[:, ucols[k]], in_=ub[:, ucols[k]], func=ACT.Tanh)
+            nm, i0, n = uparts[k]
+            for m in range(n):
+                i = i0 + m
+                nc.scalar.activation(out=utt[:, i, :], in_=ps["u", k][:, m, :], func=ACT.Tanh,
+                                     bias=bucol[:, i % 4, i // 4:i // 4 + 1], scale=1.0)
 
-        def u_du(k):
-            nc.vector.scalar_tensor_tensor(out=ub[:, ucols[k]], in0=ub[:, ucols[k]], scalar=0.5, in1=tp[:, ucols[k]],
-                                           op0=ALU.mult, op1=ALU.subtract)
+        def u_back(k):
+            nm, i0, n = uparts[k]
+            t_ = bank(("ubk", k), [P, n, P], F32)
+            for m in range(n):
+                nc.tensor.transpose(t_[:, m, :], utt[:, i0 + m, :], identf[:])
 
         def u_prod(k):
-            nc.vector.scalar_tensor_tensor(out=ub[:, ucols[k]], in0=at[:, ucols[k]], scalar=1.0, in1=ub[:, ucols[k]],
-                                           op0=ALU.add, op1=ALU.mult)
+            nc.vector.scalar_tensor_tensor(out=ub[:, ucols(k)], in0=at[:, ucols(k)], scalar=1.0,
+                                           in1=ps["ubk", k][:].rearrange("p m n -> p (m n)"), op0=ALU.add, op1=ALU.mult)
 
         def u_out(k):
-            nc.vector.scalar_tensor_tensor(out=res[:, ucols[k]], in0=tp[:, ucols[k]], scalar=2.0, in1=ub[:, ucols[k]],
-                                           op0=ALU.mult, op1=ALU.add)
+            nc.vector.scalar_tensor_tensor(out=res[:, ucols(k)], in0=ub[:, ucols(k)], scalar=0.5, in1=bh[:, ucols(k)],
+                                           op0=ALU.mult, op1=ALU.subtract)
 
         def store(k):
-            nc.sync.dma_start(out=out[:, ucols[k]], in_=res[:, ucols[k]])
+            nc.sync.dma_start(out=out[:, ucols(k)], in_=res[:, ucols(k)])
 
         init()
         dma("SP", "x")
@@ -329,22 +374,22 @@ def tile_dgrucell_w_kernel(tc, x, h, Wg_words, Wg_scales, bg, Wu_words, Wu_scale
         dma("SP", "lnb")
         dma("SP", "mask")
         dma("SP", "bg")
-        dma("SP", "Wrx")
-        dma("SP", "wgs0")
-        dma("SP", "wgs1")
-        dma("SP", "wgs2")
-        dma("SP", "wgs3")
-        dma("SP", "ln2w")
-        dma("SP", "ln2b")
         dma("SP", "bu")
+        dma("SP", "Wrx")
+        for q in range(4):
+            dma("SP", "wrs%d" % q)
         dma("SP", "Wrha")
         dma("SP", "Wrhb")
-        dma("SP", "Wg0")
-        dma("SP", "wus0")
-        dma("SP", "wus1")
-        dma("SP", "wus2")
-        dma("SP", "wus3")
-        dma("SP", "Wg1")
+        dma("SP", "ln2w")
+        dma("SP", "ln2b")
+        for q in range(4):
+            dma("SP", "wzs%d" % q)
+        dma("SP", "Wg0a")
+        dma("SP", "Wg1a")
+        dma("SP", "Wg0b")
+        dma("SP", "Wg1b")
+        for q in range(4):
+            dma("SP", "wus%d" % q)
         dma("SP", "Wg2a")
         dma("SP", "Wg2b")
         dma("SP", "Wua")
@@ -352,14 +397,14 @@ def tile_dgrucell_w_kernel(tc, x, h, Wg_words, Wg_scales, bg, Wu_words, Wu_scale
         dma("SP", "Wuc")
         dummy()
         t_rows(1)
-        xs_mm("xd", 0)
-        xs_mm("xs", 0)
-        xs_mm("xd", 1)
-        xs_mm("xs", 1)
-        xs_cp("xd", 0)
-        xs_cp("xs", 0)
-        xs_cp("xd", 1)
-        xs_cp("xs", 1)
+        spread_r(0)
+        spread_r(1)
+        t_bias()
+        spread_z(2, 0)
+        spread_z(2, 1)
+        h_scaled(hq, 0.25)
+        copy_br(0)
+        copy_br(1)
         bn(0)
         bn(1)
         bn(2)
@@ -367,132 +412,127 @@ def tile_dgrucell_w_kernel(tc, x, h, Wg_words, Wg_scales, bg, Wu_words, Wu_scale
         stats1()
         pow_(1)
         gains_(1)
+        copy_bias()
         norm(1, 0, "V")
         norm(1, 2, "S")
-        t_ln(1, 0)
         norm(1, 1, "V")
         norm(1, 3, "S")
+        t_ln(1, 0)
         t_ln(1, 1)
         t_ln(1, 2)
         t_ln(1, 3)
         evac(1, 0, "V")
         evac(1, 1, "S")
-        regroup(1, 0, "V")
-        quant(1, 0)
+        regroup(0)
         evac(1, 2, "V")
         evac(1, 3, "S")
-        regroup(1, 1, "V")
+        quant(1, 0)
+        regroup(1)
+        regroup(2)
         quant(1, 1)
-        regroup(1, 2, "V")
         quant(1, 2)
-        regroup(1, 3, "V")
-        quant(1, 3)
-        spread_r(0)
-        spread_r(1)
-        mx("r0", 1, 512)
-        copy_br(0)
-        copy_br(1)
-        mx("r1", 1, 512)
-        r_add(0)
-        mx("r2", 1, 512)
-        r_tanh(0)
-        r_add(1)
-        r_mul(0)
-        spread_z(2, 0)
-        r_tanh(1)
-        t_rows(3)
-        r_add(2)
-        mx("r3", 1, 512)
+        regroup(3)
         copy_bz(2, 0)
+        copy_bz(2, 1)
+        xd(0)
+        quant(1, 3)
+        xd(1)
+        r_mx(0)
+        r_mx(1)
+        h_scaled(hh, 0.5)
+        r_add(0)
+        r_mx(2)
+        spread_z(1, 0)
+        spread_z(1, 1)
+        r_mx(3)
+        t_rows(3)
+        r_add(1)
+        r_tanh(0)
+        r_tanh(1)
+        r_mul(0)
+        r_add(2)
+        r_sq(0)
         r_mul(1)
         r_tanh(2)
-        r_bn(0)
-        spread_z(2, 1)
-        spread_z(1, 0)
         r_add(3)
-        spread_z(1, 1)
-        copy_bz(2, 1)
-        spread_u()
-        r_mul(2)
+        r_sq(1)
         r_tanh(3)
-        r_bn(1)
-        copy_bz(1, 0)
-        r_mul(3)
-        copy_bz(1, 1)
-        r_bn(2)
-        copy_bu()
-        mx("g00", 1, 512)
-        r_bn(3)
-        stats2()
-        mx("g01", 1, 512)
+        r_mul(2)
         gains_(3)
-        pow_(2)
+        r_sq(2)
+        r_mul(3)
+        r_sq(3)
+        mx("g00")
         z_t0p(0)
-        norm(2, 1, "G")
-        norm(2, 0, "S")
-        z_t0p(1)
-        norm(2, 3, "G")
-        t_ln(2, 1)
+        mx("g10")
+        stats2()
+        copy_bz(1, 0)
+        copy_bz(1, 1)
+        pow_(2)
+        norm(2, 0, "V")
         norm(2, 2, "S")
+        norm(2, 1, "V")
+        norm(2, 3, "S")
         t_ln(2, 0)
-        evac(2, 1, "S")
-        t_ln(2, 3)
-        evac(2, 0, "V")
+        t_ln(2, 1)
+        mx("g01")
         t_ln(2, 2)
-        mx("g10", 1, 512)
-        evac(2, 3, "S")
-        regroup(2, 1, "V")
-        evac(2, 2, "V")
-        mx("g11", 1, 512)
-        regroup(2, 0, "V")
+        t_ln(2, 3)
+        z_max(0)
         z_dp(0)
-        mx("g20", 1, 512)
-        regroup(2, 3, "V")
+        evac(2, 1, "S")
         z_ptanh(0)
-        regroup(2, 2, "V")
-        z_dp(1)
+        evac(2, 0, "V")
         z_abs(0)
-        quant(2, 1)
-        quant(2, 0)
-        z_ptanh(1)
-        z_pmul(0, "G")
-        quant(2, 3)
-        quant(2, 2)
-        z_t(1, 0)
-        z_abs(1)
-        mx("g21", 1, 512)
-        z_t(1, 1)
+        z_maxb(0)
+        evac(2, 2, "S")
+        regroup(0)
         z_ln(0)
-        z_padd(0, "G")
-        z_rt(0)
-        z_rt(1)
-        z_pmul(1, "G")
-        z_ar(0)
-        mx("u0", 2, 512)
-        z_ar(1)
-        z_ln(1)
-        z_padd(1, "G")
+        evac(2, 3, "S")
+        regroup(1)
+        quant(2, 0)
+        z_t0p(1)
+        quant(2, 1)
+        mx("g11")
+        z_pd(0)
+        regroup(2)
+        z_max(1)
+        z_dp(1)
+        z_soft(1)
+        dummy()
+        z_ptanh(1)
+        quant(2, 2)
+        regroup(3)
+        z_bh(0)
+        quant(2, 3)
+        z_maxb(1)
+        z_pre(0)
+        mx("g20")
+        z_pres(1)
+        mx("g21")
         z_arg(0)
-        mx("u1", 2, 256)
-        z_arg(1)
         z_qtanh(0)
-        u_add(0)
-        u_add(1)
-        mx("u2", 2, 256)
-        u_tanh(0)
-        u_add(2)
-        u_tanh(1)
-        u_du(0)
+        z_arg(1)
         z_qtanh(1)
+        z_pd(1)
+        z_na(0)
+        z_bh(1)
+        u_mx(0)
+        u_tanh(0)
+        u_mx(1)
+        u_back(0)
+        u_mx(2)
+        z_na(1)
         u_prod(0)
+        u_tanh(1)
+        u_back(1)
         u_tanh(2)
-        u_du(1)
-        u_du(2)
-        u_prod(1)
-        u_prod(2)
         u_out(0)
-        u_out(1)
+        u_back(2)
+        u_prod(1)
         store(0)
-        u_out(2)
+        u_prod(2)
+        u_out(1)
         store(1)
+        u_out(2)
         store(2)

@@ -48,6 +48,11 @@ def tile_dgrucell_w_kernel(tc, x, h, Wg_words, Wg_scales, bg, Wu_words, Wu_scale
         seld = keep.tile([P, 4], BF16, name="seld")
         st = keep.tile([P, 4, 6], F32, name="st")
         mv = keep.tile([P, 2], F32, name="mv")
+        sacc = keep.tile([P, 2, 4], F32, name="sacc")
+        part = keep.tile([P, 2], F32, name="part")
+        esq = keep.tile([P, 1], F32, name="esq")
+        msq = keep.tile([P, 1], F32, name="msq")
+        junk = keep.tile([P, 512], F32, name="junk")
         vpe = {1: keep.tile([P, 1], F32, name="vpe1"), 2: keep.tile([P, 1], F32, name="vpe2")}
         negm = {1: keep.tile([P, 1], F32, name="negm1"), 2: keep.tile([P, 1], F32, name="negm2")}
         rstd = {1: keep.tile([P, 1], F32, name="rstd1"), 2: keep.tile([P, 1], F32, name="rstd2")}
@@ -66,15 +71,10 @@ def tile_dgrucell_w_kernel(tc, x, h, Wg_words, Wg_scales, bg, Wu_words, Wu_scale
         bucol = keep.tile([P, 4, 2], F32, name="bucol")
         b_z = keep.tile([P, 2, D], F32, name="b_z")
         hq = keep.tile([P, D], F32, name="hq")
-        hh = keep.tile([P, D], F32, name="hh")
+        x4 = keep.tile([P, D], F32, name="x4")
         d4 = keep.tile([P, D], F32, name="d4")
         tb = keep.tile([P, K], F32, name="tb")
         b_r = keep.tile([P, K], BF16, name="b_r")
-        junk = keep.tile([P, 512], F32, name="junk")
-        sacc = keep.tile([P, 2, 4], F32, name="sacc")
-        sred = keep.tile([P, 2], F32, name="sred")
-        mean2 = keep.tile([P, 1], F32, name="mean2")
-        esq = keep.tile([P, 1], F32, name="esq")
         utt = keep.tile([P, 8, P], F32, name="utt")
         mxt = keep.tile([P, D], F32, name="mxt")
         bh = keep.tile([P, D], F32, name="bh")
@@ -134,7 +134,7 @@ def tile_dgrucell_w_kernel(tc, x, h, Wg_words, Wg_scales, bg, Wu_words, Wu_scale
                 w, c0, c1 = wcols[name[1:]]
                 eng[q].dma_start(out=wt[name[1:]][:].bitcast(I32), in_=wsrc[w][:, :, c0:c1])
 
-        def dummy():
+        def dummy(i):
             nc.scalar.activation(out=dummy_t[:], in_=mhalf[:], func=ACT.Tanh)
 
         def bn(j):
@@ -186,8 +186,12 @@ def tile_dgrucell_w_kernel(tc, x, h, Wg_words, Wg_scales, bg, Wu_words, Wu_scale
         def copy_bz(i, c):
             nc.scalar.copy(out=b_z[:, i - 1, sl(c)], in_=ps["bz", i, c][:])
 
-        def h_scaled(dst, factor):
-            nc.scalar.activation(out=dst[:], in_=xh[:, D:K], func=ACT.Copy, scale=factor)
+        def h_quarter():
+            nc.scalar.activation(out=hq[:], in_=xh[:, D:K], func=ACT.Copy, scale=0.25)
+
+        def xs(c):
+            nc.vector.scalar_tensor_tensor(out=x4[:, sl(c)], in0=xh[:, sl(c)], scalar=0.25, in1=hq[:, sl(c)],
+                                           op0=ALU.mult, op1=ALU.add)
 
         def xd(c):
             nc.vector.scalar_tensor_tensor(out=d4[:, sl(c)], in0=xh[:, sl(c)], scalar=0.25, in1=hq[:, sl(c)],
@@ -220,7 +224,7 @@ def tile_dgrucell_w_kernel(tc, x, h, Wg_words, Wg_scales, bg, Wu_words, Wu_scale
                     nc.scalar.activation(out=planar[:, g, t, :], in_=ps["pt", ln, g][:, t, :], func=ACT.Identity,
                                          bias=gb, scale=gw)
 
-        def regroup(g):
+        def regroup(ln, g):
             nc.vector.tensor_copy(out=grouped[:, g, :, :], in_=planar[:, g, :, :].rearrange("p t b -> p b t"))
 
         def quant(ln, g):
@@ -272,13 +276,19 @@ def tile_dgrucell_w_kernel(tc, x, h, Wg_words, Wg_scales, bg, Wu_words, Wu_scale
         def r_sq(j):
             nc.scalar.activation(out=junk[:], in_=c2[:, sl(j)], func=ACT.Square, accum_out=sacc[:, 1, j:j + 1])
 
-        def stats2():
-            nc.vector.tensor_reduce(out=sred[:], in_=sacc[:], op=ALU.add, axis=AX.X)
-            nc.vector.tensor_scalar(out=negm[2][:], in0=sred[:, 0:1], scalar1=-1.0 / K, scalar2=None, op0=ALU.mult)
-            nc.vector.tensor_scalar(out=mean2[:], in0=sred[:, 0:1], scalar1=1.0 / K, scalar2=None, op0=ALU.mult)
-            nc.vector.tensor_scalar(out=esq[:], in0=sred[:, 1:2], scalar1=1.0 / K, scalar2=4.0 * EPS,
+        def sums(i):
+            nc.vector.tensor_reduce(out=part[:, i:i + 1], in_=sacc[:, i, 0:3], op=ALU.add, axis=AX.X)
+
+        def mean2_():
+            nc.vector.tensor_scalar(out=negm[2][:], in0=sacc[:, 0, 3:4], scalar1=part[:, 0:1], scalar2=-1.0 / K,
+                                    op0=ALU.add, op1=ALU.mult)
+            nc.vector.tensor_scalar(out=esq[:], in0=part[:, 1:2], scalar1=1.0 / K, scalar2=4.0 * EPS,
                                     op0=ALU.mult, op1=ALU.add)
-            nc.vector.scalar_tensor_tensor(out=vpe[2][:], in0=mean2[:], scalar=negm[2][:, 0:1], in1=esq[:],
+            nc.vector.tensor_tensor(out=msq[:], in0=negm[2][:], in1=negm[2][:], op=ALU.mult)
+            nc.vector.tensor_tensor(out=esq[:], in0=esq[:], in1=msq[:], op=ALU.subtract)
+
+        def var2():
+            nc.vector.scalar_tensor_tensor(out=vpe[2][:], in0=sacc[:, 1, 3:4], scalar=1.0 / K, in1=esq[:],
                                            op0=ALU.mult, op1=ALU.add)
 
         def z_t0p(c):
@@ -299,6 +309,10 @@ def tile_dgrucell_w_kernel(tc, x, h, Wg_words, Wg_scales, bg, Wu_words, Wu_scale
         def z_abs(c):
             nc.scalar.activation(out=at[:, sl(c)], in_=tp[:, sl(c)], func=ACT.Abs)
 
+        def z_absv(c):
+            nc.vector.scalar_tensor_tensor(out=at[:, sl(c)], in0=tp[:, sl(c)], scalar=-1.0, in1=tp[:, sl(c)],
+                                           op0=ALU.mult, op1=ALU.max)
+
         def z_ln(c):
             nc.scalar.activation(out=at[:, sl(c)], in_=at[:, sl(c)], func=ACT.Ln, bias=0.5, scale=0.5)
 
@@ -317,12 +331,11 @@ def tile_dgrucell_w_kernel(tc, x, h, Wg_words, Wg_scales, bg, Wu_words, Wu_scale
         def z_arg(c):
             nc.vector.tensor_tensor(out=at[:, sl(c)], in0=ps["g2%d" % c][:], in1=at[:, sl(c)], op=ALU.add)
 
-        def z_pd(c):
-            nc.vector.scalar_tensor_tensor(out=bh[:, sl(c)], in0=tp[:, sl(c)], scalar=1.0, in1=d4[:, sl(c)],
-                                           op0=ALU.add, op1=ALU.mult)
+        def z_pd(c, e):
+            eng[e].tensor_tensor(out=bh[:, sl(c)], in0=tp[:, sl(c)], in1=d4[:, sl(c)], op=ALU.mult)
 
-        def z_bh(c):
-            nc.vector.tensor_tensor(out=bh[:, sl(c)], in0=bh[:, sl(c)], in1=hh[:, sl(c)], op=ALU.add)
+        def z_bh(c, e):
+            eng[e].tensor_tensor(out=bh[:, sl(c)], in0=bh[:, sl(c)], in1=x4[:, sl(c)], op=ALU.add)
 
         def z_qtanh(c):
             nc.scalar.activation(out=at[:, sl(c)], in_=at[:, sl(c)], func=ACT.Tanh, scale=0.5)
@@ -360,6 +373,18 @@ def tile_dgrucell_w_kernel(tc, x, h, Wg_words, Wg_scales, bg, Wu_words, Wu_scale
             nc.vector.scalar_tensor_tensor(out=ub[:, ucols(k)], in0=at[:, ucols(k)], scalar=1.0,
                                            in1=ps["ubk", k][:].rearrange("p m n -> p (m n)"), op0=ALU.add, op1=ALU.mult)
 
+        def u_du(k):
+            nc.vector.scalar_tensor_tensor(out=ub[:, ucols(k)], in0=ps["ubk", k][:].rearrange("p m n -> p (m n)"),
+                                           scalar=0.5, in1=bh[:, ucols(k)], op0=ALU.mult, op1=ALU.subtract)
+
+        def u_dprod(k):
+            nc.vector.scalar_tensor_tensor(out=ub[:, ucols(k)], in0=at[:, ucols(k)], scalar=1.0, in1=ub[:, ucols(k)],
+                                           op0=ALU.add, op1=ALU.mult)
+
+        def u_dout(k):
+            nc.vector.scalar_tensor_tensor(out=res[:, ucols(k)], in0=bh[:, ucols(k)], scalar=2.0, in1=ub[:, ucols(k)],
+                                           op0=ALU.mult, op1=ALU.add)
+
         def u_out(k):
             nc.vector.scalar_tensor_tensor(out=res[:, ucols(k)], in0=ub[:, ucols(k)], scalar=0.5, in1=bh[:, ucols(k)],
                                            op0=ALU.mult, op1=ALU.subtract)
@@ -367,170 +392,181 @@ def tile_dgrucell_w_kernel(tc, x, h, Wg_words, Wg_scales, bg, Wu_words, Wu_scale
         def store(k):
             nc.sync.dma_start(out=out[:, ucols(k)], in_=res[:, ucols(k)])
 
-        init()
         dma("SP", "x")
         dma("S", "h")
+        init()
         dma("SP", "lnw")
         dma("SP", "lnb")
         dma("SP", "mask")
         dma("SP", "bg")
         dma("SP", "bu")
         dma("SP", "Wrx")
-        for q in range(4):
-            dma("SP", "wrs%d" % q)
+        dma("SP", "wrs0")
+        dma("SP", "wrs1")
+        dma("SP", "wrs2")
+        dma("SP", "wrs3")
         dma("SP", "Wrha")
         dma("SP", "Wrhb")
         dma("SP", "ln2w")
         dma("SP", "ln2b")
-        for q in range(4):
-            dma("SP", "wzs%d" % q)
+        dma("SP", "wzs0")
+        dma("SP", "wzs1")
+        dma("SP", "wzs2")
+        dma("SP", "wzs3")
         dma("SP", "Wg0a")
         dma("SP", "Wg1a")
         dma("SP", "Wg0b")
         dma("SP", "Wg1b")
-        for q in range(4):
-            dma("SP", "wus%d" % q)
+        dma("SP", "wus0")
+        dma("SP", "wus1")
+        dma("SP", "wus2")
+        dma("SP", "wus3")
         dma("SP", "Wg2a")
         dma("SP", "Wg2b")
         dma("SP", "Wua")
         dma("SP", "Wub")
         dma("SP", "Wuc")
-        dummy()
-        t_rows(1)
-        spread_r(0)
-        spread_r(1)
-        t_bias()
-        spread_z(2, 0)
-        spread_z(2, 1)
-        h_scaled(hq, 0.25)
-        copy_br(0)
-        copy_br(1)
         bn(0)
         bn(1)
         bn(2)
         bn(3)
         stats1()
         pow_(1)
+        dummy(0)
+        h_quarter()
+        t_rows(1)
         gains_(1)
-        copy_bias()
+        xd(0)
         norm(1, 0, "V")
-        norm(1, 2, "S")
         norm(1, 1, "V")
+        spread_r(0)
+        copy_br(0)
+        spread_r(1)
+        copy_br(1)
+        t_bias()
+        copy_bias()
+        spread_z(2, 0)
+        copy_bz(2, 0)
+        spread_z(2, 1)
+        copy_bz(2, 1)
+        norm(1, 2, "S")
         norm(1, 3, "S")
         t_ln(1, 0)
-        t_ln(1, 1)
-        t_ln(1, 2)
-        t_ln(1, 3)
         evac(1, 0, "V")
+        regroup(1, 0)
+        t_ln(1, 1)
         evac(1, 1, "S")
-        regroup(0)
+        t_ln(1, 2)
         evac(1, 2, "V")
-        evac(1, 3, "S")
         quant(1, 0)
-        regroup(1)
-        regroup(2)
+        regroup(1, 1)
+        regroup(1, 2)
         quant(1, 1)
         quant(1, 2)
-        regroup(3)
-        copy_bz(2, 0)
-        copy_bz(2, 1)
-        xd(0)
+        t_ln(1, 3)
+        evac(1, 3, "S")
+        regroup(1, 3)
         quant(1, 3)
         xd(1)
-        r_mx(0)
-        r_mx(1)
-        h_scaled(hh, 0.5)
-        r_add(0)
-        r_mx(2)
         spread_z(1, 0)
+        copy_bz(1, 0)
         spread_z(1, 1)
-        r_mx(3)
-        t_rows(3)
-        r_add(1)
+        copy_bz(1, 1)
+        r_mx(0)
+        r_add(0)
+        xs(0)
         r_tanh(0)
-        r_tanh(1)
+        r_mx(1)
+        r_add(1)
         r_mul(0)
-        r_add(2)
+        r_tanh(1)
         r_sq(0)
+        r_mx(2)
+        r_add(2)
         r_mul(1)
         r_tanh(2)
-        r_add(3)
         r_sq(1)
-        r_tanh(3)
+        t_rows(3)
+        r_mx(3)
+        r_add(3)
         r_mul(2)
         gains_(3)
-        r_sq(2)
+        r_tanh(3)
         r_mul(3)
+        sums(0)
+        r_sq(2)
+        sums(1)
+        mean2_()
         r_sq(3)
         mx("g00")
         z_t0p(0)
-        mx("g10")
-        stats2()
-        copy_bz(1, 0)
-        copy_bz(1, 1)
+        var2()
         pow_(2)
-        norm(2, 0, "V")
+        xs(1)
         norm(2, 2, "S")
-        norm(2, 1, "V")
         norm(2, 3, "S")
-        t_ln(2, 0)
-        t_ln(2, 1)
-        mx("g01")
-        t_ln(2, 2)
-        t_ln(2, 3)
+        mx("g10")
         z_max(0)
         z_dp(0)
-        evac(2, 1, "S")
-        z_ptanh(0)
-        evac(2, 0, "V")
-        z_abs(0)
+        norm(2, 0, "V")
+        norm(2, 1, "V")
         z_maxb(0)
-        evac(2, 2, "S")
-        regroup(0)
-        z_ln(0)
-        evac(2, 3, "S")
-        regroup(1)
-        quant(2, 0)
+        z_ptanh(0)
+        z_pd(0, "G")
+        z_bh(0, "G")
+        mx("g01")
         z_t0p(1)
-        quant(2, 1)
+        t_ln(2, 0)
+        evac(2, 0, "V")
+        regroup(2, 0)
+        t_ln(2, 1)
+        evac(2, 1, "S")
+        z_abs(0)
         mx("g11")
-        z_pd(0)
-        regroup(2)
         z_max(1)
         z_dp(1)
-        z_soft(1)
-        dummy()
+        quant(2, 0)
+        regroup(2, 1)
+        t_ln(2, 2)
+        evac(2, 2, "S")
         z_ptanh(1)
+        z_pd(1, "G")
+        z_bh(1, "G")
+        z_ln(0)
+        t_ln(2, 3)
+        evac(2, 3, "V")
+        z_absv(1)
+        quant(2, 1)
+        regroup(2, 2)
+        regroup(2, 3)
         quant(2, 2)
-        regroup(3)
-        z_bh(0)
-        quant(2, 3)
         z_maxb(1)
+        quant(2, 3)
         z_pre(0)
+        z_ln(1)
+        z_pre(1)
+        dummy(1)
         mx("g20")
-        z_pres(1)
-        mx("g21")
         z_arg(0)
-        z_qtanh(0)
+        mx("g21")
         z_arg(1)
-        z_qtanh(1)
-        z_pd(1)
-        z_na(0)
-        z_bh(1)
         u_mx(0)
         u_tanh(0)
+        z_qtanh(0)
+        z_qtanh(1)
         u_mx(1)
-        u_back(0)
-        u_mx(2)
-        z_na(1)
-        u_prod(0)
         u_tanh(1)
-        u_back(1)
-        u_tanh(2)
-        u_out(0)
-        u_back(2)
-        u_prod(1)
+        u_back(0)
+        u_du(0)
+        u_dprod(0)
+        z_na(1)
+        u_dout(0)
         store(0)
+        u_mx(2)
+        u_tanh(2)
+        u_back(1)
+        u_prod(1)
+        u_back(2)
         u_prod(2)
         u_out(1)
         store(1)

@@ -32,10 +32,8 @@ def tile_dgrucell_w_kernel(tc, x, h, Wg_words, Wg_scales, bg, Wu_words, Wu_scale
 
         xh = keep.tile([P, K], BF16, name="xh")
         wsc = keep.tile([P, 6 * D], U8, name="wsc", align_bytes=64)
-        wcols = {"rx": ("g", 0, 1024), "rha": ("g", 1024, 1536), "rhb": ("g", 1536, 2048),
-                 "g0a": ("g", 2048, 2560), "g0b": ("g", 2560, 3072), "g1a": ("g", 3072, 3584), "g1b": ("g", 3584, 4096),
-                 "g2a": ("g", 4096, 4608), "g2b": ("g", 4608, 5120),
-                 "ua": ("u", 0, 512), "ub": ("u", 512, 768), "uc": ("u", 768, 1024)}
+        wcols = {"rx": ("g", 0, 1024), "rh": ("g", 1024, 2048), "g0": ("g", 2048, 3072), "g1": ("g", 3072, 4096),
+                 "g2": ("g", 4096, 5120), "ua": ("u", 0, 768), "ub": ("u", 768, 1024)}
         wt = {}
         for nm in wcols:
             wt[nm] = keep.tile([P, G, wcols[nm][2] - wcols[nm][1]], U32, name="w_" + nm, align_bytes=64)
@@ -80,6 +78,7 @@ def tile_dgrucell_w_kernel(tc, x, h, Wg_words, Wg_scales, bg, Wu_words, Wu_scale
         bh = keep.tile([P, D], F32, name="bh")
         tp = keep.tile([P, D], F32, name="tp")
         at = keep.tile([P, D], F32, name="at")
+        t0 = keep.tile([P, D], F32, name="t0")
         dp = keep.tile([P, D], F32, name="dp")
         ub = keep.tile([P, D], F32, name="ub")
         res = keep.tile([P, D], F32, name="res")
@@ -178,6 +177,11 @@ def tile_dgrucell_w_kernel(tc, x, h, Wg_words, Wg_scales, bg, Wu_words, Wu_scale
         def copy_br(i):
             nc.scalar.copy(out=b_r[:, 1024 * i:1024 * (i + 1)], in_=ps["br", i][:])
 
+        def warm(i, n):
+            t_ = bank(("warm", i), [P, 4, P], F32)
+            for k in range(n):
+                nc.tensor.matmul(t_[:, k % 4, :], lhsT=identf[:], rhs=identf[:], start=True, stop=True)
+
         def spread_z(i, c):
             t_ = bank(("bz", i, c), [P, 512], F32)
             nc.tensor.matmul(t_[:], lhsT=seld[:, 4 - 2 * i + c:5 - 2 * i + c].to_broadcast([P, P]), rhs=rows[2][:],
@@ -231,15 +235,15 @@ def tile_dgrucell_w_kernel(tc, x, h, Wg_words, Wg_scales, bg, Wu_words, Wu_scale
             nc.vector.quantize_mx(out=code[ln][:, g, :].bitcast(FP8X4), scales=plane[ln][:, g, :],
                                   in_=grouped[:, g, :, :].rearrange("p b t -> p (b t)"))
 
-        zcols = {"g00": "g0a", "g01": "g0b", "g10": "g1a", "g11": "g1b", "g20": "g2a", "g21": "g2b"}
-
         def mx(key):
-            nm = zcols[key]
-            s0 = wcols[nm][1]
+            nm = key[0:2]
+            c0 = 512 * int(key[2])
+            s0 = wcols[nm][1] + c0
             t_ = bank(key, [P, 512], F32)
             for g in range(G):
                 nc.tensor.matmul_mx(out=t_[:], lhsT=code[1][:, g, :].bitcast(FP8X4), lhsT_scale=plane[1][:, g, :],
-                                    rhs=wt[nm][:, g, :].bitcast(FP8X4), rhs_scale=wsc[4 * g:P, s0:s0 + 512],
+                                    rhs=wt[nm][:, g, c0:c0 + 512].bitcast(FP8X4),
+                                    rhs_scale=wsc[4 * g:P, s0:s0 + 512],
                                     start=(g == 0), stop=(g == G - 1))
 
         def mxt_pass(dst, ln, nm, c, g):
@@ -248,7 +252,7 @@ def tile_dgrucell_w_kernel(tc, x, h, Wg_words, Wg_scales, bg, Wu_words, Wu_scale
                                 rhs=code[ln][:, g, :].bitcast(FP8X4), rhs_scale=plane[ln][:, g, :],
                                 start=(g == 0), stop=(g == G - 1))
 
-        rcols = {0: ("rx", 0), 1: ("rx", 512), 2: ("rha", 0), 3: ("rhb", 0)}
+        rcols = {0: ("rx", 0), 1: ("rx", 512), 2: ("rh", 0), 3: ("rh", 512)}
 
         def r_pass(j, g):
             nm, c0 = rcols[j]
@@ -292,16 +296,16 @@ def tile_dgrucell_w_kernel(tc, x, h, Wg_words, Wg_scales, bg, Wu_words, Wu_scale
                                            op0=ALU.mult, op1=ALU.add)
 
         def z_t0p(c):
-            nc.vector.tensor_tensor(out=dp[:, sl(c)], in0=ps["g0%d" % c][:], in1=b_z[:, 1, sl(c)], op=ALU.add)
+            nc.vector.tensor_tensor(out=t0[:, sl(c)], in0=ps["g0%d" % c][:], in1=b_z[:, 1, sl(c)], op=ALU.add)
 
         def z_max(c):
-            nc.vector.tensor_tensor(out=mxt[:, sl(c)], in0=dp[:, sl(c)], in1=ps["g1%d" % c][:], op=ALU.max)
+            nc.vector.tensor_tensor(out=mxt[:, sl(c)], in0=t0[:, sl(c)], in1=ps["g1%d" % c][:], op=ALU.max)
 
         def z_dp(c):
-            nc.vector.tensor_tensor(out=dp[:, sl(c)], in0=dp[:, sl(c)], in1=ps["g1%d" % c][:], op=ALU.subtract)
+            nc.vector.tensor_tensor(out=dp[:, sl(c)], in0=t0[:, sl(c)], in1=ps["g1%d" % c][:], op=ALU.subtract)
 
-        def z_maxb(c):
-            nc.vector.tensor_tensor(out=mxt[:, sl(c)], in0=mxt[:, sl(c)], in1=b_z[:, 0, sl(c)], op=ALU.add)
+        def z_maxb(c, e):
+            eng[e].tensor_tensor(out=mxt[:, sl(c)], in0=mxt[:, sl(c)], in1=b_z[:, 0, sl(c)], op=ALU.add)
 
         def z_ptanh(c):
             nc.scalar.activation(out=tp[:, sl(c)], in_=dp[:, sl(c)], func=ACT.Tanh, scale=0.5)
@@ -344,7 +348,7 @@ def tile_dgrucell_w_kernel(tc, x, h, Wg_words, Wg_scales, bg, Wu_words, Wu_scale
             nc.vector.scalar_tensor_tensor(out=bh[:, sl(c)], in0=at[:, sl(c)], scalar=1.0, in1=bh[:, sl(c)],
                                            op0=ALU.subtract, op1=ALU.mult)
 
-        uparts = {0: ("ua", 0, 4), 1: ("ub", 4, 2), 2: ("uc", 6, 2)}
+        uparts = {0: ("ua", 0, 2), 1: ("ua", 2, 2), 2: ("ua", 4, 2), 3: ("ub", 6, 2)}
 
         def ucols(k):
             return slice(P * uparts[k][1], P * (uparts[k][1] + uparts[k][2]))
@@ -354,7 +358,7 @@ def tile_dgrucell_w_kernel(tc, x, h, Wg_words, Wg_scales, bg, Wu_words, Wu_scale
             t_ = bank(("u", k), [P, n, P], F32)
             for m in range(n):
                 for g in range(G):
-                    mxt_pass(t_[:, m, :], 2, nm, P * m, g)
+                    mxt_pass(t_[:, m, :], 2, nm, P * (i0 + m) - wcols[nm][1], g)
 
         def u_tanh(k):
             nm, i0, n = uparts[k]
@@ -405,27 +409,22 @@ def tile_dgrucell_w_kernel(tc, x, h, Wg_words, Wg_scales, bg, Wu_words, Wu_scale
         dma("SP", "wrs1")
         dma("SP", "wrs2")
         dma("SP", "wrs3")
-        dma("SP", "Wrha")
-        dma("SP", "Wrhb")
+        dma("SP", "Wrh")
         dma("SP", "ln2w")
         dma("SP", "ln2b")
         dma("SP", "wzs0")
         dma("SP", "wzs1")
         dma("SP", "wzs2")
         dma("SP", "wzs3")
-        dma("SP", "Wg0a")
-        dma("SP", "Wg1a")
-        dma("SP", "Wg0b")
-        dma("SP", "Wg1b")
+        dma("SP", "Wg0")
+        dma("SP", "Wg1")
         dma("SP", "wus0")
         dma("SP", "wus1")
         dma("SP", "wus2")
         dma("SP", "wus3")
-        dma("SP", "Wg2a")
-        dma("SP", "Wg2b")
+        dma("SP", "Wg2")
         dma("SP", "Wua")
         dma("SP", "Wub")
-        dma("SP", "Wuc")
         bn(0)
         bn(1)
         bn(2)
@@ -443,19 +442,17 @@ def tile_dgrucell_w_kernel(tc, x, h, Wg_words, Wg_scales, bg, Wu_words, Wu_scale
         copy_br(0)
         spread_r(1)
         copy_br(1)
+        norm(1, 2, "S")
+        norm(1, 3, "S")
         t_bias()
         copy_bias()
         spread_z(2, 0)
-        copy_bz(2, 0)
-        spread_z(2, 1)
-        copy_bz(2, 1)
-        norm(1, 2, "S")
-        norm(1, 3, "S")
         t_ln(1, 0)
         evac(1, 0, "V")
         regroup(1, 0)
         t_ln(1, 1)
         evac(1, 1, "S")
+        copy_bz(2, 0)
         t_ln(1, 2)
         evac(1, 2, "V")
         quant(1, 0)
@@ -468,10 +465,10 @@ def tile_dgrucell_w_kernel(tc, x, h, Wg_words, Wg_scales, bg, Wu_words, Wu_scale
         regroup(1, 3)
         quant(1, 3)
         xd(1)
+        spread_z(2, 1)
+        copy_bz(2, 1)
         spread_z(1, 0)
         copy_bz(1, 0)
-        spread_z(1, 1)
-        copy_bz(1, 1)
         r_mx(0)
         r_add(0)
         xs(0)
@@ -481,6 +478,7 @@ def tile_dgrucell_w_kernel(tc, x, h, Wg_words, Wg_scales, bg, Wu_words, Wu_scale
         r_mul(0)
         r_tanh(1)
         r_sq(0)
+        spread_z(1, 1)
         r_mx(2)
         r_add(2)
         r_mul(1)
@@ -489,8 +487,9 @@ def tile_dgrucell_w_kernel(tc, x, h, Wg_words, Wg_scales, bg, Wu_words, Wu_scale
         t_rows(3)
         r_mx(3)
         r_add(3)
-        r_mul(2)
         gains_(3)
+        r_mul(2)
+        xs(1)
         r_tanh(3)
         r_mul(3)
         sums(0)
@@ -498,22 +497,15 @@ def tile_dgrucell_w_kernel(tc, x, h, Wg_words, Wg_scales, bg, Wu_words, Wu_scale
         sums(1)
         mean2_()
         r_sq(3)
-        mx("g00")
-        z_t0p(0)
         var2()
         pow_(2)
-        xs(1)
-        norm(2, 2, "S")
-        norm(2, 3, "S")
-        mx("g10")
-        z_max(0)
-        z_dp(0)
         norm(2, 0, "V")
         norm(2, 1, "V")
-        z_maxb(0)
-        z_ptanh(0)
-        z_pd(0, "G")
-        z_bh(0, "G")
+        copy_bz(1, 1)
+        norm(2, 2, "S")
+        norm(2, 3, "S")
+        mx("g00")
+        z_t0p(0)
         mx("g01")
         z_t0p(1)
         t_ln(2, 0)
@@ -521,54 +513,67 @@ def tile_dgrucell_w_kernel(tc, x, h, Wg_words, Wg_scales, bg, Wu_words, Wu_scale
         regroup(2, 0)
         t_ln(2, 1)
         evac(2, 1, "S")
-        z_abs(0)
-        mx("g11")
-        z_max(1)
-        z_dp(1)
-        quant(2, 0)
         regroup(2, 1)
+        quant(2, 0)
         t_ln(2, 2)
         evac(2, 2, "S")
+        regroup(2, 2)
+        quant(2, 1)
+        t_ln(2, 3)
+        evac(2, 3, "S")
+        mx("g10")
+        z_dp(0)
+        z_ptanh(0)
+        z_pd(0, "G")
+        z_bh(0, "G")
+        z_abs(0)
+        mx("g11")
+        z_dp(1)
+        regroup(2, 3)
+        quant(2, 2)
+        quant(2, 3)
+        z_max(0)
+        z_max(1)
         z_ptanh(1)
         z_pd(1, "G")
         z_bh(1, "G")
-        z_ln(0)
-        t_ln(2, 3)
-        evac(2, 3, "V")
         z_absv(1)
-        quant(2, 1)
-        regroup(2, 2)
-        regroup(2, 3)
-        quant(2, 2)
-        z_maxb(1)
-        quant(2, 3)
+        z_maxb(0, "V")
+        z_maxb(1, "V")
+        z_ln(0)
         z_pre(0)
         z_ln(1)
         z_pre(1)
         dummy(1)
         mx("g20")
         z_arg(0)
+        z_qtanh(0)
         mx("g21")
         z_arg(1)
+        z_na(0)
+        z_qtanh(1)
+        z_na(1)
         u_mx(0)
         u_tanh(0)
-        z_qtanh(0)
-        z_qtanh(1)
         u_mx(1)
         u_tanh(1)
-        u_back(0)
-        u_du(0)
-        u_dprod(0)
-        z_na(1)
-        u_dout(0)
-        store(0)
         u_mx(2)
         u_tanh(2)
+        u_mx(3)
+        u_tanh(3)
+        u_back(0)
+        u_prod(0)
         u_back(1)
         u_prod(1)
         u_back(2)
         u_prod(2)
+        u_out(0)
+        store(0)
         u_out(1)
         store(1)
+        u_back(3)
+        u_prod(3)
         u_out(2)
         store(2)
+        u_out(3)
+        store(3)

from contextlib import ExitStack

import concourse.mybir as mybir
from concourse.masks import make_identity

F32 = mybir.dt.float32
BF16 = mybir.dt.bfloat16
I32 = mybir.dt.int32
U32 = mybir.dt.uint32
U8 = mybir.dt.uint8
FP8X4 = mybir.dt.float8_e4m3fn_x4
ALU = mybir.AluOpType
ACT = mybir.ActivationFunctionType
AX = mybir.AxisListType

P = 128
D = 1024
K = 2 * D
G = K // 512
EPS = 1e-5
FLOPS = 2 * 128 * 2048 * 6144


def tile_dgrucell_w_kernel(tc, x, h, Wg_words, Wg_scales, bg, Wu_words, Wu_scales, bu,
                                         ln_w, ln_b, ln2_w, ln2_b, dropout_mask, out):
    nc = tc.nc
    with ExitStack() as ctx:
        keep = ctx.enter_context(tc.tile_pool(name="keep", bufs=1))
        psum = ctx.enter_context(tc.psum_pool(name="psum", bufs=1))
        ctx.enter_context(tc.manual_schedule())
        eng = {"V": nc.vector, "S": nc.scalar, "G": nc.gpsimd, "SP": nc.sync}

        xh = keep.tile([P, K], BF16, name="xh")
        wsc = keep.tile([P, 6 * D], U8, name="wsc", align_bytes=64)
        wcols = {"rx": ("g", 0, 1024), "rh": ("g", 1024, 2048), "g0": ("g", 2048, 3072), "g1": ("g", 3072, 4096),
                 "g2": ("g", 4096, 5120), "ua": ("u", 0, 768), "ub": ("u", 768, 1024)}
        wt = {}
        for nm in wcols:
            wt[nm] = keep.tile([P, G, wcols[nm][2] - wcols[nm][1]], U32, name="w_" + nm, align_bytes=64)
        identf = keep.tile([P, P], F32, name="identf")
        identb = keep.tile([P, P], BF16, name="identb")
        rows = {1: keep.tile([P, 512], BF16, name="rows1"), 2: keep.tile([P, 512], BF16, name="rows2"),
                3: keep.tile([P, 512], BF16, name="rows3")}
        dummy_t = keep.tile([P, 1], F32, name="dummy_t")
        mhalf = keep.tile([P, 1], F32, name="mhalf")
        seld = keep.tile([P, 4], BF16, name="seld")
        st = keep.tile([P, 4, 6], F32, name="st")
        mv = keep.tile([P, 2], F32, name="mv")
        sacc = keep.tile([P, 2, 4], F32, name="sacc")
        part = keep.tile([P, 2], F32, name="part")
        esq = keep.tile([P, 1], F32, name="esq")
        msq = keep.tile([P, 1], F32, name="msq")
        junk = keep.tile([P, 512], F32, name="junk")
        vpe = {1: keep.tile([P, 1], F32, name="vpe1"), 2: keep.tile([P, 1], F32, name="vpe2")}
        negm = {1: keep.tile([P, 1], F32, name="negm1"), 2: keep.tile([P, 1], F32, name="negm2")}
        rstd = {1: keep.tile([P, 1], F32, name="rstd1"), 2: keep.tile([P, 1], F32, name="rstd2")}
        nmr = {1: keep.tile([P, 1], F32, name="nmr1"), 2: keep.tile([P, 1], F32, name="nmr2")}
        vt = {1: keep.tile([P, 4, 12], F32, name="vt1"), 3: keep.tile([P, 4, 8], F32, name="vt3")}
        gains = {1: keep.tile([P, 4, 2, 4], F32, name="gains1"), 2: keep.tile([P, 4, 2, 4], F32, name="gains2")}
        gains[3] = gains[2]
        nrm = keep.tile([P, K], F32, name="nrm")
        c2 = keep.tile([P, K], F32, name="c2")
        planar = keep.tile([P, G, 4, P], BF16, name="planar")
        grouped = keep.tile([P, G, P, 4], BF16, name="grouped", align_bytes=64)
        code = {1: keep.tile([P, G, P], U32, name="code1", align_bytes=64),
                2: keep.tile([P, G, P], U32, name="code2", align_bytes=64)}
        plane = {1: keep.tile([P, G, P], U8, name="plane1", align_bytes=64),
                 2: keep.tile([P, G, P], U8, name="plane2", align_bytes=64)}
        bucol = keep.tile([P, 4, 2], F32, name="bucol")
        b_z = keep.tile([P, 2, D], F32, name="b_z")
        hq = keep.tile([P, D], F32, name="hq")
        x4 = keep.tile([P, D], F32, name="x4")
        d4 = keep.tile([P, D], F32, name="d4")
        tb = keep.tile([P, K], F32, name="tb")
        b_r = keep.tile([P, K], BF16, name="b_r")
        utt = keep.tile([P, 8, P], F32, name="utt")
        mxt = keep.tile([P, D], F32, name="mxt")
        bh = keep.tile([P, D], F32, name="bh")
        tp = keep.tile([P, D], F32, name="tp")
        at = keep.tile([P, D], F32, name="at")
        t0 = keep.tile([P, D], F32, name="t0")
        dp = keep.tile([P, D], F32, name="dp")
        ub = keep.tile([P, D], F32, name="ub")
        res = keep.tile([P, D], F32, name="res")

        ps = {}
        count = [0]

        def bank(key, shape, dtype):
            n = count[0] % 8
            count[0] = count[0] + 1
            ps[key] = psum.tile(shape, dtype, name="bank%d" % n, tag="bank%d" % n)
            return ps[key]

        def sl(c):
            return slice(512 * c, 512 * (c + 1))

        wsc32 = wsc[:].bitcast(I32)
        wsrc = {"g": Wg_words.rearrange("g p n t -> g p (n t)").bitcast(I32).rearrange("g p n -> p g n"),
                "u": Wu_words.rearrange("g p n t -> g p (n t)").bitcast(I32).rearrange("g p n -> p g n")}
        small = {"lnw": (1, 0, 4, ln_w), "lnb": (1, 4, 8, ln_b), "mask": (1, 8, 12, dropout_mask),
                 "ln2w": (3, 0, 4, ln2_w), "ln2b": (3, 4, 8, ln2_b), "bg": (2, 0, 10, bg), "bu": (2, 12, 14, bu)}

        def init():
            make_identity(nc, identb[:])
            nc.vector.memset(rows[1][:], 0.0)
            nc.vector.memset(rows[2][:], 0.0)
            nc.vector.memset(mhalf[:], -0.5)
            nc.vector.memset(rows[3][:], 0.0)
            nc.gpsimd.memset(wsc32, 0)
            make_identity(nc, identf[:])
            nc.vector.tensor_tensor(out=seld[:, 0:2], in0=identb[:, 4:6], in1=identb[:, 6:8], op=ALU.subtract)
            nc.vector.tensor_tensor(out=seld[:, 2:4], in0=identb[:, 6:8], in1=identb[:, 8:10], op=ALU.subtract)

        def dma(q, name):
            if name == "x":
                eng[q].dma_start(out=xh[:, 0:D], in_=x)
            elif name == "h":
                eng[q].dma_start(out=xh[:, D:K], in_=h)
            elif name in small:
                i, r0, r1, src = small[name]
                eng[q].dma_start(out=rows[i][r0:r1, :], in_=src.rearrange("(r c) -> r c", c=512))
            elif name[0:3] in ("wrs", "wzs"):
                qd = int(name[3])
                a, b = (0, 512) if name[1] == "r" else (512, 1280)
                eng[q].dma_start(out=wsc32[32 * qd:32 * qd + 16, a:b],
                                 in_=Wg_scales.bitcast(I32)[:, 4 * qd:4 * qd + 4, a:b])
            elif name[0:3] == "wus":
                qd = int(name[3])
                eng[q].dma_start(out=wsc32[32 * qd:32 * qd + 16, 1280:1536],
                                 in_=Wu_scales.bitcast(I32)[:, 4 * qd:4 * qd + 4, :])
            else:
                w, c0, c1 = wcols[name[1:]]
                eng[q].dma_start(out=wt[name[1:]][:].bitcast(I32), in_=wsrc[w][:, :, c0:c1])

        def dummy(i):
            nc.scalar.activation(out=dummy_t[:], in_=mhalf[:], func=ACT.Tanh)

        def bn(j):
            nc.vector.bn_stats(out=st[:, j, :], in_=xh[:, sl(j)])

        def stats1():
            nc.vector.bn_aggr(out=mv[:], in_=st[:].rearrange("p a b -> p (a b)"))
            nc.vector.tensor_scalar(out=vpe[1][:], in0=mv[:, 1:2], scalar1=EPS, scalar2=None, op0=ALU.add)
            nc.vector.tensor_scalar(out=negm[1][:], in0=mv[:, 0:1], scalar1=-1.0, scalar2=None, op0=ALU.mult)

        def pow_(ln):
            nc.gpsimd.tensor_tensor(out=rstd[ln][:], in0=vpe[ln][:], in1=mhalf[:], op=ALU.pow)
            nc.gpsimd.tensor_tensor(out=nmr[ln][:], in0=rstd[ln][:], in1=negm[ln][:], op=ALU.mult)

        def t_rows(i):
            t_ = bank(("vp", i), [P, 4, P], BF16)
            for t in range(4):
                nc.tensor.transpose(t_[:, t, :], rows[i][:, t:512:4], identb[:])

        def gains_(i):
            n = 12 if i == 1 else 8
            nc.vector.tensor_copy(out=vt[i][:], in_=ps["vp", i][:, :, 0:n])
            nc.vector.tensor_tensor(out=gains[i][:], in0=vt[i][:, :, 0:8].rearrange("p t (v g) -> p t v g", v=2),
                                    in1=vt[1][:, :, 8:12].unsqueeze(2).to_broadcast([P, 4, 2, 4]), op=ALU.mult)

        def t_bias():
            t_ = bank("bc", [P, 4, P], BF16)
            for m in range(4):
                nc.tensor.transpose(t_[:, m, :], rows[2][:, P * m:P * (m + 1)], identb[:])

        def copy_bias():
            nc.vector.tensor_copy(out=bucol[:], in_=ps["bc"][:, :, 12:14])

        def spread_r(i):
            t_ = bank(("br", i), [P, 1024], BF16)
            for c in range(2):
                r0 = 2 * i + c
                nc.tensor.matmul(t_[:, sl(c)], lhsT=identb[:, r0:r0 + 1].to_broadcast([P, P]), rhs=rows[2][:],
                                 start=True, stop=True)

        def copy_br(i):
            nc.scalar.copy(out=b_r[:, 1024 * i:1024 * (i + 1)], in_=ps["br", i][:])

        def warm(i, n):
            t_ = bank(("warm", i), [P, 4, P], F32)
            for k in range(n):
                nc.tensor.matmul(t_[:, k % 4, :], lhsT=identf[:], rhs=identf[:], start=True, stop=True)

        def spread_z(i, c):
            t_ = bank(("bz", i, c), [P, 512], F32)
            nc.tensor.matmul(t_[:], lhsT=seld[:, 4 - 2 * i + c:5 - 2 * i + c].to_broadcast([P, P]), rhs=rows[2][:],
                             start=True, stop=True)

        def copy_bz(i, c):
            nc.scalar.copy(out=b_z[:, i - 1, sl(c)], in_=ps["bz", i, c][:])

        def h_quarter():
            nc.scalar.activation(out=hq[:], in_=xh[:, D:K], func=ACT.Copy, scale=0.25)

        def xs(c):
            nc.vector.scalar_tensor_tensor(out=x4[:, sl(c)], in0=xh[:, sl(c)], scalar=0.25, in1=hq[:, sl(c)],
                                           op0=ALU.mult, op1=ALU.add)

        def xd(c):
            nc.vector.scalar_tensor_tensor(out=d4[:, sl(c)], in0=xh[:, sl(c)], scalar=0.25, in1=hq[:, sl(c)],
                                           op0=ALU.mult, op1=ALU.subtract)

        def norm(ln, g, e):
            src = xh if ln == 1 else c2
            dst = nrm if ln == 1 else c2
            if e == "S":
                nc.scalar.activation(out=dst[:, sl(g)], in_=src[:, sl(g)], func=ACT.Identity,
                                     bias=nmr[ln][:, 0:1], scale=rstd[ln][:, 0:1])
            else:
                nc.vector.tensor_scalar(out=dst[:, sl(g)], in0=src[:, sl(g)], scalar1=negm[ln][:, 0:1],
                                        scalar2=rstd[ln][:, 0:1], op0=ALU.add, op1=ALU.mult)

        def t_ln(ln, g):
            src = nrm if ln == 1 else c2
            t_ = bank(("pt", ln, g), [P, 4, P], F32)
            for t in range(4):
                nc.tensor.transpose(t_[:, t, :], src[:, 512 * g + t:512 * (g + 1):4], identf[:])

        def evac(ln, g, e):
            for t in range(4):
                gw = gains[ln][:, t, 0, g:g + 1]
                gb = gains[ln][:, t, 1, g:g + 1]
                if e == "V":
                    nc.vector.tensor_scalar(out=planar[:, g, t, :], in0=ps["pt", ln, g][:, t, :], scalar1=gw,
                                            scalar2=gb, op0=ALU.mult, op1=ALU.add)
                else:
                    nc.scalar.activation(out=planar[:, g, t, :], in_=ps["pt", ln, g][:, t, :], func=ACT.Identity,
                                         bias=gb, scale=gw)

        def regroup(ln, g):
            nc.vector.tensor_copy(out=grouped[:, g, :, :], in_=planar[:, g, :, :].rearrange("p t b -> p b t"))

        def quant(ln, g):
            nc.vector.quantize_mx(out=code[ln][:, g, :].bitcast(FP8X4), scales=plane[ln][:, g, :],
                                  in_=grouped[:, g, :, :].rearrange("p b t -> p (b t)"))

        def mx(key):
            nm = key[0:2]
            c0 = 512 * int(key[2])
            s0 = wcols[nm][1] + c0
            t_ = bank(key, [P, 512], F32)
            for g in range(G):
                nc.tensor.matmul_mx(out=t_[:], lhsT=code[1][:, g, :].bitcast(FP8X4), lhsT_scale=plane[1][:, g, :],
                                    rhs=wt[nm][:, g, c0:c0 + 512].bitcast(FP8X4),
                                    rhs_scale=wsc[4 * g:P, s0:s0 + 512],
                                    start=(g == 0), stop=(g == G - 1))

        def mxt_pass(dst, ln, nm, c, g):
            s0 = wcols[nm][1] + c + (5 * D if wcols[nm][0] == "u" else 0)
            nc.tensor.matmul_mx(out=dst, lhsT=wt[nm][:, g, c:c + P].bitcast(FP8X4), lhsT_scale=wsc[4 * g:P, s0:s0 + P],
                                rhs=code[ln][:, g, :].bitcast(FP8X4), rhs_scale=plane[ln][:, g, :],
                                start=(g == 0), stop=(g == G - 1))

        rcols = {0: ("rx", 0), 1: ("rx", 512), 2: ("rh", 0), 3: ("rh", 512)}

        def r_pass(j, g):
            nm, c0 = rcols[j]
            s0 = wcols[nm][1] + c0
            if g == 0:
                bank(("r", j), [P, 512], F32)
            nc.tensor.matmul_mx(out=ps["r", j][:], lhsT=code[1][:, g, :].bitcast(FP8X4), lhsT_scale=plane[1][:, g, :],
                                rhs=wt[nm][:, g, c0:c0 + 512].bitcast(FP8X4), rhs_scale=wsc[4 * g:P, s0:s0 + 512],
                                start=(g == 0), stop=(g == G - 1))

        def r_mx(j):
            for g in range(G):
                r_pass(j, g)

        def r_add(j):
            nc.vector.tensor_tensor(out=tb[:, sl(j)], in0=ps["r", j][:], in1=b_r[:, sl(j)], op=ALU.add)

        def r_tanh(j):
            nc.scalar.activation(out=tb[:, sl(j)], in_=tb[:, sl(j)], func=ACT.Tanh, scale=0.5)

        def r_mul(j):
            nc.vector.scalar_tensor_tensor(out=c2[:, sl(j)], in0=tb[:, sl(j)], scalar=1.0, in1=xh[:, sl(j)],
                                           op0=ALU.add, op1=ALU.mult, accum_out=sacc[:, 0, j:j + 1])

        def r_sq(j):
            nc.scalar.activation(out=junk[:], in_=c2[:, sl(j)], func=ACT.Square, accum_out=sacc[:, 1, j:j + 1])

        def sums(i):
            nc.vector.tensor_reduce(out=part[:, i:i + 1], in_=sacc[:, i, 0:3], op=ALU.add, axis=AX.X)

        def mean2_():
            nc.vector.tensor_scalar(out=negm[2][:], in0=sacc[:, 0, 3:4], scalar1=part[:, 0:1], scalar2=-1.0 / K,
                                    op0=ALU.add, op1=ALU.mult)
            nc.vector.tensor_scalar(out=esq[:], in0=part[:, 1:2], scalar1=1.0 / K, scalar2=4.0 * EPS,
                                    op0=ALU.mult, op1=ALU.add)
            nc.vector.tensor_tensor(out=msq[:], in0=negm[2][:], in1=negm[2][:], op=ALU.mult)
            nc.vector.tensor_tensor(out=esq[:], in0=esq[:], in1=msq[:], op=ALU.subtract)

        def var2():
            nc.vector.scalar_tensor_tensor(out=vpe[2][:], in0=sacc[:, 1, 3:4], scalar=1.0 / K, in1=esq[:],
                                           op0=ALU.mult, op1=ALU.add)

        def z_t0p(c):
            nc.vector.tensor_tensor(out=t0[:, sl(c)], in0=ps["g0%d" % c][:], in1=b_z[:, 1, sl(c)], op=ALU.add)

        def z_max(c):
            nc.vector.tensor_tensor(out=mxt[:, sl(c)], in0=t0[:, sl(c)], in1=ps["g1%d" % c][:], op=ALU.max)

        def z_dp(c):
            nc.vector.tensor_tensor(out=dp[:, sl(c)], in0=t0[:, sl(c)], in1=ps["g1%d" % c][:], op=ALU.subtract)

        def z_maxb(c, e):
            eng[e].tensor_tensor(out=mxt[:, sl(c)], in0=mxt[:, sl(c)], in1=b_z[:, 0, sl(c)], op=ALU.add)

        def z_ptanh(c):
            nc.scalar.activation(out=tp[:, sl(c)], in_=dp[:, sl(c)], func=ACT.Tanh, scale=0.5)

        def z_abs(c):
            nc.scalar.activation(out=at[:, sl(c)], in_=tp[:, sl(c)], func=ACT.Abs)

        def z_absv(c):
            nc.vector.scalar_tensor_tensor(out=at[:, sl(c)], in0=tp[:, sl(c)], scalar=-1.0, in1=tp[:, sl(c)],
                                           op0=ALU.mult, op1=ALU.max)

        def z_ln(c):
            nc.scalar.activation(out=at[:, sl(c)], in_=at[:, sl(c)], func=ACT.Ln, bias=0.5, scale=0.5)

        def z_soft(c):
            nc.scalar.activation(out=at[:, sl(c)], in_=dp[:, sl(c)], func=ACT.Abs)
            nc.scalar.activation(out=at[:, sl(c)], in_=at[:, sl(c)], func=ACT.Exp, scale=-1.0)
            nc.scalar.activation(out=at[:, sl(c)], in_=at[:, sl(c)], func=ACT.Ln, bias=1.0, scale=1.0)

        def z_pres(c):
            nc.vector.scalar_tensor_tensor(out=at[:, sl(c)], in0=at[:, sl(c)], scalar=-1.0, in1=mxt[:, sl(c)],
                                           op0=ALU.mult, op1=ALU.subtract)

        def z_pre(c):
            nc.vector.tensor_tensor(out=at[:, sl(c)], in0=at[:, sl(c)], in1=mxt[:, sl(c)], op=ALU.subtract)

        def z_arg(c):
            nc.vector.tensor_tensor(out=at[:, sl(c)], in0=ps["g2%d" % c][:], in1=at[:, sl(c)], op=ALU.add)

        def z_pd(c, e):
            eng[e].tensor_tensor(out=bh[:, sl(c)], in0=tp[:, sl(c)], in1=d4[:, sl(c)], op=ALU.mult)

        def z_bh(c, e):
            eng[e].tensor_tensor(out=bh[:, sl(c)], in0=bh[:, sl(c)], in1=x4[:, sl(c)], op=ALU.add)

        def z_qtanh(c):
            nc.scalar.activation(out=at[:, sl(c)], in_=at[:, sl(c)], func=ACT.Tanh, scale=0.5)

        def z_na(c):
            nc.vector.scalar_tensor_tensor(out=bh[:, sl(c)], in0=at[:, sl(c)], scalar=1.0, in1=bh[:, sl(c)],
                                           op0=ALU.subtract, op1=ALU.mult)

        uparts = {0: ("ua", 0, 2), 1: ("ua", 2, 2), 2: ("ua", 4, 2), 3: ("ub", 6, 2)}

        def ucols(k):
            return slice(P * uparts[k][1], P * (uparts[k][1] + uparts[k][2]))

        def u_mx(k):
            nm, i0, n = uparts[k]
            t_ = bank(("u", k), [P, n, P], F32)
            for m in range(n):
                for g in range(G):
                    mxt_pass(t_[:, m, :], 2, nm, P * (i0 + m) - wcols[nm][1], g)

        def u_tanh(k):
            nm, i0, n = uparts[k]
            for m in range(n):
                i = i0 + m
                nc.scalar.activation(out=utt[:, i, :], in_=ps["u", k][:, m, :], func=ACT.Tanh,
                                     bias=bucol[:, i % 4, i // 4:i // 4 + 1], scale=1.0)

        def u_back(k):
            nm, i0, n = uparts[k]
            t_ = bank(("ubk", k), [P, n, P], F32)
            for m in range(n):
                nc.tensor.transpose(t_[:, m, :], utt[:, i0 + m, :], identf[:])

        def u_prod(k):
            nc.vector.scalar_tensor_tensor(out=ub[:, ucols(k)], in0=at[:, ucols(k)], scalar=1.0,
                                           in1=ps["ubk", k][:].rearrange("p m n -> p (m n)"), op0=ALU.add, op1=ALU.mult)

        def u_du(k):
            nc.vector.scalar_tensor_tensor(out=ub[:, ucols(k)], in0=ps["ubk", k][:].rearrange("p m n -> p (m n)"),
                                           scalar=0.5, in1=bh[:, ucols(k)], op0=ALU.mult, op1=ALU.subtract)

        def u_dprod(k):
            nc.vector.scalar_tensor_tensor(out=ub[:, ucols(k)], in0=at[:, ucols(k)], scalar=1.0, in1=ub[:, ucols(k)],
                                           op0=ALU.add, op1=ALU.mult)

        def u_dout(k):
            nc.vector.scalar_tensor_tensor(out=res[:, ucols(k)], in0=bh[:, ucols(k)], scalar=2.0, in1=ub[:, ucols(k)],
                                           op0=ALU.mult, op1=ALU.add)

        def u_out(k):
            nc.vector.scalar_tensor_tensor(out=res[:, ucols(k)], in0=ub[:, ucols(k)], scalar=0.5, in1=bh[:, ucols(k)],
                                           op0=ALU.mult, op1=ALU.subtract)

        def store(k):
            nc.sync.dma_start(out=out[:, ucols(k)], in_=res[:, ucols(k)])

        dma("SP", "x")
        dma("S", "h")
        init()
        dma("SP", "lnw")
        dma("SP", "lnb")
        dma("SP", "mask")
        dma("SP", "bg")
        dma("SP", "bu")
        dma("SP", "Wrx")
        dma("SP", "wrs0")
        dma("SP", "wrs1")
        dma("SP", "wrs2")
        dma("SP", "wrs3")
        dma("SP", "Wrh")
        dma("SP", "ln2w")
        dma("SP", "ln2b")
        dma("SP", "wzs0")
        dma("SP", "wzs1")
        dma("SP", "wzs2")
        dma("SP", "wzs3")
        dma("SP", "Wg0")
        dma("SP", "Wg1")
        dma("SP", "wus0")
        dma("SP", "wus1")
        dma("SP", "wus2")
        dma("SP", "wus3")
        dma("SP", "Wg2")
        dma("SP", "Wua")
        dma("SP", "Wub")
        bn(0)
        bn(1)
        bn(2)
        bn(3)
        stats1()
        pow_(1)
        dummy(0)
        h_quarter()
        t_rows(1)
        gains_(1)
        xd(0)
        norm(1, 0, "V")
        norm(1, 1, "V")
        spread_r(0)
        copy_br(0)
        spread_r(1)
        copy_br(1)
        norm(1, 2, "S")
        norm(1, 3, "S")
        t_bias()
        copy_bias()
        spread_z(2, 0)
        t_ln(1, 0)
        evac(1, 0, "V")
        regroup(1, 0)
        t_ln(1, 1)
        evac(1, 1, "S")
        copy_bz(2, 0)
        t_ln(1, 2)
        evac(1, 2, "V")
        quant(1, 0)
        regroup(1, 1)
        regroup(1, 2)
        quant(1, 1)
        quant(1, 2)
        t_ln(1, 3)
        evac(1, 3, "S")
        regroup(1, 3)
        quant(1, 3)
        xd(1)
        spread_z(2, 1)
        copy_bz(2, 1)
        spread_z(1, 0)
        copy_bz(1, 0)
        r_mx(0)
        r_add(0)
        xs(0)
        r_tanh(0)
        r_mx(1)
        r_add(1)
        r_mul(0)
        r_tanh(1)
        r_sq(0)
        spread_z(1, 1)
        r_mx(2)
        r_add(2)
        r_mul(1)
        r_tanh(2)
        r_sq(1)
        t_rows(3)
        r_mx(3)
        r_add(3)
        gains_(3)
        r_mul(2)
        xs(1)
        r_tanh(3)
        r_mul(3)
        sums(0)
        r_sq(2)
        sums(1)
        mean2_()
        r_sq(3)
        var2()
        pow_(2)
        norm(2, 0, "V")
        norm(2, 1, "V")
        copy_bz(1, 1)
        norm(2, 2, "S")
        norm(2, 3, "S")
        mx("g00")
        z_t0p(0)
        mx("g01")
        z_t0p(1)
        t_ln(2, 0)
        evac(2, 0, "V")
        regroup(2, 0)
        t_ln(2, 1)
        evac(2, 1, "S")
        regroup(2, 1)
        quant(2, 0)
        t_ln(2, 2)
        evac(2, 2, "S")
        regroup(2, 2)
        quant(2, 1)
        t_ln(2, 3)
        evac(2, 3, "S")
        mx("g10")
        z_dp(0)
        z_ptanh(0)
        z_pd(0, "G")
        z_bh(0, "G")
        z_abs(0)
        mx("g11")
        z_dp(1)
        regroup(2, 3)
        quant(2, 2)
        quant(2, 3)
        z_max(0)
        z_max(1)
        z_ptanh(1)
        z_pd(1, "G")
        z_bh(1, "G")
        z_absv(1)
        z_maxb(0, "V")
        z_maxb(1, "V")
        z_ln(0)
        z_pre(0)
        z_ln(1)
        z_pre(1)
        dummy(1)
        mx("g20")
        z_arg(0)
        z_qtanh(0)
        mx("g21")
        z_arg(1)
        z_na(0)
        z_qtanh(1)
        z_na(1)
        u_mx(0)
        u_tanh(0)
        u_mx(1)
        u_tanh(1)
        u_mx(2)
        u_tanh(2)
        u_mx(3)
        u_tanh(3)
        u_back(0)
        u_prod(0)
        u_back(1)
        u_prod(1)
        u_back(2)
        u_prod(2)
        u_out(0)
        store(0)
        u_out(1)
        store(1)
        u_back(3)
        u_prod(3)
        u_out(2)
        store(2)
        u_out(3)
        store(3)
